import numpy as np
import ml_dtypes


def mxq(x, axis, fmt="e4m3"):
    dtype, down = {"e4m3": (ml_dtypes.float8_e4m3fn, 7), "e5m2": (ml_dtypes.float8_e5m2, 14)}[fmt]
    v = np.moveaxis(np.asarray(x, np.float32).astype(ml_dtypes.bfloat16).astype(np.float64), axis, -1)
    blocks = v.reshape(v.shape[:-1] + (-1, 32))
    amax = np.abs(blocks).max(-1, keepdims=True)
    byte = np.maximum(np.where(amax > 0, np.frexp(amax)[1] - 1 + 127, 0) - down, 1)
    scale = np.exp2(byte - 127.0)
    codes = (blocks / scale).astype(np.float32).astype(dtype).astype(np.float64)
    return np.moveaxis((codes * scale).reshape(v.shape), -1, axis)


WIDE = False


def mx_kscale(k):
    if not WIDE:
        return np.ones(k)
    levels = np.array([18, -18])
    if k % 512:
        return np.exp2(np.random.permutation(np.resize(levels, k // 32))).repeat(32)
    a = np.empty((k // 512, 16))
    for p in range(k // 512):
        a[p, :8] = np.random.permutation(np.resize(levels, 8))
        for g in range(8):
            far = levels[np.abs(levels - a[p, g]) >= 10]
            a[p, g + 8] = far[np.random.randint(len(far))]
    return np.exp2(a.ravel()).repeat(32)


BF16 = ml_dtypes.bfloat16


def bf(x):
    return np.asarray(x, np.float32).astype(BF16)


def f64(x):
    return np.asarray(x).astype(np.float64)


B, D = 1536, 1024


def softplus(v):
    return np.logaddexp(v, 0.0)


def sigmoid(v):
    return 1.0 / (1.0 + np.exp(-v))


def setup_inputs():
    s = mx_kscale(B)[:, None]
    u = mx_kscale(D)
    xt0 = bf(np.random.standard_normal((B, D)) * 1.3)
    eps = bf(np.random.standard_normal((B, D)))
    x = bf(np.random.standard_normal((B, D)))
    t_rand = bf(np.random.uniform(0.0, 1.0, (B, 1)))
    Wm0 = bf(np.random.standard_normal((D, D)) / np.sqrt(D))
    bm = bf(np.random.standard_normal(D) * 0.5)
    Wv0 = bf(np.random.standard_normal((D, D)) / np.sqrt(D))
    bv = bf(np.random.standard_normal(D) * 0.5)
    g = bf(4.0 * np.random.standard_normal((B, D)) * np.exp2(np.random.randint(-6, 1, (B, 1))) / s * u)
    v = f64(xt0) @ f64(Wv0).T + f64(bv)
    return {"xt": bf(f64(xt0) * s), "eps": eps, "x": x, "t_rand": t_rand,
            "Wm": bf(f64(Wm0) / u[:, None]), "bm": bm,
            "Wv": bf(f64(Wv0) / u[:, None]), "bv": bv,
            "v": np.asarray(v, np.float32), "grad_out": g}


def reference(xt, eps, x, t_rand, Wm, bm, Wv, bv, v, grad_out):
    dmu = f64(t_rand) * f64(grad_out)
    dv = dmu * f64(eps) * sigmoid(f64(v))
    dz = np.concatenate([dmu, dv], 1)
    w = np.concatenate([f64(Wm), f64(Wv)], 0)
    dxt = mxq(dz, 1, "e5m2") @ mxq(w, 0, "e4m3")
    dWv = mxq(dv, 0, "e5m2").T @ mxq(f64(xt), 0, "e4m3")
    return dxt, dWv

@@ -1,0 +1,250 @@
+from contextlib import ExitStack
+
+import concourse.mybir as mybir
+from concourse.masks import make_identity
+
+B, D = 1536, 1024
+P = 128
+PACK = 4
+GROUPS = B // (P * PACK)
+N_TILE = 512
+ZC = 6
+TPN = 2
+ORDER = """Lva0/Y Lga0/Y dmu00/V A00/P Lea0/Y sig00/S stt00/V tt00/V Lvb0/Y sig01/S Lgb0/Y Leb0/Y Lvc0/Y stt01/V B00/P dmu01/V a00/S Lgc0/Y tt01/V sig02/S b00/S A01/P B01/P Lec0/Y stt02/V Lw0/Y Lw1/Y dmu02/V a01/S Lw2/Y tt02/V B02/P b01/S Wi01/V Z01/V Wi11/V Wq01/V Wi00/S Wq00/V Wi10/S Wq11/V Wi20/V Wq10/V A02/P Lw3/Y Wi30/V a02/S b02/S Lga1/Y dmu10/V A10/P Wi21/S dmu11/V A11/P Wq30/V Wq20/V Wq21/V Z02/V Wi31/S Lva1/Y a10/S Wq31/V Lvd0/Y Lgd0/Y Z00/V sig10/S Lea1/Y dmu03/V M010/P sig03/S stt10/V M020/P Led0/Y stt03/V M021/P m010/S tt10/V Leb1/Y M000/P a11/S Lgb1/Y dmu13/V M001/P Lvb1/Y m020/S sig11/S m000/S A03/P m001/S B10/P tt03/V a03/S B03/P b10/S Lgb2/Y stt11/V sig12/S dmu12/V Z10/V A13/P a13/S tt11/V b03/S M011/P stt12/V Lga2/Y Lea2/Y sig13/S M101/P Z03/V stt13/V m011/S B11/P dmu20/V m021/S tt13/V A12/P Lva2/Y m101/S tt12/V b11/S dmu22/V Lvb2/Y sig20/S M030/P Leb2/Y M031/P Lx0/Y dmu21/V a12/S Z11/V m030/S B13/P B12/P b13/S A21/P b12/S sig22/S O01/Y dmu23/V A22/P a22/S M100/P Di01/V sig21/S Lx1/Y a21/S Z12/V M120/P m031/S stt20/V m100/S Z13/V Di00/V M121/P sig23/S O00/Y M110/P stt22/V M111/P stt23/V A23/P Di10/S a23/S O02/Y O10/Y A20/P tt20/V a20/S M131/P O03/Y tt22/V B20/P m121/S Lx2/Y B22/P m110/S b20/S stt21/V tt23/V tt21/V b22/S Z22/V M130/P dq01/V Z20/V m120/S B23/P Xi10/S B21/P dq10/V b23/S m131/S m111/S b21/S O11/Y Xi00/V dq00/V M221/P M201/P m201/S M220/P Z23/V O12/Y Xq10/V m220/S m130/S M200/P m200/S M231/P Z21/V m221/S Xq00/V Di20/V M230/P O20/Y Xi20/V Di11/S O22/Y dq20/V m231/S Xq20/V Di21/V O13/Y dq11/V m230/S M211/P O23/Y m211/S N00a/P M210/P m210/S O21/Y N01a/P N00b/P N02a/P N03a/P dq21/V Xi11/V N01b/P n01/V n00/S N02b/P N04a/P N04b/P N05a/P N05b/P Xi01/S Xq11/V Q00/Y N06a/P Xq01/V n02/S Xi21/V Xq21/V N03b/P n03/S Q01/Y n04/S n05/S Q02/Y N06b/P N07a/P N07b/P N14a/P N15a/P N16a/P N17a/P N17b/P n06/S n07/S N15b/P N14b/P n14/S N16b/P n16/S N10a/P N10b/P Q03/Y n15/S n17/V Q17/Y Q14/Y Q16/Y Q15/Y n10/S N11a/P N11b/P n11/S N12a/P N12b/P Q10/Y Q11/Y N13a/P N13b/P n13/V n12/S Q12/Y Q13/Y"""
+FLOPS = 2 * B * D * D * 3
+BYTES = 2 * (3 * B * D + 2 * D * D + B) + 4 * B * D + 4 * (B * D + D * D)
+
+F32 = mybir.dt.float32
+BF16 = mybir.dt.bfloat16
+U32 = mybir.dt.uint32
+U8 = mybir.dt.uint8
+E4M3 = mybir.dt.float8_e4m3fn_x4
+E5M2 = mybir.dt.float8_e5m2_x4
+MULT = mybir.AluOpType.mult
+SIGMOID = mybir.ActivationFunctionType.Sigmoid
+
+
+def tile_diffscm_pb_v_kernel(
+    tc, xt, eps, x, t_rand, Wm, bm, Wv, bv, v, grad_out, out_0, out_1
+):
+    nc = tc.nc
+    by_group = lambda a: a.rearrange("(g p j) w -> p g j w", g=GROUPS, j=PACK)
+    xt_v, eps_v, v_v, grad_v, out0_v = [by_group(a) for a in (xt, eps, v, grad_out, out_0)]
+    w_v = [w.rearrange("(g p j) w -> p g j w", g=2, j=PACK) for w in (Wm, Wv)]
+
+    with ExitStack() as ctx:
+        const = ctx.enter_context(tc.tile_pool(name="const", bufs=1))
+        inp = ctx.enter_context(tc.tile_pool(name="inp", bufs=1))
+        keep = ctx.enter_context(tc.tile_pool(name="keep", bufs=1))
+        work = ctx.enter_context(tc.tile_pool(name="work", bufs=1))
+        psum = ctx.enter_context(tc.psum_pool(name="psum", bufs=4))
+        ctx.enter_context(tc.manual_schedule())
+
+        t_bf = const.tile([P, GROUPS, PACK], BF16, name="t_bf")
+        t_f = const.tile([P, GROUPS, PACK], F32, name="t_f")
+        warm = const.tile([P, 1], F32, name="warm")
+        ident = const.tile([P, P], F32, name="ident")
+
+        w_codes = keep.tile([P, 4, D], U32, align_bytes=64, name="w_codes")
+        w_scales = keep.tile([P, 4, D], U8, align_bytes=64, name="w_scales")
+        x_codes = keep.tile([P, GROUPS, D], U32, align_bytes=64, name="x_codes")
+        x_scales = keep.tile([P, GROUPS, D], U8, align_bytes=64, name="x_scales")
+        d_codes = keep.tile([P, GROUPS, D], U32, align_bytes=64, name="d_codes")
+        d_scales = keep.tile([P, GROUPS, D], U8, align_bytes=64, name="d_scales")
+
+        def bf_tile(name):
+            return inp.tile([P, PACK, D], BF16, tag="bf", bufs=8, name=name)
+
+        raw = {}
+        for i in range(4):
+            raw["w", i] = bf_tile("raw_bf")
+        for g in range(2):
+            raw["e", g] = bf_tile("raw_bf")
+            raw["g", g] = bf_tile("raw_bf")
+            raw["v", g] = inp.tile([P, PACK, D], F32, tag="v", bufs=2, name="raw_v")
+        views = {"e": eps_v, "g": grad_v, "v": v_v, "x": xt_v}
+
+        nc.scalar.dma_start(out=t_bf[:], in_=t_rand.rearrange("(g p j) o -> p g (j o)", g=GROUPS, j=PACK))
+        nc.gpsimd.memset(warm[:], 0.0)
+        nc.scalar.activation(out=warm[:], in_=warm[:], func=SIGMOID)
+        make_identity(nc, ident[:])
+        nc.vector.tensor_copy(out=t_f[:], in_=t_bf[:])
+
+        def copy(engine, out, in_):
+            if engine == "V":
+                nc.vector.tensor_copy(out=out, in_=in_)
+            else:
+                nc.scalar.copy(out=out, in_=in_)
+
+        grp, dmu, dv, tps, dzt, dz, acc, res = {}, {}, {}, {}, {}, {}, {}, {}
+
+        def fetch_w(e, i):
+            nc.sync.dma_start(out=raw["w", i][:], in_=w_v[i // 2][:, i % 2])
+
+        def fetch(e, kind, g, lo, hi):
+            if (kind, g) not in raw:
+                if kind == "v":
+                    raw[kind, g] = inp.tile([P, PACK, D], F32, tag="v", bufs=2, name="raw_v")
+                else:
+                    raw[kind, g] = bf_tile("raw_bf")
+            nc.sync.dma_start(out=raw[kind, g][:, lo:hi, :], in_=views[kind][:, g, lo:hi, :])
+
+        def grp_tile(key):
+            if key not in grp:
+                grp[key] = work.tile([P, N_TILE, PACK], BF16, tag="grp", bufs=4, align_bytes=64, name="grp")
+            return grp[key]
+
+        def source(kind, i):
+            return dv[i] if kind == "d" else raw[kind, i]
+
+        def interleave(e, kind, i, h):
+            tile = grp_tile((kind, i, h))
+            cols = source(kind, i)[:, :, h * N_TILE : (h + 1) * N_TILE]
+            copy(e, tile[:].rearrange("p (c i) t -> p c t i", i=4), cols.rearrange("p t (c i) -> p c t i", i=4))
+
+        def quantize(e, kind, i, h):
+            codes, scales, fmt = {"w": (w_codes, w_scales, E4M3), "x": (x_codes, x_scales, E4M3), "d": (d_codes, d_scales, E5M2)}[kind]
+            c = slice(h * N_TILE, (h + 1) * N_TILE)
+            nc.vector.quantize_mx(
+                out=codes[:, i, c].bitcast(fmt), scales=scales[:, i, c],
+                in_=grp[kind, i, h][:].rearrange("p c t -> p (c t)"),
+            )
+
+        def do_dmu(e, g, j):
+            dmu[g, j] = work.tile([P, D], BF16, tag="dmu", bufs=4, name="dmu")
+            nc.vector.tensor_scalar(
+                out=dmu[g, j][:], in0=raw["g", g][:, j, :], scalar1=t_f[:, g, j : j + 1], scalar2=None, op0=MULT
+            )
+
+        def do_sig(e, g, j):
+            vv = raw["v", g][:, j, :]
+            nc.scalar.activation(out=vv, in_=vv, func=SIGMOID)
+
+        def do_stt(e, g, j):
+            vv = raw["v", g][:, j, :]
+            nc.vector.scalar_tensor_tensor(
+                out=vv, in0=raw["e", g][:, j, :], scalar=t_f[:, g, j : j + 1], in1=vv, op0=MULT, op1=MULT
+            )
+
+        def do_tt(e, g, j):
+            if g not in dv:
+                dv[g] = work.tile([P, PACK, D], BF16, tag="dv", bufs=2, name="dv")
+            nc.vector.tensor_tensor(out=dv[g][:, j, :], in0=raw["v", g][:, j, :], in1=raw["g", g][:, j, :], op=MULT)
+
+        def turn(e, g, j, head):
+            words = (dv[g][:, j, :] if head else dmu[g, j][:]).bitcast(F32)
+            tp = psum.tile([P, 2, 2, P], F32, tag="tp", bufs=TPN, name="tp")
+            for k in range(2):
+                for w in range(2):
+                    nc.tensor.transpose(tp[:, k, w, :], words[:, 256 * k + w : 256 * (k + 1) : 2], ident[:])
+            tps[g, j, head] = tp
+
+        def turn_out(e, g, j, head):
+            if (g, j) not in dzt:
+                dzt[g, j] = work.tile([P, 2, 2, P, PACK], BF16, tag="dzt", bufs=4, align_bytes=64, name="dzt")
+            dst = dzt[g, j][:, head].rearrange("p k c t -> p (k c t)").bitcast(F32)
+            copy(e, dst.rearrange("p (k c w) -> p k c w", k=2, w=2), tps[g, j, head][:].rearrange("p k w c -> p k c w"))
+
+        def z_quant(e, g, j):
+            codes = work.tile([P, 4 * P], U32, tag="zc", bufs=ZC, align_bytes=64, name="zc")
+            scales = work.tile([P, 4 * P], U8, tag="zs", bufs=ZC, align_bytes=64, name="zs")
+            nc.vector.quantize_mx(
+                out=codes[:].bitcast(E5M2), scales=scales[:], in_=dzt[g, j][:].rearrange("p h k c t -> p (h k c t)")
+            )
+            dz[g, j] = (codes, scales)
+
+        def m_pass(e, g, j, n):
+            acc[g, j, n] = psum.tile([P, N_TILE], F32, tag="acc", bufs=8 - TPN, name="acc")
+            cols = slice(n * N_TILE, (n + 1) * N_TILE)
+            for i in range(4):
+                codes, scales = dz[g, j]
+                rows = slice(i * P, (i + 1) * P)
+                nc.tensor.matmul_mx(
+                    out=acc[g, j, n][:],
+                    lhsT=codes[:, rows].bitcast(E5M2), lhsT_scale=scales[:, rows],
+                    rhs=w_codes[:, i, cols].bitcast(E4M3), rhs_scale=w_scales[:, i, cols],
+                    start=(i == 0), stop=(i == 3),
+                )
+
+        def res_tile(key):
+            if key not in res:
+                res[key] = work.tile([P, 2, N_TILE], F32, tag="res", bufs=5, name="res")
+            return res[key]
+
+        def m_out(e, g, j, n):
+            copy(e, res_tile((g, j))[:, n, :], acc[g, j, n][:])
+
+        def m_store(e, g, j):
+            nc.sync.dma_start(out=out0_v[:, g, j, :], in_=res[g, j][:].rearrange("p n w -> p (n w)"))
+
+        def n_pass(e, n, m, part):
+            if part == "a":
+                acc["n", n, m] = psum.tile([P, N_TILE], F32, tag="acc", bufs=8 - TPN, name="acc")
+            cols = slice(n * N_TILE, (n + 1) * N_TILE)
+            rows = slice(m * P, (m + 1) * P)
+            for g in ([0, 1] if part == "a" else [2]):
+                nc.tensor.matmul_mx(
+                    out=acc["n", n, m][:],
+                    lhsT=d_codes[:, g, rows].bitcast(E5M2), lhsT_scale=d_scales[:, g, rows],
+                    rhs=x_codes[:, g, cols].bitcast(E4M3), rhs_scale=x_scales[:, g, cols],
+                    start=(g == 0), stop=(g == GROUPS - 1),
+                )
+
+        out1_v = out_1.rearrange("(m p) w -> p m w", p=P)
+
+        def n_out(e, n, m):
+            copy(e, res_tile(("n", n, m // 2))[:, m % 2, :], acc["n", n, m][:])
+
+        def n_store(e, n, q):
+            cols = slice(n * N_TILE, (n + 1) * N_TILE)
+            if n == 0:
+                nc.sync.dma_start(out=out1_v[:, 2 * q : 2 * q + 2, cols], in_=res["n", n, q][:])
+            else:
+                nc.sync.dma_start(out=out1_v[:, q, cols], in_=res["n", n, q // 2][:, q % 2, :])
+
+        kinds = {"W": "w", "D": "d", "X": "x"}
+        for item in ORDER.split():
+            name, e = item.split("/")
+            d = [int(ch) for ch in name if ch in "0123456789"]
+            c = name[0]
+            if c == "L":
+                if name[1] == "w":
+                    fetch_w(e, d[0])
+                elif name[1] == "x":
+                    fetch(e, "x", d[0], 0, PACK)
+                else:
+                    step = 1 if d[0] == 0 else 2
+                    lo = ["a", "b", "c", "d"].index(name[2]) * step
+                    fetch(e, name[1], d[0], lo, lo + step)
+            elif c in kinds or name[:2] == "dq":
+                kind = kinds.get(c, "d")
+                if name[1] == "q":
+                    quantize(e, kind, d[0], d[1])
+                else:
+                    interleave(e, kind, d[0], d[1])
+            elif name.startswith("dmu"):
+                do_dmu(e, d[0], d[1])
+            elif name.startswith("sig"):
+                do_sig(e, d[0], d[1])
+            elif name.startswith("stt"):
+                do_stt(e, d[0], d[1])
+            elif name.startswith("tt"):
+                do_tt(e, d[0], d[1])
+            elif c in "AB":
+                turn(e, d[0], d[1], int(c == "B"))
+            elif c in "ab":
+                turn_out(e, d[0], d[1], int(c == "b"))
+            elif c == "Z":
+                z_quant(e, d[0], d[1])
+            elif c == "M":
+                m_pass(e, d[0], d[1], d[2])
+            elif c == "m":
+                m_out(e, d[0], d[1], d[2])
+            elif c == "O":
+                m_store(e, d[0], d[1])
+            elif c == "N":
+                n_pass(e, d[0], d[1], name[3])
+            elif c == "n":
+                n_out(e, d[0], d[1])
+            else:
+                n_store(e, d[0], d[1])

@@ -7,10 +7,8 @@ B, D = 1536, 1024
 P = 128
 PACK = 4
 GROUPS = B // (P * PACK)
+SLICES = GROUPS * PACK
 N_TILE = 512
-ZC = 6
-TPN = 2
-ORDER = """Lva0/Y Lga0/Y dmu00/V A00/P Lea0/Y sig00/S stt00/V tt00/V Lvb0/Y sig01/S Lgb0/Y Leb0/Y Lvc0/Y stt01/V B00/P dmu01/V a00/S Lgc0/Y tt01/V sig02/S b00/S A01/P B01/P Lec0/Y stt02/V Lw0/Y Lw1/Y dmu02/V a01/S Lw2/Y tt02/V B02/P b01/S Wi01/V Z01/V Wi11/V Wq01/V Wi00/S Wq00/V Wi10/S Wq11/V Wi20/V Wq10/V A02/P Lw3/Y Wi30/V a02/S b02/S Lga1/Y dmu10/V A10/P Wi21/S dmu11/V A11/P Wq30/V Wq20/V Wq21/V Z02/V Wi31/S Lva1/Y a10/S Wq31/V Lvd0/Y Lgd0/Y Z00/V sig10/S Lea1/Y dmu03/V M010/P sig03/S stt10/V M020/P Led0/Y stt03/V M021/P m010/S tt10/V Leb1/Y M000/P a11/S Lgb1/Y dmu13/V M001/P Lvb1/Y m020/S sig11/S m000/S A03/P m001/S B10/P tt03/V a03/S B03/P b10/S Lgb2/Y stt11/V sig12/S dmu12/V Z10/V A13/P a13/S tt11/V b03/S M011/P stt12/V Lga2/Y Lea2/Y sig13/S M101/P Z03/V stt13/V m011/S B11/P dmu20/V m021/S tt13/V A12/P Lva2/Y m101/S tt12/V b11/S dmu22/V Lvb2/Y sig20/S M030/P Leb2/Y M031/P Lx0/Y dmu21/V a12/S Z11/V m030/S B13/P B12/P b13/S A21/P b12/S sig22/S O01/Y dmu23/V A22/P a22/S M100/P Di01/V sig21/S Lx1/Y a21/S Z12/V M120/P m031/S stt20/V m100/S Z13/V Di00/V M121/P sig23/S O00/Y M110/P stt22/V M111/P stt23/V A23/P Di10/S a23/S O02/Y O10/Y A20/P tt20/V a20/S M131/P O03/Y tt22/V B20/P m121/S Lx2/Y B22/P m110/S b20/S stt21/V tt23/V tt21/V b22/S Z22/V M130/P dq01/V Z20/V m120/S B23/P Xi10/S B21/P dq10/V b23/S m131/S m111/S b21/S O11/Y Xi00/V dq00/V M221/P M201/P m201/S M220/P Z23/V O12/Y Xq10/V m220/S m130/S M200/P m200/S M231/P Z21/V m221/S Xq00/V Di20/V M230/P O20/Y Xi20/V Di11/S O22/Y dq20/V m231/S Xq20/V Di21/V O13/Y dq11/V m230/S M211/P O23/Y m211/S N00a/P M210/P m210/S O21/Y N01a/P N00b/P N02a/P N03a/P dq21/V Xi11/V N01b/P n01/V n00/S N02b/P N04a/P N04b/P N05a/P N05b/P Xi01/S Xq11/V Q00/Y N06a/P Xq01/V n02/S Xi21/V Xq21/V N03b/P n03/S Q01/Y n04/S n05/S Q02/Y N06b/P N07a/P N07b/P N14a/P N15a/P N16a/P N17a/P N17b/P n06/S n07/S N15b/P N14b/P n14/S N16b/P n16/S N10a/P N10b/P Q03/Y n15/S n17/V Q17/Y Q14/Y Q16/Y Q15/Y n10/S N11a/P N11b/P n11/S N12a/P N12b/P Q10/Y Q11/Y N13a/P N13b/P n13/V n12/S Q12/Y Q13/Y"""
 FLOPS = 2 * B * D * D * 3
 BYTES = 2 * (3 * B * D + 2 * D * D + B) + 4 * B * D + 4 * (B * D + D * D)
 
@@ -28,47 +26,57 @@ def tile_diffscm_pb_v_kernel(
     tc, xt, eps, x, t_rand, Wm, bm, Wv, bv, v, grad_out, out_0, out_1
 ):
     nc = tc.nc
-    by_group = lambda a: a.rearrange("(g p j) w -> p g j w", g=GROUPS, j=PACK)
-    xt_v, eps_v, v_v, grad_v, out0_v = [by_group(a) for a in (xt, eps, v, grad_out, out_0)]
-    w_v = [w.rearrange("(g p j) w -> p g j w", g=2, j=PACK) for w in (Wm, Wv)]
+    by_group = lambda a: a.rearrange("(g p j) w -> g p (j w)", p=P, j=PACK)
+    hbm = {"x": by_group(xt), "e": by_group(eps), "v": by_group(v), "g": by_group(grad_out)}
+    w_hbm = [by_group(w)[k] for w in (Wm, Wv) for k in range(2)]
+    out0_v = by_group(out_0)
+    out1_v = out_1.rearrange("(m p) w -> m p w", p=P)
 
     with ExitStack() as ctx:
         const = ctx.enter_context(tc.tile_pool(name="const", bufs=1))
         inp = ctx.enter_context(tc.tile_pool(name="inp", bufs=1))
         keep = ctx.enter_context(tc.tile_pool(name="keep", bufs=1))
         work = ctx.enter_context(tc.tile_pool(name="work", bufs=1))
-        psum = ctx.enter_context(tc.psum_pool(name="psum", bufs=4))
+        psum = ctx.enter_context(tc.psum_pool(name="psum", bufs=8))
         ctx.enter_context(tc.manual_schedule())
 
-        t_bf = const.tile([P, GROUPS, PACK], BF16, name="t_bf")
-        t_f = const.tile([P, GROUPS, PACK], F32, name="t_f")
-        warm = const.tile([P, 1], F32, name="warm")
+        t_col = const.tile([P, SLICES], BF16, name="t_col")
         ident = const.tile([P, P], F32, name="ident")
 
-        w_codes = keep.tile([P, 4, D], U32, align_bytes=64, name="w_codes")
-        w_scales = keep.tile([P, 4, D], U8, align_bytes=64, name="w_scales")
-        x_codes = keep.tile([P, GROUPS, D], U32, align_bytes=64, name="x_codes")
-        x_scales = keep.tile([P, GROUPS, D], U8, align_bytes=64, name="x_scales")
-        d_codes = keep.tile([P, GROUPS, D], U32, align_bytes=64, name="d_codes")
-        d_scales = keep.tile([P, GROUPS, D], U8, align_bytes=64, name="d_scales")
+        w_codes = keep.tile([P, 4 * D], U32, align_bytes=64, name="w_codes")
+        w_scales = keep.tile([P, 4 * D], U8, align_bytes=64, name="w_scales")
+        x_codes = keep.tile([P, GROUPS * D], U32, align_bytes=64, name="x_codes")
+        x_scales = keep.tile([P, GROUPS * D], U8, align_bytes=64, name="x_scales")
+        d_codes = keep.tile([P, GROUPS * D], U32, align_bytes=64, name="d_codes")
+        d_scales = keep.tile([P, GROUPS * D], U8, align_bytes=64, name="d_scales")
+        planes = {"w": (w_codes, w_scales, E4M3), "x": (x_codes, x_scales, E4M3), "d": (d_codes, d_scales, E5M2)}
 
-        def bf_tile(name):
-            return inp.tile([P, PACK, D], BF16, tag="bf", bufs=8, name=name)
+        def big_tile(shape, dtype):
+            return inp.tile(shape, dtype, tag="big", bufs=7, name="big")
 
         raw = {}
-        for i in range(4):
-            raw["w", i] = bf_tile("raw_bf")
-        for g in range(2):
-            raw["e", g] = bf_tile("raw_bf")
-            raw["g", g] = bf_tile("raw_bf")
-            raw["v", g] = inp.tile([P, PACK, D], F32, tag="v", bufs=2, name="raw_v")
-        views = {"e": eps_v, "g": grad_v, "v": v_v, "x": xt_v}
+        for k in range(4):
+            raw["w", k] = big_tile([P, PACK * D], BF16)
+        for g in range(GROUPS):
+            raw["g", g] = big_tile([P, PACK * D], BF16)
+            raw["e", g] = inp.tile([P, PACK * D], BF16, tag="e", bufs=GROUPS, name="raw_e")
+            raw["v", g] = inp.tile([P, PACK * D], F32, tag="v", bufs=GROUPS, name="raw_v")
 
-        nc.scalar.dma_start(out=t_bf[:], in_=t_rand.rearrange("(g p j) o -> p g (j o)", g=GROUPS, j=PACK))
-        nc.gpsimd.memset(warm[:], 0.0)
-        nc.scalar.activation(out=warm[:], in_=warm[:], func=SIGMOID)
-        make_identity(nc, ident[:])
-        nc.vector.tensor_copy(out=t_f[:], in_=t_bf[:])
+        def part(kind, i, n=1):
+            g, j = divmod(i, PACK)
+            return raw[kind, g][:, j * D : (j + n) * D]
+
+        def load_slices(i, n):
+            g, j = divmod(i, PACK)
+            for kind in "vge":
+                nc.sync.dma_start(out=part(kind, i, n), in_=hbm[kind][g][:, j * D : (j + n) * D])
+
+        def load_w(k):
+            nc.sync.dma_start(out=raw["w", k][:], in_=w_hbm[k])
+
+        def load_x(g):
+            raw["x", g] = big_tile([P, PACK * D], BF16)
+            nc.sync.dma_start(out=raw["x", g][:], in_=hbm["x"][g])
 
         def copy(engine, out, in_):
             if engine == "V":
@@ -76,175 +84,231 @@ def tile_diffscm_pb_v_kernel(
             else:
                 nc.scalar.copy(out=out, in_=in_)
 
-        grp, dmu, dv, tps, dzt, dz, acc, res = {}, {}, {}, {}, {}, {}, {}, {}
+        grp, prod, dmu, banks, dzt, dz, acc, acc1 = {}, {}, {}, {}, {}, {}, {}, {}
 
-        def fetch_w(e, i):
-            nc.sync.dma_start(out=raw["w", i][:], in_=w_v[i // 2][:, i % 2])
+        def interleave(engine, piece, a=0, b=None):
+            kind, k, lo, width = piece
+            b = width if b is None else b
+            if a == b:
+                return
+            if piece not in grp:
+                tag = "grp" + engine
+                grp[piece] = work.tile([P, width * PACK], BF16, tag=tag, bufs=3, align_bytes=64, name=tag)
+            tile = grp[piece]
+            if kind == "d":
+                dst = tile[:].rearrange("p (w a u e t) -> p u w t a e", a=2, u=2, e=2, t=PACK)
+                src = raw["e", k][:].rearrange("p (t u w a e) -> p u w t a e", t=PACK, u=2, a=2, e=2)
+                for u in range(2):
+                    copy(engine, dst[:, u, a // 8 : b // 8], src[:, u, (lo + a) // 8 : (lo + b) // 8])
+                return
+            dst = tile[:].rearrange("p (c i t) -> p c t i", i=4, t=PACK)
+            src = raw[kind, k][:].rearrange("p (t c i) -> p c t i", t=PACK, i=4)
+            copy(engine, dst[:, a // 4 : b // 4], src[:, (lo + a) // 4 : (lo + b) // 4])
 
-        def fetch(e, kind, g, lo, hi):
-            if (kind, g) not in raw:
-                if kind == "v":
-                    raw[kind, g] = inp.tile([P, PACK, D], F32, tag="v", bufs=2, name="raw_v")
-                else:
-                    raw[kind, g] = bf_tile("raw_bf")
-            nc.sync.dma_start(out=raw[kind, g][:, lo:hi, :], in_=views[kind][:, g, lo:hi, :])
+        def quantize(piece):
+            kind, k, lo, width = piece
+            codes, scales, fmt = planes[kind]
+            c = slice(k * D + lo, k * D + lo + width)
+            nc.vector.quantize_mx(out=codes[:, c].bitcast(fmt), scales=scales[:, c], in_=grp[piece][:])
 
-        def grp_tile(key):
-            if key not in grp:
-                grp[key] = work.tile([P, N_TILE, PACK], BF16, tag="grp", bufs=4, align_bytes=64, name="grp")
-            return grp[key]
+        def sigmoid(i):
+            nc.scalar.activation(out=part("v", i), in_=part("v", i), func=SIGMOID)
 
-        def source(kind, i):
-            return dv[i] if kind == "d" else raw[kind, i]
-
-        def interleave(e, kind, i, h):
-            tile = grp_tile((kind, i, h))
-            cols = source(kind, i)[:, :, h * N_TILE : (h + 1) * N_TILE]
-            copy(e, tile[:].rearrange("p (c i) t -> p c t i", i=4), cols.rearrange("p t (c i) -> p c t i", i=4))
-
-        def quantize(e, kind, i, h):
-            codes, scales, fmt = {"w": (w_codes, w_scales, E4M3), "x": (x_codes, x_scales, E4M3), "d": (d_codes, d_scales, E5M2)}[kind]
-            c = slice(h * N_TILE, (h + 1) * N_TILE)
-            nc.vector.quantize_mx(
-                out=codes[:, i, c].bitcast(fmt), scales=scales[:, i, c],
-                in_=grp[kind, i, h][:].rearrange("p c t -> p (c t)"),
-            )
-
-        def do_dmu(e, g, j):
-            dmu[g, j] = work.tile([P, D], BF16, tag="dmu", bufs=4, name="dmu")
-            nc.vector.tensor_scalar(
-                out=dmu[g, j][:], in0=raw["g", g][:, j, :], scalar1=t_f[:, g, j : j + 1], scalar2=None, op0=MULT
-            )
-
-        def do_sig(e, g, j):
-            vv = raw["v", g][:, j, :]
-            nc.scalar.activation(out=vv, in_=vv, func=SIGMOID)
-
-        def do_stt(e, g, j):
-            vv = raw["v", g][:, j, :]
+        def first_product(i):
+            prod[i] = work.tile([P, D], F32, tag="prod", bufs=2, name="prod")
             nc.vector.scalar_tensor_tensor(
-                out=vv, in0=raw["e", g][:, j, :], scalar=t_f[:, g, j : j + 1], in1=vv, op0=MULT, op1=MULT
+                out=prod[i][:], in0=part("g", i), scalar=t_col[:, i : i + 1], in1=part("e", i), op0=MULT, op1=MULT
             )
 
-        def do_tt(e, g, j):
-            if g not in dv:
-                dv[g] = work.tile([P, PACK, D], BF16, tag="dv", bufs=2, name="dv")
-            nc.vector.tensor_tensor(out=dv[g][:, j, :], in0=raw["v", g][:, j, :], in1=raw["g", g][:, j, :], op=MULT)
+        sorted_in = lambda a: a.rearrange("p (w u e) -> p u w e", u=2, e=2)
+        sorted_out = lambda a: a.rearrange("p (u w e) -> p u w e", u=2, e=2)
 
-        def turn(e, g, j, head):
-            words = (dv[g][:, j, :] if head else dmu[g, j][:]).bitcast(F32)
-            tp = psum.tile([P, 2, 2, P], F32, tag="tp", bufs=TPN, name="tp")
+        def make_dmu(i):
+            dmu[i] = work.tile([P, D], BF16, tag="dmu", bufs=2, name="dmu")
+            nc.vector.tensor_scalar(
+                out=sorted_out(dmu[i][:]), in0=sorted_in(part("g", i)), scalar1=t_col[:, i : i + 1], scalar2=None, op0=MULT
+            )
+
+        def make_dv(i):
+            nc.vector.tensor_tensor(
+                out=sorted_out(part("e", i)), in0=sorted_in(prod[i][:]), in1=sorted_in(part("v", i)), op=MULT
+            )
+
+        def turn(i, head):
+            bank = psum.tile([P, 2, 2, P], F32, tag="bank", name="bank")
+            words = (part("e", i) if head else dmu[i][:]).bitcast(F32)
             for k in range(2):
-                for w in range(2):
-                    nc.tensor.transpose(tp[:, k, w, :], words[:, 256 * k + w : 256 * (k + 1) : 2], ident[:])
-            tps[g, j, head] = tp
+                for u in range(2):
+                    nc.tensor.transpose(bank[:, k, u, :], words[:, 256 * u + P * k : 256 * u + P * (k + 1)], ident[:])
+            banks[i, head] = bank
 
-        def turn_out(e, g, j, head):
-            if (g, j) not in dzt:
-                dzt[g, j] = work.tile([P, 2, 2, P, PACK], BF16, tag="dzt", bufs=4, align_bytes=64, name="dzt")
-            dst = dzt[g, j][:, head].rearrange("p k c t -> p (k c t)").bitcast(F32)
-            copy(e, dst.rearrange("p (k c w) -> p k c w", k=2, w=2), tps[g, j, head][:].rearrange("p k w c -> p k c w"))
-
-        def z_quant(e, g, j):
-            codes = work.tile([P, 4 * P], U32, tag="zc", bufs=ZC, align_bytes=64, name="zc")
-            scales = work.tile([P, 4 * P], U8, tag="zs", bufs=ZC, align_bytes=64, name="zs")
-            nc.vector.quantize_mx(
-                out=codes[:].bitcast(E5M2), scales=scales[:], in_=dzt[g, j][:].rearrange("p h k c t -> p (h k c t)")
+        def turn_out(i, head):
+            if not head:
+                dzt[i] = work.tile([P, 2 * D], BF16, tag="dzt", bufs=3, align_bytes=64, name="dzt")
+            dst = dzt[i][:, head * D : (head + 1) * D].bitcast(F32)
+            nc.scalar.copy(
+                out=dst.rearrange("p (k c u) -> p k c u", k=2, u=2),
+                in_=banks[i, head][:].rearrange("p k u c -> p k c u"),
             )
-            dz[g, j] = (codes, scales)
 
-        def m_pass(e, g, j, n):
-            acc[g, j, n] = psum.tile([P, N_TILE], F32, tag="acc", bufs=8 - TPN, name="acc")
-            cols = slice(n * N_TILE, (n + 1) * N_TILE)
-            for i in range(4):
-                codes, scales = dz[g, j]
-                rows = slice(i * P, (i + 1) * P)
+        def quantize_dz(i):
+            codes = work.tile([P, 4 * P], U32, tag="zc", bufs=3, align_bytes=64, name="zc")
+            scales = work.tile([P, 4 * P], U8, tag="zs", bufs=3, align_bytes=64, name="zs")
+            nc.vector.quantize_mx(out=codes[:].bitcast(E5M2), scales=scales[:], in_=dzt[i][:])
+            dz[i] = (codes, scales)
+
+        def product0(i, n):
+            if (i, n) not in acc:
+                acc[i, n] = psum.tile([P, N_TILE], F32, tag="bank", name="bank")
+            codes, scales = dz[i]
+            for k in range(4):
+                rows = slice(k * P, (k + 1) * P)
+                cols = slice(k * D + n * N_TILE, k * D + (n + 1) * N_TILE)
                 nc.tensor.matmul_mx(
-                    out=acc[g, j, n][:],
+                    out=acc[i, n][:],
                     lhsT=codes[:, rows].bitcast(E5M2), lhsT_scale=scales[:, rows],
-                    rhs=w_codes[:, i, cols].bitcast(E4M3), rhs_scale=w_scales[:, i, cols],
-                    start=(i == 0), stop=(i == 3),
+                    rhs=w_codes[:, cols].bitcast(E4M3), rhs_scale=w_scales[:, cols],
+                    start=(k == 0), stop=(k == 3),
                 )
 
-        def res_tile(key):
-            if key not in res:
-                res[key] = work.tile([P, 2, N_TILE], F32, tag="res", bufs=5, name="res")
-            return res[key]
+        def result0(i, n):
+            nc.scalar.copy(out=part("v", i)[:, n * N_TILE : (n + 1) * N_TILE], in_=acc[i, n][:])
 
-        def m_out(e, g, j, n):
-            copy(e, res_tile((g, j))[:, n, :], acc[g, j, n][:])
+        def store0(i):
+            g, j = divmod(i, PACK)
+            nc.sync.dma_start(out=out0_v[g][:, j * D : (j + 1) * D], in_=part("v", i))
 
-        def m_store(e, g, j):
-            nc.sync.dma_start(out=out0_v[:, g, j, :], in_=res[g, j][:].rearrange("p n w -> p (n w)"))
+        def pass1(m, n, g, first, final):
+            if first:
+                acc1[m, n] = psum.tile([P, N_TILE], F32, tag="bank", name="bank")
+            rows = slice(g * D + m * P, g * D + (m + 1) * P)
+            cols = slice(g * D + n * N_TILE, g * D + (n + 1) * N_TILE)
+            nc.tensor.matmul_mx(
+                out=acc1[m, n][:],
+                lhsT=d_codes[:, rows].bitcast(E5M2), lhsT_scale=d_scales[:, rows],
+                rhs=x_codes[:, cols].bitcast(E4M3), rhs_scale=x_scales[:, cols],
+                start=first, stop=final,
+            )
 
-        def n_pass(e, n, m, part):
-            if part == "a":
-                acc["n", n, m] = psum.tile([P, N_TILE], F32, tag="acc", bufs=8 - TPN, name="acc")
-            cols = slice(n * N_TILE, (n + 1) * N_TILE)
-            rows = slice(m * P, (m + 1) * P)
-            for g in ([0, 1] if part == "a" else [2]):
-                nc.tensor.matmul_mx(
-                    out=acc["n", n, m][:],
-                    lhsT=d_codes[:, g, rows].bitcast(E5M2), lhsT_scale=d_scales[:, g, rows],
-                    rhs=x_codes[:, g, cols].bitcast(E4M3), rhs_scale=x_scales[:, g, cols],
-                    start=(g == 0), stop=(g == GROUPS - 1),
-                )
+        def result1(engine, m, n):
+            res = big_tile([P, N_TILE], F32)
+            copy(engine, res[:], acc1[m, n][:])
+            nc.sync.dma_start(out=out1_v[m][:, n * N_TILE : (n + 1) * N_TILE], in_=res[:])
 
-        out1_v = out_1.rearrange("(m p) w -> p m w", p=P)
+        nc.scalar.dma_start(out=t_col[:].rearrange("p (g j) -> p g j", j=PACK), in_=t_rand.rearrange("(g p j) o -> p g (j o)", p=P, j=PACK))
+        load_slices(0, 1)
+        load_w(0)
+        load_w(1)
+        load_w(2)
+        load_w(3)
+        load_slices(1, 1)
+        load_slices(2, 1)
+        load_slices(3, 1)
+        make_identity(nc, ident[:])
 
-        def n_out(e, n, m):
-            copy(e, res_tile(("n", n, m // 2))[:, m % 2, :], acc["n", n, m][:])
+        def products0(s):
+            for n in range(2):
+                product0(s, n)
 
-        def n_store(e, n, q):
-            cols = slice(n * N_TILE, (n + 1) * N_TILE)
-            if n == 0:
-                nc.sync.dma_start(out=out1_v[:, 2 * q : 2 * q + 2, cols], in_=res["n", n, q][:])
-            else:
-                nc.sync.dma_start(out=out1_v[:, q, cols], in_=res["n", n, q // 2][:, q % 2, :])
+        def results0(s):
+            for n in range(2):
+                result0(s, n)
+            store0(s)
 
-        kinds = {"W": "w", "D": "d", "X": "x"}
-        for item in ORDER.split():
-            name, e = item.split("/")
-            d = [int(ch) for ch in name if ch in "0123456789"]
-            c = name[0]
-            if c == "L":
-                if name[1] == "w":
-                    fetch_w(e, d[0])
-                elif name[1] == "x":
-                    fetch(e, "x", d[0], 0, PACK)
-                else:
-                    step = 1 if d[0] == 0 else 2
-                    lo = ["a", "b", "c", "d"].index(name[2]) * step
-                    fetch(e, name[1], d[0], lo, lo + step)
-            elif c in kinds or name[:2] == "dq":
-                kind = kinds.get(c, "d")
-                if name[1] == "q":
-                    quantize(e, kind, d[0], d[1])
-                else:
-                    interleave(e, kind, d[0], d[1])
-            elif name.startswith("dmu"):
-                do_dmu(e, d[0], d[1])
-            elif name.startswith("sig"):
-                do_sig(e, d[0], d[1])
-            elif name.startswith("stt"):
-                do_stt(e, d[0], d[1])
-            elif name.startswith("tt"):
-                do_tt(e, d[0], d[1])
-            elif c in "AB":
-                turn(e, d[0], d[1], int(c == "B"))
-            elif c in "ab":
-                turn_out(e, d[0], d[1], int(c == "b"))
-            elif c == "Z":
-                z_quant(e, d[0], d[1])
-            elif c == "M":
-                m_pass(e, d[0], d[1], d[2])
-            elif c == "m":
-                m_out(e, d[0], d[1], d[2])
-            elif c == "O":
-                m_store(e, d[0], d[1])
-            elif c == "N":
-                n_pass(e, d[0], d[1], name[3])
-            elif c == "n":
-                n_out(e, d[0], d[1])
-            else:
-                n_store(e, d[0], d[1])
+        def front(i):
+            first_product(i)
+            make_dmu(i)
+            make_dv(i)
+            turn(i, 0)
+            turn(i, 1)
+
+        def quadrant(n, g, first, final):
+            for m in range(4):
+                pass1(m, n, g, first, final)
+
+        H = N_TILE
+        SW = 256
+        sigmoid(0)
+        front(0)
+        halves = [("w", k, lo, H) for k in range(4) for lo in (0, H)]
+        for q, half in enumerate(halves):
+            interleave("V", half, 0, H - SW)
+            interleave("S", half, H - SW, H)
+            if q < 2:
+                turn_out(0, q)
+            if q == 2:
+                quantize_dz(0)
+            if q:
+                quantize(halves[q - 1])
+        for g in range(GROUPS):
+            if g:
+                load_slices(g * PACK + 2, 2)
+            if g + 1 < GROUPS:
+                load_slices((g + 1) * PACK, 2)
+                load_x(g)
+        load_x(2)
+        sigmoid(1)
+        first_product(1)
+        quantize(halves[-1])
+        products0(0)
+        make_dmu(1)
+        make_dv(1)
+        turn(1, 0)
+        turn(1, 1)
+        sigmoid(2)
+        turn_out(1, 0)
+        turn_out(1, 1)
+        results0(0)
+        sigmoid(3)
+        last = SLICES - 1
+        ES = 256
+        for i in range(2, SLICES):
+            front(i)
+            turn_out(i, 0)
+            turn_out(i, 1)
+            if i + 2 < SLICES:
+                sigmoid(i + 2)
+            if i == 4 + 1:
+                quantize(("d", 0, 0, H))
+            g, half = divmod(i - 4, 2)
+            if g - 1 in range(GROUPS) and half == 1:
+                quantize(("x", g - 1, 0, H))
+            quantize_dz(i - 1)
+            if i == 4:
+                interleave("V", ("d", 0, 0, H))
+            if g in range(GROUPS):
+                interleave("S", ("x", g, 0, H), half * ES // 2, (half + 1) * ES // 2)
+                if half:
+                    interleave("V", ("x", g, 0, H), ES, H)
+            products0(i - 1)
+            results0(i - 1)
+        interleave("S", ("x", 0, H, H))
+        for n in range(2):
+            acc[last, n] = psum.tile([P, N_TILE], F32, tag="bank", name="bank")
+        quadrant(0, 0, True, False)
+        on_vector = [("d", 1, 0, H), ("d", 2, 0, H), ("x", 2, H, H), ("x", 1, H, H)]
+        on_vector += [("d", g, lo, 256) for lo in (H, H + 256) for g in range(GROUPS)]
+        interleave("V", on_vector[0])
+        quantize_dz(last)
+        products0(last)
+        results0(last)
+        for q, piece in enumerate(on_vector):
+            if q + 1 < len(on_vector):
+                interleave("V", on_vector[q + 1])
+            quantize(piece)
+            kind, g, lo, width = piece
+            if kind == "d" and lo == 0:
+                quadrant(0, g, False, g == 2)
+            if kind == "x":
+                quadrant(1, g, g == 2, g == 1)
+                if g == 2:
+                    quantize(("x", 0, H, H))
+                    quadrant(1, 0, False, False)
+                for m in range(4):
+                    result1("S", m, 2 - g)
+            if kind == "d" and g == 2 and lo >= H:
+                for m in range(lo // P, lo // P + 2):
+                    for n in range(2):
+                        for gg in range(GROUPS):
+                            pass1(m, n, gg, gg == 0, gg == 2)
+                        result1("V" if q + 1 == len(on_vector) and n else "S", m, n)

@@ -47,19 +47,21 @@ def tile_diffscm_pb_v_kernel(
         w_scales = keep.tile([P, 4 * D], U8, align_bytes=64, name="w_scales")
         x_codes = keep.tile([P, GROUPS * D], U32, align_bytes=64, name="x_codes")
         x_scales = keep.tile([P, GROUPS * D], U8, align_bytes=64, name="x_scales")
-        d_codes = keep.tile([P, GROUPS * D], U32, align_bytes=64, name="d_codes")
-        d_scales = keep.tile([P, GROUPS * D], U8, align_bytes=64, name="d_scales")
+        d_codes = keep.tile([P, GROUPS * N_TILE], U32, align_bytes=64, name="d_codes")
+        d_scales = keep.tile([P, GROUPS * N_TILE], U8, align_bytes=64, name="d_scales")
         planes = {"w": (w_codes, w_scales, E4M3), "x": (x_codes, x_scales, E4M3), "d": (d_codes, d_scales, E5M2)}
 
         def big_tile(shape, dtype):
             return inp.tile(shape, dtype, tag="big", bufs=7, name="big")
 
         raw = {}
+        e_all = inp.tile([P, SLICES * D], BF16, name="e_all")
         for k in range(4):
             raw["w", k] = big_tile([P, PACK * D], BF16)
         for g in range(GROUPS):
             raw["g", g] = big_tile([P, PACK * D], BF16)
-            raw["e", g] = inp.tile([P, PACK * D], BF16, tag="e", bufs=GROUPS, name="raw_e")
+            raw["e", g] = e_all[:, g * PACK * D : (g + 1) * PACK * D]
+            raw["d", g] = raw["e", g]
             raw["v", g] = inp.tile([P, PACK * D], F32, tag="v", bufs=GROUPS, name="raw_v")
 
         def part(kind, i, n=1):
@@ -68,7 +70,7 @@ def tile_diffscm_pb_v_kernel(
 
         def load_slices(i, n):
             g, j = divmod(i, PACK)
-            for kind in "vge":
+            for kind in "vge" if i else "gev":
                 nc.sync.dma_start(out=part(kind, i, n), in_=hbm[kind][g][:, j * D : (j + n) * D])
 
         def load_w(k):
@@ -84,7 +86,7 @@ def tile_diffscm_pb_v_kernel(
             else:
                 nc.scalar.copy(out=out, in_=in_)
 
-        grp, prod, dmu, banks, dzt, dz, acc, acc1 = {}, {}, {}, {}, {}, {}, {}, {}
+        grp, prod, dmu, banks, dzt, dz, acc, acc1, dv_mx = {}, {}, {}, {}, {}, {}, {}, {}, {}
 
         def interleave(engine, piece, a=0, b=None):
             kind, k, lo, width = piece
@@ -95,12 +97,6 @@ def tile_diffscm_pb_v_kernel(
                 tag = "grp" + engine
                 grp[piece] = work.tile([P, width * PACK], BF16, tag=tag, bufs=3, align_bytes=64, name=tag)
             tile = grp[piece]
-            if kind == "d":
-                dst = tile[:].rearrange("p (w a u e t) -> p u w t a e", a=2, u=2, e=2, t=PACK)
-                src = raw["e", k][:].rearrange("p (t u w a e) -> p u w t a e", t=PACK, u=2, a=2, e=2)
-                for u in range(2):
-                    copy(engine, dst[:, u, a // 8 : b // 8], src[:, u, (lo + a) // 8 : (lo + b) // 8])
-                return
             dst = tile[:].rearrange("p (c i t) -> p c t i", i=4, t=PACK)
             src = raw[kind, k][:].rearrange("p (t c i) -> p c t i", t=PACK, i=4)
             copy(engine, dst[:, a // 4 : b // 4], src[:, (lo + a) // 4 : (lo + b) // 4])
@@ -108,8 +104,26 @@ def tile_diffscm_pb_v_kernel(
         def quantize(piece):
             kind, k, lo, width = piece
             codes, scales, fmt = planes[kind]
-            c = slice(k * D + lo, k * D + lo + width)
+            first = k * (N_TILE if kind == "d" else D) + lo
+            c = slice(first, first + width)
             nc.vector.quantize_mx(out=codes[:, c].bitcast(fmt), scales=scales[:, c], in_=grp[piece][:])
+
+        def interleave_rows(m):
+            grp[m] = work.tile([P, GROUPS * P * PACK], BF16, tag="grpV", bufs=3, align_bytes=64, name="grpV")
+            src = e_all[:].rearrange("p (g t c i) -> p g c t i", g=GROUPS, t=PACK, i=4)
+            dst = grp[m][:].rearrange("p (g c i t) -> p g c t i", g=GROUPS, i=4, t=PACK)
+            for lo, hi in ((0, 2), (2, 3)):
+                nc.vector.tensor_copy(out=dst[:, lo:hi], in_=src[:, lo:hi, m * P // 4 : (m + 1) * P // 4])
+
+        def quantize_rows(m):
+            codes = work.tile([P, GROUPS * P], U32, tag="rc", bufs=3, align_bytes=64, name="rc")
+            scales = work.tile([P, GROUPS * P], U8, tag="rs", bufs=3, align_bytes=64, name="rs")
+            for lo, hi in ((0, 2 * P), (2 * P, 3 * P)):
+                nc.vector.quantize_mx(
+                    out=codes[:, lo:hi].bitcast(E5M2), scales=scales[:, lo:hi], in_=grp[m][:, lo * PACK : hi * PACK]
+                )
+            for g in range(GROUPS):
+                dv_mx[g, m] = (codes[:, g * P : (g + 1) * P], scales[:, g * P : (g + 1) * P])
 
         def sigmoid(i):
             nc.scalar.activation(out=part("v", i), in_=part("v", i), func=SIGMOID)
@@ -131,7 +145,7 @@ def tile_diffscm_pb_v_kernel(
 
         def make_dv(i):
             nc.vector.tensor_tensor(
-                out=sorted_out(part("e", i)), in0=sorted_in(prod[i][:]), in1=sorted_in(part("v", i)), op=MULT
+                out=part("e", i), in0=prod[i][:], in1=part("v", i), op=MULT
             )
 
         def turn(i, head):
@@ -139,7 +153,11 @@ def tile_diffscm_pb_v_kernel(
             words = (part("e", i) if head else dmu[i][:]).bitcast(F32)
             for k in range(2):
                 for u in range(2):
-                    nc.tensor.transpose(bank[:, k, u, :], words[:, 256 * u + P * k : 256 * u + P * (k + 1)], ident[:])
+                    if head:
+                        block = words[:, 256 * k + u : 256 * (k + 1) : 2]
+                    else:
+                        block = words[:, 256 * u + P * k : 256 * u + P * (k + 1)]
+                    nc.tensor.transpose(bank[:, k, u, :], block, ident[:])
             banks[i, head] = bank
 
         def turn_out(i, head):
@@ -178,14 +196,19 @@ def tile_diffscm_pb_v_kernel(
             g, j = divmod(i, PACK)
             nc.sync.dma_start(out=out0_v[g][:, j * D : (j + 1) * D], in_=part("v", i))
 
+        for g in range(GROUPS):
+            for m in range(4):
+                rows = slice(g * N_TILE + m * P, g * N_TILE + (m + 1) * P)
+                dv_mx[g, m] = (d_codes[:, rows], d_scales[:, rows])
+
         def pass1(m, n, g, first, final):
             if first:
                 acc1[m, n] = psum.tile([P, N_TILE], F32, tag="bank", name="bank")
-            rows = slice(g * D + m * P, g * D + (m + 1) * P)
+            codes, scales = dv_mx[g, m]
             cols = slice(g * D + n * N_TILE, g * D + (n + 1) * N_TILE)
             nc.tensor.matmul_mx(
                 out=acc1[m, n][:],
-                lhsT=d_codes[:, rows].bitcast(E5M2), lhsT_scale=d_scales[:, rows],
+                lhsT=codes.bitcast(E5M2), lhsT_scale=scales,
                 rhs=x_codes[:, cols].bitcast(E4M3), rhs_scale=x_scales[:, cols],
                 start=first, stop=final,
             )
@@ -231,21 +254,22 @@ def tile_diffscm_pb_v_kernel(
         sigmoid(0)
         front(0)
         halves = [("w", k, lo, H) for k in range(4) for lo in (0, H)]
+        turn_out(0, 0)
         for q, half in enumerate(halves):
             interleave("V", half, 0, H - SW)
             interleave("S", half, H - SW, H)
-            if q < 2:
-                turn_out(0, q)
+            if q == 0:
+                turn_out(0, 1)
             if q == 2:
                 quantize_dz(0)
             if q:
                 quantize(halves[q - 1])
-        for g in range(GROUPS):
-            if g:
-                load_slices(g * PACK + 2, 2)
-            if g + 1 < GROUPS:
-                load_slices((g + 1) * PACK, 2)
-                load_x(g)
+        load_slices(4, 2)
+        load_slices(6, 2)
+        load_slices(8, 2)
+        load_x(0)
+        load_slices(10, 2)
+        load_x(1)
         load_x(2)
         sigmoid(1)
         first_product(1)
@@ -261,43 +285,45 @@ def tile_diffscm_pb_v_kernel(
         results0(0)
         sigmoid(3)
         last = SLICES - 1
-        ES = 256
+        ES = 192
+        early = [("d", 0, 0, H), ("x", 0, 0, H), ("x", 1, 0, H)]
         for i in range(2, SLICES):
             front(i)
             turn_out(i, 0)
             turn_out(i, 1)
             if i + 2 < SLICES:
                 sigmoid(i + 2)
-            if i == 4 + 1:
-                quantize(("d", 0, 0, H))
-            g, half = divmod(i - 4, 2)
-            if g - 1 in range(GROUPS) and half == 1:
-                quantize(("x", g - 1, 0, H))
             quantize_dz(i - 1)
-            if i == 4:
-                interleave("V", ("d", 0, 0, H))
-            if g in range(GROUPS):
-                interleave("S", ("x", g, 0, H), half * ES // 2, (half + 1) * ES // 2)
+            e, half = divmod(i - 4, 2)
+            if e - 1 in range(len(early)) and half == 1:
+                quantize(early[e - 1])
+            if e in range(len(early)):
+                interleave("S", early[e], half * ES // 2, (half + 1) * ES // 2)
                 if half:
-                    interleave("V", ("x", g, 0, H), ES, H)
+                    interleave("V", early[e], ES, H)
             products0(i - 1)
+            if i == last:
+                interleave("S", ("x", 2, 0, H))
             results0(i - 1)
-        interleave("S", ("x", 0, H, H))
         for n in range(2):
             acc[last, n] = psum.tile([P, N_TILE], F32, tag="bank", name="bank")
         quadrant(0, 0, True, False)
         on_vector = [("d", 1, 0, H), ("d", 2, 0, H), ("x", 2, H, H), ("x", 1, H, H)]
-        on_vector += [("d", g, lo, 256) for lo in (H, H + 256) for g in range(GROUPS)]
         interleave("V", on_vector[0])
         quantize_dz(last)
         products0(last)
+        interleave("S", ("x", 0, H, H))
         results0(last)
         for q, piece in enumerate(on_vector):
             if q + 1 < len(on_vector):
                 interleave("V", on_vector[q + 1])
+            else:
+                interleave_rows(4)
             quantize(piece)
             kind, g, lo, width = piece
             if kind == "d" and lo == 0:
+                if g == 2:
+                    quantize(("x", 2, 0, H))
                 quadrant(0, g, False, g == 2)
             if kind == "x":
                 quadrant(1, g, g == 2, g == 1)
@@ -306,9 +332,13 @@ def tile_diffscm_pb_v_kernel(
                     quadrant(1, 0, False, False)
                 for m in range(4):
                     result1("S", m, 2 - g)
-            if kind == "d" and g == 2 and lo >= H:
-                for m in range(lo // P, lo // P + 2):
-                    for n in range(2):
-                        for gg in range(GROUPS):
-                            pass1(m, n, gg, gg == 0, gg == 2)
-                        result1("V" if q + 1 == len(on_vector) and n else "S", m, n)
+        for m in range(4, 8):
+            if m + 1 < 8:
+                interleave_rows(m + 1)
+            quantize_rows(m)
+            for n in range(2):
+                for g in range(GROUPS):
+                    pass1(m, n, g, g == 0, g == 2)
+        for m in range(4, 8):
+            for n in range(2):
+                result1("V" if m >= 6 and n else "S", m, n)

@@ -30,6 +30,7 @@ def tile_diffscm_pb_v_kernel(
     hbm = {"x": by_group(xt), "e": by_group(eps), "v": by_group(v), "g": by_group(grad_out)}
     w_hbm = [by_group(w)[k] for w in (Wm, Wv) for k in range(2)]
     out0_v = by_group(out_0)
+    out1_s = out_1.rearrange("(h w u e) c -> h u e w c", h=4, u=2, e=2)
     out1_v = out_1.rearrange("(m p) w -> m p w", p=P)
 
     with ExitStack() as ctx:
@@ -37,7 +38,7 @@ def tile_diffscm_pb_v_kernel(
         inp = ctx.enter_context(tc.tile_pool(name="inp", bufs=1))
         keep = ctx.enter_context(tc.tile_pool(name="keep", bufs=1))
         work = ctx.enter_context(tc.tile_pool(name="work", bufs=1))
-        psum = ctx.enter_context(tc.psum_pool(name="psum", bufs=8))
+        psum = ctx.enter_context(tc.psum_pool(name="psum", bufs=1))
         ctx.enter_context(tc.manual_schedule())
 
         t_col = const.tile([P, SLICES], BF16, name="t_col")
@@ -64,14 +65,25 @@ def tile_diffscm_pb_v_kernel(
             raw["d", g] = raw["e", g]
             raw["v", g] = inp.tile([P, PACK * D], F32, tag="v", bufs=GROUPS, name="raw_v")
 
+        turnover = list(range(8))
+
+        def take_bank(shape, keep_out=False):
+            b = turnover.pop(0)
+            if not keep_out:
+                turnover.append(b)
+            return b, psum.tile(shape, F32, tag="bank%d" % b, name="bank")
+
         def part(kind, i, n=1):
             g, j = divmod(i, PACK)
             return raw[kind, g][:, j * D : (j + n) * D]
 
         def load_slices(i, n):
             g, j = divmod(i, PACK)
-            for kind in "vge" if i else "gev":
+            for kind in "vge" if i > 1 else "ge":
                 nc.sync.dma_start(out=part(kind, i, n), in_=hbm[kind][g][:, j * D : (j + n) * D])
+            if i < 2:
+                for half in range(2):
+                    nc.sync.dma_start(out=part("v", i)[:, columns(half)], in_=hbm["v"][0][:, i * D : (i + 1) * D][:, columns(half)])
 
         def load_w(k):
             nc.sync.dma_start(out=raw["w", k][:], in_=w_hbm[k])
@@ -86,7 +98,7 @@ def tile_diffscm_pb_v_kernel(
             else:
                 nc.scalar.copy(out=out, in_=in_)
 
-        grp, prod, dmu, banks, dzt, dz, acc, acc1, dv_mx = {}, {}, {}, {}, {}, {}, {}, {}, {}
+        grp, prod, dmu, banks, dzt, dz, acc, acc1, dv_mx, held = {}, {}, {}, {}, {}, {}, {}, {}, {}, {}
 
         def interleave(engine, piece, a=0, b=None):
             kind, k, lo, width = piece
@@ -97,6 +109,12 @@ def tile_diffscm_pb_v_kernel(
                 tag = "grp" + engine
                 grp[piece] = work.tile([P, width * PACK], BF16, tag=tag, bufs=3, align_bytes=64, name=tag)
             tile = grp[piece]
+            if kind == "d":
+                dst = tile[:].rearrange("p (w a u e t) -> p u w t a e", a=2, u=2, e=2, t=PACK)
+                src = raw["e", k].rearrange("p (t u w a e) -> p u w t a e", t=PACK, u=2, a=2, e=2)
+                for u in range(2):
+                    copy(engine, dst[:, u, a // 8 : b // 8], src[:, u, (lo + a) // 8 : (lo + b) // 8])
+                return
             dst = tile[:].rearrange("p (c i t) -> p c t i", i=4, t=PACK)
             src = raw[kind, k][:].rearrange("p (t c i) -> p c t i", t=PACK, i=4)
             copy(engine, dst[:, a // 4 : b // 4], src[:, (lo + a) // 4 : (lo + b) // 4])
@@ -108,12 +126,13 @@ def tile_diffscm_pb_v_kernel(
             c = slice(first, first + width)
             nc.vector.quantize_mx(out=codes[:, c].bitcast(fmt), scales=scales[:, c], in_=grp[piece][:])
 
-        def interleave_rows(m):
+        def interleave_rows(m, third):
             grp[m] = work.tile([P, GROUPS * P * PACK], BF16, tag="grpV", bufs=3, align_bytes=64, name="grpV")
             src = e_all[:].rearrange("p (g t c i) -> p g c t i", g=GROUPS, t=PACK, i=4)
+            first = m % 2 * N_TILE + m // 2 * P
             dst = grp[m][:].rearrange("p (g c i t) -> p g c t i", g=GROUPS, i=4, t=PACK)
-            for lo, hi in ((0, 2), (2, 3)):
-                nc.vector.tensor_copy(out=dst[:, lo:hi], in_=src[:, lo:hi, m * P // 4 : (m + 1) * P // 4])
+            for engine, lo, hi in (("V", 0, 2), (third, 2, 3)):
+                copy(engine, dst[:, lo:hi], src[:, lo:hi, first // 4 : (first + P) // 4])
 
         def quantize_rows(m):
             codes = work.tile([P, GROUPS * P], U32, tag="rc", bufs=3, align_bytes=64, name="rc")
@@ -125,8 +144,12 @@ def tile_diffscm_pb_v_kernel(
             for g in range(GROUPS):
                 dv_mx[g, m] = (codes[:, g * P : (g + 1) * P], scales[:, g * P : (g + 1) * P])
 
-        def sigmoid(i):
-            nc.scalar.activation(out=part("v", i), in_=part("v", i), func=SIGMOID)
+        def columns(half):
+            return slice(0, D) if half is None else slice(half * N_TILE, (half + 1) * N_TILE)
+
+        def sigmoid(i, half=None):
+            values = part("v", i)[:, columns(half)]
+            nc.scalar.activation(out=values, in_=values, func=SIGMOID)
 
         def first_product(i):
             prod[i] = work.tile([P, D], F32, tag="prod", bufs=2, name="prod")
@@ -143,20 +166,19 @@ def tile_diffscm_pb_v_kernel(
                 out=sorted_out(dmu[i][:]), in0=sorted_in(part("g", i)), scalar1=t_col[:, i : i + 1], scalar2=None, op0=MULT
             )
 
-        def make_dv(i):
+        def make_dv(i, half=None):
+            words = slice(0, 256) if half is None else slice(half * P, (half + 1) * P)
             nc.vector.tensor_tensor(
-                out=part("e", i), in0=prod[i][:], in1=part("v", i), op=MULT
+                out=sorted_out(part("e", i))[:, :, words], in0=sorted_in(prod[i][:])[:, :, words],
+                in1=sorted_in(part("v", i))[:, :, words], op=MULT,
             )
 
         def turn(i, head):
-            bank = psum.tile([P, 2, 2, P], F32, tag="bank", name="bank")
+            bank = take_bank([P, 2, 2, P])[1]
             words = (part("e", i) if head else dmu[i][:]).bitcast(F32)
             for k in range(2):
                 for u in range(2):
-                    if head:
-                        block = words[:, 256 * k + u : 256 * (k + 1) : 2]
-                    else:
-                        block = words[:, 256 * u + P * k : 256 * u + P * (k + 1)]
+                    block = words[:, 256 * u + P * k : 256 * u + P * (k + 1)]
                     nc.tensor.transpose(bank[:, k, u, :], block, ident[:])
             banks[i, head] = bank
 
@@ -170,14 +192,13 @@ def tile_diffscm_pb_v_kernel(
             )
 
         def quantize_dz(i):
-            codes = work.tile([P, 4 * P], U32, tag="zc", bufs=3, align_bytes=64, name="zc")
-            scales = work.tile([P, 4 * P], U8, tag="zs", bufs=3, align_bytes=64, name="zs")
+            codes = work.tile([P, 4 * P], U32, tag="zc", bufs=4, align_bytes=64, name="zc")
+            scales = work.tile([P, 4 * P], U8, tag="zs", bufs=4, align_bytes=64, name="zs")
             nc.vector.quantize_mx(out=codes[:].bitcast(E5M2), scales=scales[:], in_=dzt[i][:])
             dz[i] = (codes, scales)
 
         def product0(i, n):
-            if (i, n) not in acc:
-                acc[i, n] = psum.tile([P, N_TILE], F32, tag="bank", name="bank")
+            acc[i, n] = take_bank([P, N_TILE])[1]
             codes, scales = dz[i]
             for k in range(4):
                 rows = slice(k * P, (k + 1) * P)
@@ -203,7 +224,7 @@ def tile_diffscm_pb_v_kernel(
 
         def pass1(m, n, g, first, final):
             if first:
-                acc1[m, n] = psum.tile([P, N_TILE], F32, tag="bank", name="bank")
+                held[m, n], acc1[m, n] = take_bank([P, N_TILE], keep_out=True)
             codes, scales = dv_mx[g, m]
             cols = slice(g * D + n * N_TILE, g * D + (n + 1) * N_TILE)
             nc.tensor.matmul_mx(
@@ -216,15 +237,21 @@ def tile_diffscm_pb_v_kernel(
         def result1(engine, m, n):
             res = big_tile([P, N_TILE], F32)
             copy(engine, res[:], acc1[m, n][:])
-            nc.sync.dma_start(out=out1_v[m][:, n * N_TILE : (n + 1) * N_TILE], in_=res[:])
+            turnover.append(held[m, n])
+            cols = slice(n * N_TILE, (n + 1) * N_TILE)
+            if m < 4:
+                nc.sync.dma_start(out=out1_v[m][:, cols], in_=res[:])
+            else:
+                for e in range(2):
+                    nc.sync.dma_start(out=out1_s[m // 2, m % 2, e][:, cols], in_=res[e:P:2, :])
 
         nc.scalar.dma_start(out=t_col[:].rearrange("p (g j) -> p g j", j=PACK), in_=t_rand.rearrange("(g p j) o -> p g (j o)", p=P, j=PACK))
         load_slices(0, 1)
+        load_slices(1, 1)
         load_w(0)
         load_w(1)
         load_w(2)
         load_w(3)
-        load_slices(1, 1)
         load_slices(2, 1)
         load_slices(3, 1)
         make_identity(nc, ident[:])
@@ -249,19 +276,35 @@ def tile_diffscm_pb_v_kernel(
             for m in range(4):
                 pass1(m, n, g, first, final)
 
+        def rows1(m):
+            for n in range(2):
+                for g in range(GROUPS):
+                    pass1(m, n, g, g == 0, g == 2)
+
         H = N_TILE
         SW = 256
-        sigmoid(0)
-        front(0)
-        halves = [("w", k, lo, H) for k in range(4) for lo in (0, H)]
+        first_product(0)
+        make_dmu(0)
+        turn(0, 0)
+        for half in range(2):
+            sigmoid(0, half)
+            make_dv(0, half)
+        turn(0, 1)
         turn_out(0, 0)
+        sigmoid(1, 0)
+        sigmoid(1, 1)
+        turn_out(0, 1)
+        front(1)
+        halves = [("w", k, lo, H) for k in range(4) for lo in (0, H)]
+        quantize_dz(0)
+        turn_out(1, 0)
         for q, half in enumerate(halves):
             interleave("V", half, 0, H - SW)
             interleave("S", half, H - SW, H)
             if q == 0:
-                turn_out(0, 1)
+                turn_out(1, 1)
             if q == 2:
-                quantize_dz(0)
+                quantize_dz(1)
             if q:
                 quantize(halves[q - 1])
         load_slices(4, 2)
@@ -271,29 +314,28 @@ def tile_diffscm_pb_v_kernel(
         load_slices(10, 2)
         load_x(1)
         load_x(2)
-        sigmoid(1)
-        first_product(1)
+        sigmoid(2)
+        first_product(2)
         quantize(halves[-1])
         products0(0)
-        make_dmu(1)
-        make_dv(1)
-        turn(1, 0)
-        turn(1, 1)
-        sigmoid(2)
-        turn_out(1, 0)
-        turn_out(1, 1)
-        results0(0)
         sigmoid(3)
+        results0(0)
         last = SLICES - 1
         ES = 192
         early = [("d", 0, 0, H), ("x", 0, 0, H), ("x", 1, 0, H)]
         for i in range(2, SLICES):
-            front(i)
+            if i > 2:
+                first_product(i)
+            make_dmu(i)
+            make_dv(i)
+            turn(i, 0)
+            turn(i, 1)
             turn_out(i, 0)
             turn_out(i, 1)
             if i + 2 < SLICES:
                 sigmoid(i + 2)
-            quantize_dz(i - 1)
+            if i > 2:
+                quantize_dz(i - 1)
             e, half = divmod(i - 4, 2)
             if e - 1 in range(len(early)) and half == 1:
                 quantize(early[e - 1])
@@ -302,43 +344,40 @@ def tile_diffscm_pb_v_kernel(
                 if half:
                     interleave("V", early[e], ES, H)
             products0(i - 1)
+            if i == 11:
+                quadrant(0, 0, True, False)
             if i == last:
                 interleave("S", ("x", 2, 0, H))
             results0(i - 1)
-        for n in range(2):
-            acc[last, n] = psum.tile([P, N_TILE], F32, tag="bank", name="bank")
-        quadrant(0, 0, True, False)
-        on_vector = [("d", 1, 0, H), ("d", 2, 0, H), ("x", 2, H, H), ("x", 1, H, H)]
-        interleave("V", on_vector[0])
+        d1, d2 = ("d", 1, 0, H), ("d", 2, 0, H)
+        x_right = [("x", g, H, H) for g in range(GROUPS)]
+        interleave("V", d1)
         quantize_dz(last)
         products0(last)
-        interleave("S", ("x", 0, H, H))
+        interleave("S", x_right[0])
         results0(last)
-        for q, piece in enumerate(on_vector):
-            if q + 1 < len(on_vector):
-                interleave("V", on_vector[q + 1])
-            else:
-                interleave_rows(4)
-            quantize(piece)
-            kind, g, lo, width = piece
-            if kind == "d" and lo == 0:
-                if g == 2:
-                    quantize(("x", 2, 0, H))
-                quadrant(0, g, False, g == 2)
-            if kind == "x":
-                quadrant(1, g, g == 2, g == 1)
-                if g == 2:
-                    quantize(("x", 0, H, H))
-                    quadrant(1, 0, False, False)
-                for m in range(4):
-                    result1("S", m, 2 - g)
+        interleave("V", d2)
+        quantize(d1)
+        quadrant(0, 1, False, False)
+        interleave("V", x_right[2])
+        quantize(d2)
+        quantize(("x", 2, 0, H))
+        quadrant(0, 2, False, True)
+        for m in range(4):
+            result1("S", m, 0)
+        quantize(x_right[2])
+        quadrant(1, 2, True, False)
+        interleave("V", x_right[1])
+        quantize(x_right[0])
+        quadrant(1, 0, False, False)
+        quantize(x_right[1])
+        quadrant(1, 1, False, True)
+        for m in range(4):
+            result1("S", m, 1)
         for m in range(4, 8):
-            if m + 1 < 8:
-                interleave_rows(m + 1)
+            interleave_rows(m, "V")
             quantize_rows(m)
-            for n in range(2):
-                for g in range(GROUPS):
-                    pass1(m, n, g, g == 0, g == 2)
+            rows1(m)
         for m in range(4, 8):
             for n in range(2):
                 result1("V" if m >= 6 and n else "S", m, n)

@@ -30,7 +30,6 @@ def tile_diffscm_pb_v_kernel(
     hbm = {"x": by_group(xt), "e": by_group(eps), "v": by_group(v), "g": by_group(grad_out)}
     w_hbm = [by_group(w)[k] for w in (Wm, Wv) for k in range(2)]
     out0_v = by_group(out_0)
-    out1_s = out_1.rearrange("(h w u e) c -> h u e w c", h=4, u=2, e=2)
     out1_v = out_1.rearrange("(m p) w -> m p w", p=P)
 
     with ExitStack() as ctx:
@@ -98,7 +97,7 @@ def tile_diffscm_pb_v_kernel(
             else:
                 nc.scalar.copy(out=out, in_=in_)
 
-        grp, prod, dmu, banks, dzt, dz, acc, acc1, dv_mx, held = {}, {}, {}, {}, {}, {}, {}, {}, {}, {}
+        grp, prod, dmu, banks, dzt, dz, acc, acc1, dv_mx, held, res = {}, {}, {}, {}, {}, {}, {}, {}, {}, {}, {}
 
         def interleave(engine, piece, a=0, b=None):
             kind, k, lo, width = piece
@@ -109,12 +108,6 @@ def tile_diffscm_pb_v_kernel(
                 tag = "grp" + engine
                 grp[piece] = work.tile([P, width * PACK], BF16, tag=tag, bufs=3, align_bytes=64, name=tag)
             tile = grp[piece]
-            if kind == "d":
-                dst = tile[:].rearrange("p (w a u e t) -> p u w t a e", a=2, u=2, e=2, t=PACK)
-                src = raw["e", k].rearrange("p (t u w a e) -> p u w t a e", t=PACK, u=2, a=2, e=2)
-                for u in range(2):
-                    copy(engine, dst[:, u, a // 8 : b // 8], src[:, u, (lo + a) // 8 : (lo + b) // 8])
-                return
             dst = tile[:].rearrange("p (c i t) -> p c t i", i=4, t=PACK)
             src = raw[kind, k][:].rearrange("p (t c i) -> p c t i", t=PACK, i=4)
             copy(engine, dst[:, a // 4 : b // 4], src[:, (lo + a) // 4 : (lo + b) // 4])
@@ -129,7 +122,7 @@ def tile_diffscm_pb_v_kernel(
         def interleave_rows(m, third):
             grp[m] = work.tile([P, GROUPS * P * PACK], BF16, tag="grpV", bufs=3, align_bytes=64, name="grpV")
             src = e_all[:].rearrange("p (g t c i) -> p g c t i", g=GROUPS, t=PACK, i=4)
-            first = m % 2 * N_TILE + m // 2 * P
+            first = m * P
             dst = grp[m][:].rearrange("p (g c i t) -> p g c t i", g=GROUPS, i=4, t=PACK)
             for engine, lo, hi in (("V", 0, 2), (third, 2, 3)):
                 copy(engine, dst[:, lo:hi], src[:, lo:hi, first // 4 : (first + P) // 4])
@@ -167,10 +160,8 @@ def tile_diffscm_pb_v_kernel(
             )
 
         def make_dv(i, half=None):
-            words = slice(0, 256) if half is None else slice(half * P, (half + 1) * P)
             nc.vector.tensor_tensor(
-                out=sorted_out(part("e", i))[:, :, words], in0=sorted_in(prod[i][:])[:, :, words],
-                in1=sorted_in(part("v", i))[:, :, words], op=MULT,
+                out=part("e", i)[:, columns(half)], in0=prod[i][:, columns(half)], in1=part("v", i)[:, columns(half)], op=MULT
             )
 
         def turn(i, head):
@@ -178,7 +169,10 @@ def tile_diffscm_pb_v_kernel(
             words = (part("e", i) if head else dmu[i][:]).bitcast(F32)
             for k in range(2):
                 for u in range(2):
-                    block = words[:, 256 * u + P * k : 256 * u + P * (k + 1)]
+                    if head:
+                        block = words[:, 256 * k + u : 256 * (k + 1) : 2]
+                    else:
+                        block = words[:, 256 * u + P * k : 256 * u + P * (k + 1)]
                     nc.tensor.transpose(bank[:, k, u, :], block, ident[:])
             banks[i, head] = bank
 
@@ -234,16 +228,14 @@ def tile_diffscm_pb_v_kernel(
                 start=first, stop=final,
             )
 
-        def result1(engine, m, n):
-            res = big_tile([P, N_TILE], F32)
-            copy(engine, res[:], acc1[m, n][:])
-            turnover.append(held[m, n])
-            cols = slice(n * N_TILE, (n + 1) * N_TILE)
-            if m < 4:
-                nc.sync.dma_start(out=out1_v[m][:, cols], in_=res[:])
-            else:
-                for e in range(2):
-                    nc.sync.dma_start(out=out1_s[m // 2, m % 2, e][:, cols], in_=res[e:P:2, :])
+        def result1(engine, m, n, lo=0, hi=N_TILE):
+            four, place = ((n, m) if m < 4 else (m // 2, m % 2 * 2 + n))
+            if four not in res:
+                res[four] = big_tile([P, 4, N_TILE], F32)
+            copy(engine, res[four][:, place, lo:hi], acc1[m, n][:, lo:hi])
+            if lo == 0:
+                turnover.append(held[m, n])
+            nc.sync.dma_start(out=out1_v[m][:, n * N_TILE + lo : n * N_TILE + hi], in_=res[four][:, place, lo:hi])
 
         nc.scalar.dma_start(out=t_col[:].rearrange("p (g j) -> p g j", j=PACK), in_=t_rand.rearrange("(g p j) o -> p g (j o)", p=P, j=PACK))
         load_slices(0, 1)
@@ -332,10 +324,17 @@ def tile_diffscm_pb_v_kernel(
             turn(i, 1)
             turn_out(i, 0)
             turn_out(i, 1)
-            if i + 2 < SLICES:
-                sigmoid(i + 2)
             if i > 2:
                 quantize_dz(i - 1)
+            products0(i - 1)
+            if i == 11:
+                quadrant(0, 0, True, False)
+            if i == last:
+                interleave("S", ("x", 2, 0, H), 0, H // 2)
+            if i >= 11:
+                results0(i - 1)
+            if i + 2 < SLICES:
+                sigmoid(i + 2)
             e, half = divmod(i - 4, 2)
             if e - 1 in range(len(early)) and half == 1:
                 quantize(early[e - 1])
@@ -343,19 +342,17 @@ def tile_diffscm_pb_v_kernel(
                 interleave("S", early[e], half * ES // 2, (half + 1) * ES // 2)
                 if half:
                     interleave("V", early[e], ES, H)
-            products0(i - 1)
-            if i == 11:
-                quadrant(0, 0, True, False)
-            if i == last:
-                interleave("S", ("x", 2, 0, H))
-            results0(i - 1)
+            if i < 11:
+                results0(i - 1)
+        interleave("S", ("x", 2, 0, H), H // 2, H)
         d1, d2 = ("d", 1, 0, H), ("d", 2, 0, H)
         x_right = [("x", g, H, H) for g in range(GROUPS)]
         interleave("V", d1)
         quantize_dz(last)
         products0(last)
-        interleave("S", x_right[0])
+        interleave("S", x_right[0], 0, H // 2)
         results0(last)
+        interleave("S", x_right[0], H // 2, H)
         interleave("V", d2)
         quantize(d1)
         quadrant(0, 1, False, False)

@@ -9,6 +9,7 @@ PACK = 4
 GROUPS = B // (P * PACK)
 SLICES = GROUPS * PACK
 N_TILE = 512
+RUN = 2
 FLOPS = 2 * B * D * D * 3
 BYTES = 2 * (3 * B * D + 2 * D * D + B) + 4 * B * D + 4 * (B * D + D * D)
 
@@ -108,9 +109,9 @@ def tile_diffscm_pb_v_kernel(
                 tag = "grp" + engine
                 grp[piece] = work.tile([P, width * PACK], BF16, tag=tag, bufs=3, align_bytes=64, name=tag)
             tile = grp[piece]
-            dst = tile[:].rearrange("p (c i t) -> p c t i", i=4, t=PACK)
-            src = raw[kind, k][:].rearrange("p (t c i) -> p c t i", t=PACK, i=4)
-            copy(engine, dst[:, a // 4 : b // 4], src[:, (lo + a) // 4 : (lo + b) // 4])
+            dst = tile[:].rearrange("p (c i t) -> p c t i", i=RUN, t=PACK)
+            src = raw[kind, k][:].rearrange("p (t c i) -> p c t i", t=PACK, i=RUN)
+            copy(engine, dst[:, a // RUN : b // RUN], src[:, (lo + a) // RUN : (lo + b) // RUN])
 
         def quantize(piece):
             kind, k, lo, width = piece
@@ -121,11 +122,11 @@ def tile_diffscm_pb_v_kernel(
 
         def interleave_rows(m, third):
             grp[m] = work.tile([P, GROUPS * P * PACK], BF16, tag="grpV", bufs=3, align_bytes=64, name="grpV")
-            src = e_all[:].rearrange("p (g t c i) -> p g c t i", g=GROUPS, t=PACK, i=4)
+            src = e_all[:].rearrange("p (g t c i) -> p g c t i", g=GROUPS, t=PACK, i=RUN)
             first = m * P
-            dst = grp[m][:].rearrange("p (g c i t) -> p g c t i", g=GROUPS, i=4, t=PACK)
+            dst = grp[m][:].rearrange("p (g c i t) -> p g c t i", g=GROUPS, i=RUN, t=PACK)
             for engine, lo, hi in (("V", 0, 2), (third, 2, 3)):
-                copy(engine, dst[:, lo:hi], src[:, lo:hi, first // 4 : (first + P) // 4])
+                copy(engine, dst[:, lo:hi], src[:, lo:hi, first // RUN : (first + P) // RUN])
 
         def quantize_rows(m):
             codes = work.tile([P, GROUPS * P], U32, tag="rc", bufs=3, align_bytes=64, name="rc")

@@ -9,7 +9,7 @@ PACK = 4
 GROUPS = B // (P * PACK)
 SLICES = GROUPS * PACK
 N_TILE = 512
-RUN = 2
+RUN = 8
 FLOPS = 2 * B * D * D * 3
 BYTES = 2 * (3 * B * D + 2 * D * D + B) + 4 * B * D + 4 * (B * D + D * D)
 

@@ -276,8 +276,8 @@ def tile_diffscm_pb_v_kernel(
 
         H = N_TILE
         SW = 256
-        first_product(0)
         make_dmu(0)
+        first_product(0)
         turn(0, 0)
         for half in range(2):
             sigmoid(0, half)
@@ -287,12 +287,19 @@ def tile_diffscm_pb_v_kernel(
         sigmoid(1, 0)
         sigmoid(1, 1)
         turn_out(0, 1)
-        front(1)
+        first_product(1)
+        make_dmu(1)
+        make_dv(1, 0)
+        make_dv(1, 1)
+        turn(1, 0)
+        turn(1, 1)
         halves = [("w", k, lo, H) for k in range(4) for lo in (0, H)]
         quantize_dz(0)
         turn_out(1, 0)
         for q, half in enumerate(halves):
             interleave("V", half, 0, H - SW)
+            if q == 7:
+                sigmoid(2)
             interleave("S", half, H - SW, H)
             if q == 0:
                 turn_out(1, 1)
@@ -307,7 +314,6 @@ def tile_diffscm_pb_v_kernel(
         load_slices(10, 2)
         load_x(1)
         load_x(2)
-        sigmoid(2)
         first_product(2)
         quantize(halves[-1])
         products0(0)
@@ -337,8 +343,8 @@ def tile_diffscm_pb_v_kernel(
             if i + 2 < SLICES:
                 sigmoid(i + 2)
             e, half = divmod(i - 4, 2)
-            if e - 1 in range(len(early)) and half == 1:
-                quantize(early[e - 1])
+            if i in (7, 10, 11):
+                quantize(early[(7, 10, 11).index(i)])
             if e in range(len(early)):
                 interleave("S", early[e], half * ES // 2, (half + 1) * ES // 2)
                 if half:

@@ -384,4 +384,9 @@ def tile_diffscm_pb_v_kernel(
             rows1(m)
         for m in range(4, 8):
             for n in range(2):
-                result1("V" if m >= 6 and n else "S", m, n)
+                engine = "V" if m >= 6 and n else "S"
+                if m < 7:
+                    result1(engine, m, n)
+                else:
+                    result1(engine, m, n, 0, H // 2)
+                    result1(engine, m, n, H // 2, H)

@@ -77,11 +77,15 @@ def tile_diffscm_pb_v_kernel(
             g, j = divmod(i, PACK)
             return raw[kind, g][:, j * D : (j + n) * D]
 
+        def load(kind, i, n):
+            g, j = divmod(i, PACK)
+            nc.sync.dma_start(out=part(kind, i, n), in_=hbm[kind][g][:, j * D : (j + n) * D])
+
         def load_slices(i, n):
             g, j = divmod(i, PACK)
-            for kind in "vge" if i > 1 else "ge":
+            for kind in "vge" if i > 1 else ("gev" if i else "ge"):
                 nc.sync.dma_start(out=part(kind, i, n), in_=hbm[kind][g][:, j * D : (j + n) * D])
-            if i < 2:
+            if i < 1:
                 for half in range(2):
                     nc.sync.dma_start(out=part("v", i)[:, columns(half)], in_=hbm["v"][0][:, i * D : (i + 1) * D][:, columns(half)])
 
@@ -297,17 +301,20 @@ def tile_diffscm_pb_v_kernel(
         quantize_dz(0)
         turn_out(1, 0)
         for q, half in enumerate(halves):
+            if q == 2:
+                quantize_dz(1)
             interleave("V", half, 0, H - SW)
             if q == 7:
                 sigmoid(2)
             interleave("S", half, H - SW, H)
             if q == 0:
                 turn_out(1, 1)
-            if q == 2:
-                quantize_dz(1)
             if q:
                 quantize(halves[q - 1])
-        load_slices(4, 2)
+        load("v", 4, 1)
+        load("g", 4, 2)
+        load("e", 4, 2)
+        load("v", 5, 1)
         load_slices(6, 2)
         load_slices(8, 2)
         load_x(0)
@@ -321,7 +328,7 @@ def tile_diffscm_pb_v_kernel(
         results0(0)
         last = SLICES - 1
         ES = 192
-        early = [("d", 0, 0, H), ("x", 0, 0, H), ("x", 1, 0, H)]
+        early = [("d", 0, 0, H), ("x", 0, 0, H), ("d", 1, 0, H)]
         for i in range(2, SLICES):
             if i > 2:
                 first_product(i)
@@ -352,7 +359,7 @@ def tile_diffscm_pb_v_kernel(
             if i < 11:
                 results0(i - 1)
         interleave("S", ("x", 2, 0, H), H // 2, H)
-        d1, d2 = ("d", 1, 0, H), ("d", 2, 0, H)
+        d1, d2 = ("x", 1, 0, H), ("d", 2, 0, H)
         x_right = [("x", g, H, H) for g in range(GROUPS)]
         interleave("V", d1)
         quantize_dz(last)

@@ -10,6 +10,10 @@ GROUPS = B // (P * PACK)
 SLICES = GROUPS * PACK
 N_TILE = 512
 RUN = 8
+W_PASSES = 4
+ROW_TILES = D // P
+SCALAR_W = 256
+SCALAR_EARLY = 192
 FLOPS = 2 * B * D * D * 3
 BYTES = 2 * (3 * B * D + 2 * D * D + B) + 4 * B * D + 4 * (B * D + D * D)
 
@@ -44,8 +48,8 @@ def tile_diffscm_pb_v_kernel(
         t_col = const.tile([P, SLICES], BF16, name="t_col")
         ident = const.tile([P, P], F32, name="ident")
 
-        w_codes = keep.tile([P, 4 * D], U32, align_bytes=64, name="w_codes")
-        w_scales = keep.tile([P, 4 * D], U8, align_bytes=64, name="w_scales")
+        w_codes = keep.tile([P, W_PASSES * D], U32, align_bytes=64, name="w_codes")
+        w_scales = keep.tile([P, W_PASSES * D], U8, align_bytes=64, name="w_scales")
         x_codes = keep.tile([P, GROUPS * D], U32, align_bytes=64, name="x_codes")
         x_scales = keep.tile([P, GROUPS * D], U8, align_bytes=64, name="x_scales")
         d_codes = keep.tile([P, GROUPS * N_TILE], U32, align_bytes=64, name="d_codes")
@@ -57,7 +61,7 @@ def tile_diffscm_pb_v_kernel(
 
         raw = {}
         e_all = inp.tile([P, SLICES * D], BF16, name="e_all")
-        for k in range(4):
+        for k in range(W_PASSES):
             raw["w", k] = big_tile([P, PACK * D], BF16)
         for g in range(GROUPS):
             raw["g", g] = big_tile([P, PACK * D], BF16)
@@ -82,12 +86,8 @@ def tile_diffscm_pb_v_kernel(
             nc.sync.dma_start(out=part(kind, i, n), in_=hbm[kind][g][:, j * D : (j + n) * D])
 
         def load_slices(i, n):
-            g, j = divmod(i, PACK)
-            for kind in "vge" if i > 1 else ("gev" if i else "ge"):
-                nc.sync.dma_start(out=part(kind, i, n), in_=hbm[kind][g][:, j * D : (j + n) * D])
-            if i < 1:
-                for half in range(2):
-                    nc.sync.dma_start(out=part("v", i)[:, columns(half)], in_=hbm["v"][0][:, i * D : (i + 1) * D][:, columns(half)])
+            for kind in "vge":
+                load(kind, i, n)
 
         def load_w(k):
             nc.sync.dma_start(out=raw["w", k][:], in_=w_hbm[k])
@@ -104,11 +104,8 @@ def tile_diffscm_pb_v_kernel(
 
         grp, prod, dmu, banks, dzt, dz, acc, acc1, dv_mx, held, res = {}, {}, {}, {}, {}, {}, {}, {}, {}, {}, {}
 
-        def interleave(engine, piece, a=0, b=None):
+        def interleave(engine, piece, a=0, b=N_TILE):
             kind, k, lo, width = piece
-            b = width if b is None else b
-            if a == b:
-                return
             if piece not in grp:
                 tag = "grp" + engine
                 grp[piece] = work.tile([P, width * PACK], BF16, tag=tag, bufs=3, align_bytes=64, name=tag)
@@ -124,13 +121,13 @@ def tile_diffscm_pb_v_kernel(
             c = slice(first, first + width)
             nc.vector.quantize_mx(out=codes[:, c].bitcast(fmt), scales=scales[:, c], in_=grp[piece][:])
 
-        def interleave_rows(m, third):
+        def interleave_rows(m):
             grp[m] = work.tile([P, GROUPS * P * PACK], BF16, tag="grpV", bufs=3, align_bytes=64, name="grpV")
             src = e_all[:].rearrange("p (g t c i) -> p g c t i", g=GROUPS, t=PACK, i=RUN)
             first = m * P
             dst = grp[m][:].rearrange("p (g c i t) -> p g c t i", g=GROUPS, i=RUN, t=PACK)
-            for engine, lo, hi in (("V", 0, 2), (third, 2, 3)):
-                copy(engine, dst[:, lo:hi], src[:, lo:hi, first // RUN : (first + P) // RUN])
+            for lo, hi in ((0, 2), (2, 3)):
+                copy("V", dst[:, lo:hi], src[:, lo:hi, first // RUN : (first + P) // RUN])
 
         def quantize_rows(m):
             codes = work.tile([P, GROUPS * P], U32, tag="rc", bufs=3, align_bytes=64, name="rc")
@@ -191,33 +188,33 @@ def tile_diffscm_pb_v_kernel(
             )
 
         def quantize_dz(i):
-            codes = work.tile([P, 4 * P], U32, tag="zc", bufs=4, align_bytes=64, name="zc")
-            scales = work.tile([P, 4 * P], U8, tag="zs", bufs=4, align_bytes=64, name="zs")
+            codes = work.tile([P, W_PASSES * P], U32, tag="zc", bufs=4, align_bytes=64, name="zc")
+            scales = work.tile([P, W_PASSES * P], U8, tag="zs", bufs=4, align_bytes=64, name="zs")
             nc.vector.quantize_mx(out=codes[:].bitcast(E5M2), scales=scales[:], in_=dzt[i][:])
             dz[i] = (codes, scales)
 
         def product0(i, n):
             acc[i, n] = take_bank([P, N_TILE])[1]
             codes, scales = dz[i]
-            for k in range(4):
+            for k in range(W_PASSES):
                 rows = slice(k * P, (k + 1) * P)
                 cols = slice(k * D + n * N_TILE, k * D + (n + 1) * N_TILE)
                 nc.tensor.matmul_mx(
                     out=acc[i, n][:],
                     lhsT=codes[:, rows].bitcast(E5M2), lhsT_scale=scales[:, rows],
                     rhs=w_codes[:, cols].bitcast(E4M3), rhs_scale=w_scales[:, cols],
-                    start=(k == 0), stop=(k == 3),
+                    start=(k == 0), stop=(k == W_PASSES - 1),
                 )
 
         def result0(i, n):
-            nc.scalar.copy(out=part("v", i)[:, n * N_TILE : (n + 1) * N_TILE], in_=acc[i, n][:])
+            nc.scalar.copy(out=part("v", i)[:, columns(n)], in_=acc[i, n][:])
 
         def store0(i):
             g, j = divmod(i, PACK)
             nc.sync.dma_start(out=out0_v[g][:, j * D : (j + 1) * D], in_=part("v", i))
 
         for g in range(GROUPS):
-            for m in range(4):
+            for m in range(ROW_TILES // 2):
                 rows = slice(g * N_TILE + m * P, g * N_TILE + (m + 1) * P)
                 dv_mx[g, m] = (d_codes[:, rows], d_scales[:, rows])
 
@@ -234,7 +231,7 @@ def tile_diffscm_pb_v_kernel(
             )
 
         def result1(engine, m, n, lo=0, hi=N_TILE):
-            four, place = ((n, m) if m < 4 else (m // 2, m % 2 * 2 + n))
+            four, place = (n, m) if m < ROW_TILES // 2 else (m // 2, m % 2 * 2 + n)
             if four not in res:
                 res[four] = big_tile([P, 4, N_TILE], F32)
             copy(engine, res[four][:, place, lo:hi], acc1[m, n][:, lo:hi])
@@ -242,44 +239,40 @@ def tile_diffscm_pb_v_kernel(
                 turnover.append(held[m, n])
             nc.sync.dma_start(out=out1_v[m][:, n * N_TILE + lo : n * N_TILE + hi], in_=res[four][:, place, lo:hi])
 
-        nc.scalar.dma_start(out=t_col[:].rearrange("p (g j) -> p g j", j=PACK), in_=t_rand.rearrange("(g p j) o -> p g (j o)", p=P, j=PACK))
-        load_slices(0, 1)
-        load_slices(1, 1)
-        load_w(0)
-        load_w(1)
-        load_w(2)
-        load_w(3)
+        def products0(i):
+            for n in range(2):
+                product0(i, n)
+
+        def results0(i):
+            for n in range(2):
+                result0(i, n)
+            store0(i)
+
+        def quadrant(n, g, first, final):
+            for m in range(ROW_TILES // 2):
+                pass1(m, n, g, first, final)
+
+        def row_tile(m):
+            for n in range(2):
+                for g in range(GROUPS):
+                    pass1(m, n, g, g == 0, g == GROUPS - 1)
+
+        nc.scalar.dma_start(
+            out=t_col[:].rearrange("p (g j) -> p g j", j=PACK),
+            in_=t_rand.rearrange("(g p j) o -> p g (j o)", p=P, j=PACK),
+        )
+        load("g", 0, 1)
+        load("e", 0, 1)
+        for half in range(2):
+            nc.sync.dma_start(out=part("v", 0)[:, columns(half)], in_=hbm["v"][0][:, 0:D][:, columns(half)])
+        for kind in "gev":
+            load(kind, 1, 1)
+        for k in range(W_PASSES):
+            load_w(k)
         load_slices(2, 1)
         load_slices(3, 1)
         make_identity(nc, ident[:])
 
-        def products0(s):
-            for n in range(2):
-                product0(s, n)
-
-        def results0(s):
-            for n in range(2):
-                result0(s, n)
-            store0(s)
-
-        def front(i):
-            first_product(i)
-            make_dmu(i)
-            make_dv(i)
-            turn(i, 0)
-            turn(i, 1)
-
-        def quadrant(n, g, first, final):
-            for m in range(4):
-                pass1(m, n, g, first, final)
-
-        def rows1(m):
-            for n in range(2):
-                for g in range(GROUPS):
-                    pass1(m, n, g, g == 0, g == 2)
-
-        H = N_TILE
-        SW = 256
         make_dmu(0)
         first_product(0)
         turn(0, 0)
@@ -288,29 +281,31 @@ def tile_diffscm_pb_v_kernel(
             make_dv(0, half)
         turn(0, 1)
         turn_out(0, 0)
-        sigmoid(1, 0)
-        sigmoid(1, 1)
+        for half in range(2):
+            sigmoid(1, half)
         turn_out(0, 1)
         first_product(1)
         make_dmu(1)
-        make_dv(1, 0)
-        make_dv(1, 1)
+        for half in range(2):
+            make_dv(1, half)
         turn(1, 0)
         turn(1, 1)
-        halves = [("w", k, lo, H) for k in range(4) for lo in (0, H)]
         quantize_dz(0)
         turn_out(1, 0)
-        for q, half in enumerate(halves):
-            if q == 2:
+
+        w_pieces = [("w", k, lo, N_TILE) for k in range(W_PASSES) for lo in (0, N_TILE)]
+        for q, piece in enumerate(w_pieces):
+            if piece == ("w", 1, 0, N_TILE):
                 quantize_dz(1)
-            interleave("V", half, 0, H - SW)
-            if q == 7:
+            interleave("V", piece, 0, N_TILE - SCALAR_W)
+            if piece == w_pieces[-1]:
                 sigmoid(2)
-            interleave("S", half, H - SW, H)
+            interleave("S", piece, N_TILE - SCALAR_W, N_TILE)
             if q == 0:
                 turn_out(1, 1)
-            if q:
-                quantize(halves[q - 1])
+            else:
+                quantize(w_pieces[q - 1])
+
         load("v", 4, 1)
         load("g", 4, 2)
         load("e", 4, 2)
@@ -321,14 +316,18 @@ def tile_diffscm_pb_v_kernel(
         load_slices(10, 2)
         load_x(1)
         load_x(2)
+
         first_product(2)
-        quantize(halves[-1])
+        quantize(w_pieces[-1])
         products0(0)
         sigmoid(3)
         results0(0)
+
         last = SLICES - 1
-        ES = 192
-        early = [("d", 0, 0, H), ("x", 0, 0, H), ("d", 1, 0, H)]
+        d_left = [("d", g, 0, N_TILE) for g in range(GROUPS)]
+        x_left = [("x", g, 0, N_TILE) for g in range(GROUPS)]
+        x_right = [("x", g, N_TILE, N_TILE) for g in range(GROUPS)]
+        begins = {PACK - 1: d_left[0], 2 * PACK - 2: x_left[0], 2 * PACK: d_left[1]}
         for i in range(2, SLICES):
             if i > 2:
                 first_product(i)
@@ -341,40 +340,40 @@ def tile_diffscm_pb_v_kernel(
             if i > 2:
                 quantize_dz(i - 1)
             products0(i - 1)
-            if i == 11:
-                quadrant(0, 0, True, False)
             if i == last:
-                interleave("S", ("x", 2, 0, H), 0, H // 2)
-            if i >= 11:
+                quantize(x_left[0])
+                quadrant(0, 0, True, False)
+                interleave("S", x_left[2], 0, N_TILE // 2)
                 results0(i - 1)
             if i + 2 < SLICES:
                 sigmoid(i + 2)
-            e, half = divmod(i - 4, 2)
-            if i in (7, 10, 11):
-                quantize(early[(7, 10, 11).index(i)])
-            if e in range(len(early)):
-                interleave("S", early[e], half * ES // 2, (half + 1) * ES // 2)
-                if half:
-                    interleave("V", early[e], ES, H)
-            if i < 11:
+            if begins.get(i) == x_left[0]:
+                quantize(d_left[0])
+            if i == last:
+                quantize(d_left[1])
+            if i in begins:
+                interleave("S", begins[i], 0, SCALAR_EARLY // 2)
+            if i - 1 in begins:
+                interleave("S", begins[i - 1], SCALAR_EARLY // 2, SCALAR_EARLY)
+                interleave("V", begins[i - 1], SCALAR_EARLY, N_TILE)
+            if i < last:
                 results0(i - 1)
-        interleave("S", ("x", 2, 0, H), H // 2, H)
-        d1, d2 = ("x", 1, 0, H), ("d", 2, 0, H)
-        x_right = [("x", g, H, H) for g in range(GROUPS)]
-        interleave("V", d1)
+
+        interleave("S", x_left[2], N_TILE // 2, N_TILE)
+        interleave("V", x_left[1])
         quantize_dz(last)
         products0(last)
-        interleave("S", x_right[0], 0, H // 2)
+        interleave("S", x_right[0], 0, N_TILE // 2)
         results0(last)
-        interleave("S", x_right[0], H // 2, H)
-        interleave("V", d2)
-        quantize(d1)
+        interleave("S", x_right[0], N_TILE // 2, N_TILE)
+        interleave("V", d_left[2])
+        quantize(x_left[1])
         quadrant(0, 1, False, False)
         interleave("V", x_right[2])
-        quantize(d2)
-        quantize(("x", 2, 0, H))
+        quantize(d_left[2])
+        quantize(x_left[2])
         quadrant(0, 2, False, True)
-        for m in range(4):
+        for m in range(ROW_TILES // 2):
             result1("S", m, 0)
         quantize(x_right[2])
         quadrant(1, 2, True, False)
@@ -383,17 +382,18 @@ def tile_diffscm_pb_v_kernel(
         quadrant(1, 0, False, False)
         quantize(x_right[1])
         quadrant(1, 1, False, True)
-        for m in range(4):
+        for m in range(ROW_TILES // 2):
             result1("S", m, 1)
-        for m in range(4, 8):
-            interleave_rows(m, "V")
+
+        for m in range(ROW_TILES // 2, ROW_TILES):
+            interleave_rows(m)
             quantize_rows(m)
-            rows1(m)
-        for m in range(4, 8):
+            row_tile(m)
+        for m in range(ROW_TILES // 2, ROW_TILES):
             for n in range(2):
-                engine = "V" if m >= 6 and n else "S"
-                if m < 7:
+                engine = "V" if n and m >= ROW_TILES - 2 else "S"
+                if m < ROW_TILES - 1:
                     result1(engine, m, n)
                 else:
-                    result1(engine, m, n, 0, H // 2)
-                    result1(engine, m, n, H // 2, H)
+                    result1(engine, m, n, 0, N_TILE // 2)
+                    result1(engine, m, n, N_TILE // 2, N_TILE)

@@ -148,9 +148,11 @@ def tile_diffscm_pb_v_kernel(
 
         def first_product(i):
             prod[i] = work.tile([P, D], F32, tag="prod", bufs=2, name="prod")
-            nc.vector.scalar_tensor_tensor(
-                out=prod[i][:], in0=part("g", i), scalar=t_col[:, i : i + 1], in1=part("e", i), op0=MULT, op1=MULT
-            )
+            for c in map(columns, (None,) if i < 2 else (0, 1)):
+                nc.vector.scalar_tensor_tensor(
+                    out=prod[i][:, c], in0=part("g", i)[:, c], scalar=t_col[:, i : i + 1], in1=part("e", i)[:, c],
+                    op0=MULT, op1=MULT,
+                )
 
         sorted_in = lambda a: a.rearrange("p (w u e) -> p u w e", u=2, e=2)
         sorted_out = lambda a: a.rearrange("p (u w e) -> p u w e", u=2, e=2)
@@ -332,7 +334,8 @@ def tile_diffscm_pb_v_kernel(
             if i > 2:
                 first_product(i)
             make_dmu(i)
-            make_dv(i)
+            make_dv(i, 0)
+            make_dv(i, 1)
             turn(i, 0)
             turn(i, 1)
             turn_out(i, 0)

@@ -12,7 +12,7 @@ N_TILE = 512
 RUN = 8
 W_PASSES = 4
 ROW_TILES = D // P
-SCALAR_W = 256
+SCALAR_W = [256] * 6 + [320, 320]
 SCALAR_EARLY = 192
 FLOPS = 2 * B * D * D * 3
 BYTES = 2 * (3 * B * D + 2 * D * D + B) + 4 * B * D + 4 * (B * D + D * D)
@@ -121,13 +121,13 @@ def tile_diffscm_pb_v_kernel(
             c = slice(first, first + width)
             nc.vector.quantize_mx(out=codes[:, c].bitcast(fmt), scales=scales[:, c], in_=grp[piece][:])
 
-        def interleave_rows(m):
-            grp[m] = work.tile([P, GROUPS * P * PACK], BF16, tag="grpV", bufs=3, align_bytes=64, name="grpV")
+        def interleave_rows(engine, m, lo, hi):
+            if m not in grp:
+                grp[m] = work.tile([P, GROUPS * P * PACK], BF16, tag="grpV", bufs=3, align_bytes=64, name="grpV")
             src = e_all[:].rearrange("p (g t c i) -> p g c t i", g=GROUPS, t=PACK, i=RUN)
             first = m * P
             dst = grp[m][:].rearrange("p (g c i t) -> p g c t i", g=GROUPS, i=RUN, t=PACK)
-            for lo, hi in ((0, 2), (2, 3)):
-                copy("V", dst[:, lo:hi], src[:, lo:hi, first // RUN : (first + P) // RUN])
+            copy(engine, dst[:, lo:hi], src[:, lo:hi, first // RUN : (first + P) // RUN])
 
         def quantize_rows(m):
             codes = work.tile([P, GROUPS * P], U32, tag="rc", bufs=3, align_bytes=64, name="rc")
@@ -189,16 +189,21 @@ def tile_diffscm_pb_v_kernel(
                 in_=banks[i, head][:].rearrange("p k u c -> p k c u"),
             )
 
-        def quantize_dz(i):
-            codes = work.tile([P, W_PASSES * P], U32, tag="zc", bufs=4, align_bytes=64, name="zc")
-            scales = work.tile([P, W_PASSES * P], U8, tag="zs", bufs=4, align_bytes=64, name="zs")
-            nc.vector.quantize_mx(out=codes[:].bitcast(E5M2), scales=scales[:], in_=dzt[i][:])
-            dz[i] = (codes, scales)
+        def quantize_dz(i, head):
+            if not head:
+                codes = work.tile([P, W_PASSES * P], U32, tag="zc", bufs=4, align_bytes=64, name="zc")
+                scales = work.tile([P, W_PASSES * P], U8, tag="zs", bufs=4, align_bytes=64, name="zs")
+                dz[i] = (codes, scales)
+            c = slice(head * 2 * P, (head + 1) * 2 * P)
+            nc.vector.quantize_mx(
+                out=dz[i][0][:, c].bitcast(E5M2), scales=dz[i][1][:, c], in_=dzt[i][:, head * D : (head + 1) * D]
+            )
 
-        def product0(i, n):
-            acc[i, n] = take_bank([P, N_TILE])[1]
+        def product0(i, n, passes):
+            if passes[0] == 0:
+                held[i, n], acc[i, n] = take_bank([P, N_TILE], keep_out=True)
             codes, scales = dz[i]
-            for k in range(W_PASSES):
+            for k in passes:
                 rows = slice(k * P, (k + 1) * P)
                 cols = slice(k * D + n * N_TILE, k * D + (n + 1) * N_TILE)
                 nc.tensor.matmul_mx(
@@ -210,6 +215,7 @@ def tile_diffscm_pb_v_kernel(
 
         def result0(i, n):
             nc.scalar.copy(out=part("v", i)[:, columns(n)], in_=acc[i, n][:])
+            turnover.append(held[i, n])
 
         def store0(i):
             g, j = divmod(i, PACK)
@@ -222,7 +228,7 @@ def tile_diffscm_pb_v_kernel(
 
         def pass1(m, n, g, first, final):
             if first:
-                held[m, n], acc1[m, n] = take_bank([P, N_TILE], keep_out=True)
+                held["out_1", m, n], acc1[m, n] = take_bank([P, N_TILE], keep_out=True)
             codes, scales = dv_mx[g, m]
             cols = slice(g * D + n * N_TILE, g * D + (n + 1) * N_TILE)
             nc.tensor.matmul_mx(
@@ -238,12 +244,12 @@ def tile_diffscm_pb_v_kernel(
                 res[four] = big_tile([P, 4, N_TILE], F32)
             copy(engine, res[four][:, place, lo:hi], acc1[m, n][:, lo:hi])
             if lo == 0:
-                turnover.append(held[m, n])
+                turnover.append(held["out_1", m, n])
             nc.sync.dma_start(out=out1_v[m][:, n * N_TILE + lo : n * N_TILE + hi], in_=res[four][:, place, lo:hi])
 
-        def products0(i):
+        def products0(i, head):
             for n in range(2):
-                product0(i, n)
+                product0(i, n, (2 * head, 2 * head + 1))
 
         def results0(i):
             for n in range(2):
@@ -288,40 +294,51 @@ def tile_diffscm_pb_v_kernel(
         turn_out(0, 1)
         first_product(1)
         make_dmu(1)
+        quantize_dz(0, 0)
         for half in range(2):
             make_dv(1, half)
         turn(1, 0)
         turn(1, 1)
-        quantize_dz(0)
+        quantize_dz(0, 1)
         turn_out(1, 0)
 
         w_pieces = [("w", k, lo, N_TILE) for k in range(W_PASSES) for lo in (0, N_TILE)]
+
+        def head_passes(q):
+            quantize(w_pieces[q])
+            for i in range(2):
+                product0(i, q % 2, [q // 2])
+
         for q, piece in enumerate(w_pieces):
-            if piece == ("w", 1, 0, N_TILE):
-                quantize_dz(1)
-            interleave("V", piece, 0, N_TILE - SCALAR_W)
+            if q == 2:
+                quantize_dz(1, 1)
+            if q == len(w_pieces) - 1:
+                make_dmu(2)
+                turn(2, 0)
+            interleave("V", piece, 0, N_TILE - SCALAR_W[q])
             if piece == w_pieces[-1]:
                 sigmoid(2)
-            interleave("S", piece, N_TILE - SCALAR_W, N_TILE)
+            interleave("S", piece, N_TILE - SCALAR_W[q], N_TILE)
             if q == 0:
                 turn_out(1, 1)
+                quantize_dz(1, 0)
             else:
-                quantize(w_pieces[q - 1])
+                head_passes(q - 1)
 
         load("v", 4, 1)
         load("g", 4, 2)
         load("e", 4, 2)
         load("v", 5, 1)
         load_slices(6, 2)
-        load_slices(8, 2)
         load_x(0)
+        load_slices(8, 2)
         load_slices(10, 2)
         load_x(1)
         load_x(2)
 
         first_product(2)
-        quantize(w_pieces[-1])
-        products0(0)
+        turn_out(2, 0)
+        head_passes(len(w_pieces) - 1)
         sigmoid(3)
         results0(0)
 
@@ -329,67 +346,82 @@ def tile_diffscm_pb_v_kernel(
         d_left = [("d", g, 0, N_TILE) for g in range(GROUPS)]
         x_left = [("x", g, 0, N_TILE) for g in range(GROUPS)]
         x_right = [("x", g, N_TILE, N_TILE) for g in range(GROUPS)]
-        begins = {PACK - 1: d_left[0], 2 * PACK - 2: x_left[0], 2 * PACK: d_left[1]}
+        begins = {4: d_left[0], 6: x_left[0], 9: d_left[1]}
+        middle = (SCALAR_EARLY + N_TILE) // 2
         for i in range(2, SLICES):
             if i > 2:
                 first_product(i)
-            make_dmu(i)
+            if i < last:
+                make_dmu(i + 1)
+            if i in begins:
+                interleave("V", begins[i], SCALAR_EARLY, middle)
+            if i - 1 in begins:
+                interleave("V", begins[i - 1], middle, N_TILE)
             make_dv(i, 0)
             make_dv(i, 1)
-            turn(i, 0)
-            turn(i, 1)
-            turn_out(i, 0)
-            turn_out(i, 1)
             if i > 2:
-                quantize_dz(i - 1)
-            products0(i - 1)
+                quantize_dz(i - 1, 1)
+            quantize_dz(i, 0)
+            if i == 2 * PACK:
+                quantize(d_left[0])
+            if i < last:
+                turn(i + 1, 0)
+            turn(i, 1)
+            if i > 2:
+                products0(i - 1, 1)
+            products0(i, 0)
             if i == last:
-                quantize(x_left[0])
-                quadrant(0, 0, True, False)
                 interleave("S", x_left[2], 0, N_TILE // 2)
-                results0(i - 1)
+            turn_out(i, 1)
+            if i < last:
+                turn_out(i + 1, 0)
             if i + 2 < SLICES:
                 sigmoid(i + 2)
-            if begins.get(i) == x_left[0]:
-                quantize(d_left[0])
-            if i == last:
-                quantize(d_left[1])
             if i in begins:
                 interleave("S", begins[i], 0, SCALAR_EARLY // 2)
             if i - 1 in begins:
                 interleave("S", begins[i - 1], SCALAR_EARLY // 2, SCALAR_EARLY)
-                interleave("V", begins[i - 1], SCALAR_EARLY, N_TILE)
             if i < last:
                 results0(i - 1)
+        quantize(x_left[0])
+        quadrant(0, 0, True, False)
+        quantize(d_left[1])
 
-        interleave("S", x_left[2], N_TILE // 2, N_TILE)
         interleave("V", x_left[1])
-        quantize_dz(last)
-        products0(last)
-        interleave("S", x_right[0], 0, N_TILE // 2)
-        results0(last)
-        interleave("S", x_right[0], N_TILE // 2, N_TILE)
+        quantize_dz(last, 1)
+        products0(last, 1)
+        interleave("S", x_left[2], N_TILE // 2, N_TILE)
+        results0(last - 1)
+        interleave("S", x_right[0])
         interleave("V", d_left[2])
         quantize(x_left[1])
         quadrant(0, 1, False, False)
-        interleave("V", x_right[2])
+        results0(last)
+        interleave("V", x_right[2], 0, N_TILE // 2)
         quantize(d_left[2])
         quantize(x_left[2])
         quadrant(0, 2, False, True)
+        interleave("V", x_right[2], N_TILE // 2, N_TILE)
+        quantize(x_right[0])
+        quadrant(1, 0, True, False)
+        interleave("S", x_right[1], N_TILE // 2, N_TILE)
+        interleave("V", x_right[1], 0, N_TILE // 2)
+        quantize(x_right[2])
+        quadrant(1, 2, False, False)
         for m in range(ROW_TILES // 2):
             result1("S", m, 0)
-        quantize(x_right[2])
-        quadrant(1, 2, True, False)
-        interleave("V", x_right[1])
-        quantize(x_right[0])
-        quadrant(1, 0, False, False)
+        interleave_rows("V", 4, 0, 2)
         quantize(x_right[1])
         quadrant(1, 1, False, True)
+        interleave_rows("V", 4, 2, 3)
+        interleave_rows("S", 5, 2, 3)
         for m in range(ROW_TILES // 2):
             result1("S", m, 1)
-
         for m in range(ROW_TILES // 2, ROW_TILES):
-            interleave_rows(m)
+            if m > 4:
+                interleave_rows("V", m, 0, 2)
+            if m > 5:
+                interleave_rows("V", m, 2, 3)
             quantize_rows(m)
             row_tile(m)
         for m in range(ROW_TILES // 2, ROW_TILES):

@@ -12,8 +12,8 @@ N_TILE = 512
 RUN = 8
 W_PASSES = 4
 ROW_TILES = D // P
-SCALAR_W = [256] * 6 + [320, 320]
-SCALAR_EARLY = 192
+SCALAR_W = [256] * 8
+SCALAR_EARLY = 128
 FLOPS = 2 * B * D * D * 3
 BYTES = 2 * (3 * B * D + 2 * D * D + B) + 4 * B * D + 4 * (B * D + D * D)
 

@@ -9,6 +9,7 @@ PACK = 4
 GROUPS = B // (P * PACK)
 SLICES = GROUPS * PACK
 N_TILE = 512
+DMA_ALIGN = 256
 RUN = 8
 W_PASSES = 4
 ROW_TILES = D // P
@@ -57,17 +58,17 @@ def tile_diffscm_pb_v_kernel(
         planes = {"w": (w_codes, w_scales, E4M3), "x": (x_codes, x_scales, E4M3), "d": (d_codes, d_scales, E5M2)}
 
         def big_tile(shape, dtype):
-            return inp.tile(shape, dtype, tag="big", bufs=7, name="big")
+            return inp.tile(shape, dtype, tag="big", bufs=7, align_bytes=DMA_ALIGN, name="big")
 
         raw = {}
-        e_all = inp.tile([P, SLICES * D], BF16, name="e_all")
+        e_all = inp.tile([P, SLICES * D], BF16, align_bytes=DMA_ALIGN, name="e_all")
         for k in range(W_PASSES):
             raw["w", k] = big_tile([P, PACK * D], BF16)
         for g in range(GROUPS):
             raw["g", g] = big_tile([P, PACK * D], BF16)
             raw["e", g] = e_all[:, g * PACK * D : (g + 1) * PACK * D]
             raw["d", g] = raw["e", g]
-            raw["v", g] = inp.tile([P, PACK * D], F32, tag="v", bufs=GROUPS, name="raw_v")
+            raw["v", g] = inp.tile([P, PACK * D], F32, tag="v", bufs=GROUPS, align_bytes=DMA_ALIGN, name="raw_v")
 
         turnover = list(range(8))
 

@@ -13,7 +13,8 @@ DMA_ALIGN = 256
 RUN = 8
 W_PASSES = 4
 ROW_TILES = D // P
-SCALAR_W = [256] * 8
+MODE = "dussssss"
+VECTOR_W = [256,256]+[224]*6
 SCALAR_EARLY = 128
 FLOPS = 2 * B * D * D * 3
 BYTES = 2 * (3 * B * D + 2 * D * D + B) + 4 * B * D + 4 * (B * D + D * D)
@@ -48,6 +49,7 @@ def tile_diffscm_pb_v_kernel(
 
         t_col = const.tile([P, SLICES], BF16, name="t_col")
         ident = const.tile([P, P], F32, name="ident")
+        ident_bf = const.tile([P, P], BF16, name="ident_bf")
 
         w_codes = keep.tile([P, W_PASSES * D], U32, align_bytes=64, name="w_codes")
         w_scales = keep.tile([P, W_PASSES * D], U8, align_bytes=64, name="w_scales")
@@ -72,11 +74,11 @@ def tile_diffscm_pb_v_kernel(
 
         turnover = list(range(8))
 
-        def take_bank(shape, keep_out=False):
+        def take_bank(shape, keep_out=False, dtype=F32):
             b = turnover.pop(0)
             if not keep_out:
                 turnover.append(b)
-            return b, psum.tile(shape, F32, tag="bank%d" % b, name="bank")
+            return b, psum.tile(shape, dtype, tag="bank%d" % b, name="bank")
 
         def part(kind, i, n=1):
             g, j = divmod(i, PACK)
@@ -114,6 +116,26 @@ def tile_diffscm_pb_v_kernel(
             dst = tile[:].rearrange("p (c i t) -> p c t i", i=RUN, t=PACK)
             src = raw[kind, k][:].rearrange("p (t c i) -> p c t i", t=PACK, i=RUN)
             copy(engine, dst[:, a // RUN : b // RUN], src[:, (lo + a) // RUN : (lo + b) // RUN])
+
+        def carry(piece, stepped):
+            kind, k, lo, width = piece
+            blocks = 1 if stepped else 2
+            banks[piece] = take_bank([P, blocks, PACK * P], dtype=BF16)[1]
+            rows = raw[kind, k][:].rearrange("p (t c) -> p t c", t=PACK)
+            for b in range(blocks):
+                first = lo + width - (blocks - b) * P
+                out = banks[piece][:, b].rearrange("p (c t) -> p t c" if stepped else "p (t c) -> p t c", t=PACK)
+                nc.tensor.matmul(out, lhsT=ident_bf[:], rhs=rows[:, :, first : first + P], start=True, stop=True)
+
+        def carry_out(piece, stepped):
+            width = piece[3]
+            if stepped:
+                nc.scalar.copy(out=grp[piece][:, (width - P) * PACK :], in_=banks[piece][:, 0])
+            else:
+                nc.scalar.copy(
+                    out=grp[piece][:, (width - 2 * P) * PACK :].rearrange("p (b c t) -> p b c t", b=2, t=PACK),
+                    in_=banks[piece][:].rearrange("p b (t c) -> p b c t", t=PACK),
+                )
 
         def quantize(piece):
             kind, k, lo, width = piece
@@ -281,6 +303,7 @@ def tile_diffscm_pb_v_kernel(
         load_slices(2, 1)
         load_slices(3, 1)
         make_identity(nc, ident[:])
+        make_identity(nc, ident_bf[:])
 
         make_dmu(0)
         first_product(0)
@@ -306,7 +329,6 @@ def tile_diffscm_pb_v_kernel(
         w_pieces = [("w", k, lo, N_TILE) for k in range(W_PASSES) for lo in (0, N_TILE)]
 
         def head_passes(q):
-            quantize(w_pieces[q])
             for i in range(2):
                 product0(i, q % 2, [q // 2])
 
@@ -316,15 +338,22 @@ def tile_diffscm_pb_v_kernel(
             if q == len(w_pieces) - 1:
                 make_dmu(2)
                 turn(2, 0)
-            interleave("V", piece, 0, N_TILE - SCALAR_W[q])
+            if MODE[q] != "d":
+                carry(piece, MODE[q] == "s")
+            interleave("V", piece, 0, VECTOR_W[q])
             if piece == w_pieces[-1]:
                 sigmoid(2)
-            interleave("S", piece, N_TILE - SCALAR_W[q], N_TILE)
+            if MODE[q] != "u":
+                interleave("S", piece, VECTOR_W[q], N_TILE - P * (MODE[q] == "s"))
             if q == 0:
                 turn_out(1, 1)
                 quantize_dz(1, 0)
-            else:
-                head_passes(q - 1)
+            if MODE[q] != "d":
+                carry_out(piece, MODE[q] == "s")
+            if q > 0:
+                quantize(w_pieces[q - 1])
+            if q > 1:
+                head_passes(q - 2)
 
         load("v", 4, 1)
         load("g", 4, 2)
@@ -339,6 +368,8 @@ def tile_diffscm_pb_v_kernel(
 
         first_product(2)
         turn_out(2, 0)
+        head_passes(len(w_pieces) - 2)
+        quantize(w_pieces[-1])
         head_passes(len(w_pieces) - 1)
         sigmoid(3)
         results0(0)
@@ -405,8 +436,8 @@ def tile_diffscm_pb_v_kernel(
         interleave("V", x_right[2], N_TILE // 2, N_TILE)
         quantize(x_right[0])
         quadrant(1, 0, True, False)
-        interleave("S", x_right[1], N_TILE // 2, N_TILE)
-        interleave("V", x_right[1], 0, N_TILE // 2)
+        interleave("S", x_right[1], 3 * N_TILE // 4, N_TILE)
+        interleave("V", x_right[1], 0, 3 * N_TILE // 4)
         quantize(x_right[2])
         quadrant(1, 2, False, False)
         for m in range(ROW_TILES // 2):

@@ -117,20 +117,19 @@ def tile_diffscm_pb_v_kernel(
             src = raw[kind, k][:].rearrange("p (t c i) -> p c t i", t=PACK, i=RUN)
             copy(engine, dst[:, a // RUN : b // RUN], src[:, (lo + a) // RUN : (lo + b) // RUN])
 
-        def carry(piece, stepped):
+        def carry(piece, stepped, end=N_TILE):
             kind, k, lo, width = piece
             blocks = 1 if stepped else 2
             banks[piece] = take_bank([P, blocks, PACK * P], dtype=BF16)[1]
             rows = raw[kind, k][:].rearrange("p (t c) -> p t c", t=PACK)
             for b in range(blocks):
-                first = lo + width - (blocks - b) * P
+                first = lo + end - (blocks - b) * P
                 out = banks[piece][:, b].rearrange("p (c t) -> p t c" if stepped else "p (t c) -> p t c", t=PACK)
                 nc.tensor.matmul(out, lhsT=ident_bf[:], rhs=rows[:, :, first : first + P], start=True, stop=True)
 
-        def carry_out(piece, stepped):
-            width = piece[3]
+        def carry_out(piece, stepped, width=N_TILE):
             if stepped:
-                nc.scalar.copy(out=grp[piece][:, (width - P) * PACK :], in_=banks[piece][:, 0])
+                nc.scalar.copy(out=grp[piece][:, (width - P) * PACK : width * PACK], in_=banks[piece][:, 0])
             else:
                 nc.scalar.copy(
                     out=grp[piece][:, (width - 2 * P) * PACK :].rearrange("p (b c t) -> p b c t", b=2, t=PACK),
@@ -249,26 +248,31 @@ def tile_diffscm_pb_v_kernel(
                 rows = slice(g * N_TILE + m * P, g * N_TILE + (m + 1) * P)
                 dv_mx[g, m] = (d_codes[:, rows], d_scales[:, rows])
 
-        def pass1(m, n, g, first, final):
+        def pass1(m, n, g, first, final, lo=0, hi=N_TILE):
             if first:
-                held["out_1", m, n], acc1[m, n] = take_bank([P, N_TILE], keep_out=True)
+                held["out_1", m, n, lo], acc1[m, n, lo] = take_bank([P, hi - lo], keep_out=True)
             codes, scales = dv_mx[g, m]
-            cols = slice(g * D + n * N_TILE, g * D + (n + 1) * N_TILE)
+            cols = slice(g * D + n * N_TILE + lo, g * D + n * N_TILE + hi)
             nc.tensor.matmul_mx(
-                out=acc1[m, n][:],
+                out=acc1[m, n, lo][:],
                 lhsT=codes.bitcast(E5M2), lhsT_scale=scales,
                 rhs=x_codes[:, cols].bitcast(E4M3), rhs_scale=x_scales[:, cols],
                 start=first, stop=final,
             )
 
-        def result1(engine, m, n, lo=0, hi=N_TILE):
+        def result_of(m, n):
             four, place = (n, m) if m < ROW_TILES // 2 else (m // 2, m % 2 * 2 + n)
             if four not in res:
-                res[four] = big_tile([P, 4, N_TILE], F32)
-            copy(engine, res[four][:, place, lo:hi], acc1[m, n][:, lo:hi])
-            if lo == 0:
-                turnover.append(held["out_1", m, n])
-            nc.sync.dma_start(out=out1_v[m][:, n * N_TILE + lo : n * N_TILE + hi], in_=res[four][:, place, lo:hi])
+                res[four] = big_tile([P, 4 * N_TILE], F32)
+            return res[four][:, place * N_TILE :]
+
+        def result1(engine, m, n, lo=0, hi=N_TILE, bank=0):
+            copy(engine, result_of(m, n)[:, lo:hi], acc1[m, n, bank][:, lo - bank : hi - bank])
+            if lo == bank:
+                turnover.append(held["out_1", m, n, bank])
+
+        def store1(queue, m, n, lo=0, hi=N_TILE):
+            queue.dma_start(out=out1_v[m][:, n * N_TILE + lo : n * N_TILE + hi], in_=result_of(m, n)[:, lo:hi])
 
         def products0(i, head):
             for n in range(2):
@@ -284,9 +288,11 @@ def tile_diffscm_pb_v_kernel(
                 pass1(m, n, g, first, final)
 
         def row_tile(m):
-            for n in range(2):
+            half = N_TILE // 2
+            ranges = [(0, 0, N_TILE)] + ([(1, 0, N_TILE)] if m < ROW_TILES - 1 else [(1, 0, half), (1, half, N_TILE)])
+            for n, lo, hi in ranges:
                 for g in range(GROUPS):
-                    pass1(m, n, g, g == 0, g == GROUPS - 1)
+                    pass1(m, n, g, g == 0, g == GROUPS - 1, lo, hi)
 
         nc.scalar.dma_start(
             out=t_col[:].rearrange("p (g j) -> p g j", j=PACK),
@@ -335,13 +341,12 @@ def tile_diffscm_pb_v_kernel(
         for q, piece in enumerate(w_pieces):
             if q == 2:
                 quantize_dz(1, 1)
-            if q == len(w_pieces) - 1:
-                make_dmu(2)
-                turn(2, 0)
             if MODE[q] != "d":
                 carry(piece, MODE[q] == "s")
             interleave("V", piece, 0, VECTOR_W[q])
             if piece == w_pieces[-1]:
+                make_dmu(2)
+                turn(2, 0)
                 sigmoid(2)
             if MODE[q] != "u":
                 interleave("S", piece, VECTOR_W[q], N_TILE - P * (MODE[q] == "s"))
@@ -442,25 +447,40 @@ def tile_diffscm_pb_v_kernel(
         quadrant(1, 2, False, False)
         for m in range(ROW_TILES // 2):
             result1("S", m, 0)
-        interleave_rows("V", 4, 0, 2)
+            store1(nc.sync, m, 0)
+        interleave_rows("V", 4, 2, 3)
         quantize(x_right[1])
         quadrant(1, 1, False, True)
-        interleave_rows("V", 4, 2, 3)
-        interleave_rows("S", 5, 2, 3)
+        interleave_rows("V", 4, 0, 2)
         for m in range(ROW_TILES // 2):
             result1("S", m, 1)
+            store1(nc.sync, m, 1)
         for m in range(ROW_TILES // 2, ROW_TILES):
             if m > 4:
                 interleave_rows("V", m, 0, 2)
-            if m > 5:
+            if m > 4:
                 interleave_rows("V", m, 2, 3)
             quantize_rows(m)
+            if m == 6:
+                result1("S", 4, 0)
+                result1("S", 4, 1)
+                store1(nc.sync, 4, 0, 0, D)
+            if m == 7:
+                result1("S", 5, 0)
+                result1("S", 5, 1)
+                store1(nc.scalar, 5, 0)
+                store1(nc.sync, 5, 1)
             row_tile(m)
-        for m in range(ROW_TILES // 2, ROW_TILES):
-            for n in range(2):
-                engine = "V" if n and m >= ROW_TILES - 2 else "S"
-                if m < ROW_TILES - 1:
-                    result1(engine, m, n)
-                else:
-                    result1(engine, m, n, 0, N_TILE // 2)
-                    result1(engine, m, n, N_TILE // 2, N_TILE)
+        half, quarter = N_TILE // 2, N_TILE // 4
+        result1("S", 6, 0)
+        store1(nc.scalar, 6, 0)
+        result1("V", 6, 1)
+        store1(nc.sync, 6, 1)
+        for lo in (0, half):
+            result1("S", 7, 0, lo, lo + half)
+            store1(nc.scalar, 7, 0, lo, lo + half)
+        result1("V", 7, 1, 0, half)
+        store1(nc.sync, 7, 1, 0, half)
+        for lo in (half, half + quarter):
+            result1("V", 7, 1, lo, lo + quarter, half)
+            store1(nc.sync, 7, 1, lo, lo + quarter)

@@ -288,11 +288,9 @@ def tile_diffscm_pb_v_kernel(
                 pass1(m, n, g, first, final)
 
         def row_tile(m):
-            half = N_TILE // 2
-            ranges = [(0, 0, N_TILE)] + ([(1, 0, N_TILE)] if m < ROW_TILES - 1 else [(1, 0, half), (1, half, N_TILE)])
-            for n, lo, hi in ranges:
+            for n in range(2):
                 for g in range(GROUPS):
-                    pass1(m, n, g, g == 0, g == GROUPS - 1, lo, hi)
+                    pass1(m, n, g, g == 0, g == GROUPS - 1)
 
         nc.scalar.dma_start(
             out=t_col[:].rearrange("p (g j) -> p g j", j=PACK),
@@ -452,35 +450,29 @@ def tile_diffscm_pb_v_kernel(
         quantize(x_right[1])
         quadrant(1, 1, False, True)
         interleave_rows("V", 4, 0, 2)
+        interleave_rows("S", 5, 2, 3)
         for m in range(ROW_TILES // 2):
             result1("S", m, 1)
             store1(nc.sync, m, 1)
         for m in range(ROW_TILES // 2, ROW_TILES):
             if m > 4:
                 interleave_rows("V", m, 0, 2)
-            if m > 4:
+            if m > 5:
                 interleave_rows("V", m, 2, 3)
             quantize_rows(m)
-            if m == 6:
-                result1("S", 4, 0)
-                result1("S", 4, 1)
-                store1(nc.sync, 4, 0, 0, D)
-            if m == 7:
-                result1("S", 5, 0)
-                result1("S", 5, 1)
-                store1(nc.scalar, 5, 0)
-                store1(nc.sync, 5, 1)
             row_tile(m)
-        half, quarter = N_TILE // 2, N_TILE // 4
+        result1("S", 4, 0)
+        result1("S", 4, 1)
+        store1(nc.sync, 4, 0, 0, D)
+        result1("S", 5, 0)
+        result1("S", 5, 1)
+        store1(nc.sync, 5, 0, 0, D)
         result1("S", 6, 0)
-        store1(nc.scalar, 6, 0)
+        store1(nc.sync, 6, 0)
         result1("V", 6, 1)
         store1(nc.sync, 6, 1)
-        for lo in (0, half):
-            result1("S", 7, 0, lo, lo + half)
-            store1(nc.scalar, 7, 0, lo, lo + half)
-        result1("V", 7, 1, 0, half)
-        store1(nc.sync, 7, 1, 0, half)
-        for lo in (half, half + quarter):
-            result1("V", 7, 1, lo, lo + quarter, half)
-            store1(nc.sync, 7, 1, lo, lo + quarter)
+        result1("S", 7, 0)
+        store1(nc.sync, 7, 0)
+        for lo in (0, N_TILE // 2):
+            result1("V", 7, 1, lo, lo + N_TILE // 2)
+            store1(nc.sync, 7, 1, lo, lo + N_TILE // 2)

@@ -13,8 +13,8 @@ DMA_ALIGN = 256
 RUN = 8
 W_PASSES = 4
 ROW_TILES = D // P
-MODE = "dussssss"
-VECTOR_W = [256,256]+[224]*6
+CARRIED = [0, 256] + [128] * 5 + [256]
+VECTOR_W = [256, 256] + [208] * 5 + [96]
 SCALAR_EARLY = 128
 FLOPS = 2 * B * D * D * 3
 BYTES = 2 * (3 * B * D + 2 * D * D + B) + 4 * B * D + 4 * (B * D + D * D)
@@ -117,23 +117,25 @@ def tile_diffscm_pb_v_kernel(
             src = raw[kind, k][:].rearrange("p (t c i) -> p c t i", t=PACK, i=RUN)
             copy(engine, dst[:, a // RUN : b // RUN], src[:, (lo + a) // RUN : (lo + b) // RUN])
 
-        def carry(piece, stepped, end=N_TILE):
+        def carry(piece, a, b, stepped=True):
             kind, k, lo, width = piece
-            blocks = 1 if stepped else 2
-            banks[piece] = take_bank([P, blocks, PACK * P], dtype=BF16)[1]
+            blocks = -(-(b - a) // P)
+            w = (b - a) // blocks
+            banks[piece] = take_bank([P, blocks, PACK * w], dtype=BF16)[1]
             rows = raw[kind, k][:].rearrange("p (t c) -> p t c", t=PACK)
-            for b in range(blocks):
-                first = lo + end - (blocks - b) * P
-                out = banks[piece][:, b].rearrange("p (c t) -> p t c" if stepped else "p (t c) -> p t c", t=PACK)
-                nc.tensor.matmul(out, lhsT=ident_bf[:], rhs=rows[:, :, first : first + P], start=True, stop=True)
+            for j in range(blocks):
+                out = banks[piece][:, j].rearrange("p (c t) -> p t c" if stepped else "p (t c) -> p t c", t=PACK)
+                first = lo + a + j * w
+                nc.tensor.matmul(out, lhsT=ident_bf[:], rhs=rows[:, :, first : first + w], start=True, stop=True)
 
-        def carry_out(piece, stepped, width=N_TILE):
+        def carry_out(piece, a, b, stepped=True):
+            dst = grp[piece][:, a * PACK : b * PACK]
             if stepped:
-                nc.scalar.copy(out=grp[piece][:, (width - P) * PACK : width * PACK], in_=banks[piece][:, 0])
+                nc.scalar.copy(out=dst, in_=banks[piece][:].rearrange("p j x -> p (j x)"))
             else:
                 nc.scalar.copy(
-                    out=grp[piece][:, (width - 2 * P) * PACK :].rearrange("p (b c t) -> p b c t", b=2, t=PACK),
-                    in_=banks[piece][:].rearrange("p b (t c) -> p b c t", t=PACK),
+                    out=dst.rearrange("p (j c t) -> p j c t", c=P, t=PACK),
+                    in_=banks[piece][:].rearrange("p j (t c) -> p j c t", t=PACK),
                 )
 
         def quantize(piece):
@@ -339,20 +341,19 @@ def tile_diffscm_pb_v_kernel(
         for q, piece in enumerate(w_pieces):
             if q == 2:
                 quantize_dz(1, 1)
-            if MODE[q] != "d":
-                carry(piece, MODE[q] == "s")
+            if CARRIED[q]:
+                carry(piece, N_TILE - CARRIED[q], N_TILE, q > 1)
             interleave("V", piece, 0, VECTOR_W[q])
             if piece == w_pieces[-1]:
                 make_dmu(2)
                 turn(2, 0)
-                sigmoid(2)
-            if MODE[q] != "u":
-                interleave("S", piece, VECTOR_W[q], N_TILE - P * (MODE[q] == "s"))
+            if VECTOR_W[q] + CARRIED[q] < N_TILE:
+                interleave("S", piece, VECTOR_W[q], N_TILE - CARRIED[q])
             if q == 0:
                 turn_out(1, 1)
                 quantize_dz(1, 0)
-            if MODE[q] != "d":
-                carry_out(piece, MODE[q] == "s")
+            if CARRIED[q]:
+                carry_out(piece, N_TILE - CARRIED[q], N_TILE, q > 1)
             if q > 0:
                 quantize(w_pieces[q - 1])
             if q > 1:
@@ -369,6 +370,7 @@ def tile_diffscm_pb_v_kernel(
         load_x(1)
         load_x(2)
 
+        sigmoid(2)
         first_product(2)
         turn_out(2, 0)
         head_passes(len(w_pieces) - 2)

@@ -15,7 +15,7 @@ W_PASSES = 4
 ROW_TILES = D // P
 CARRIED = [0, 256] + [128] * 5 + [256]
 VECTOR_W = [256, 256] + [208] * 5 + [96]
-SCALAR_EARLY = 128
+SCALAR_EARLY = 96
 FLOPS = 2 * B * D * D * 3
 BYTES = 2 * (3 * B * D + 2 * D * D + B) + 4 * B * D + 4 * (B * D + D * D)
 
@@ -129,6 +129,8 @@ def tile_diffscm_pb_v_kernel(
                 nc.tensor.matmul(out, lhsT=ident_bf[:], rhs=rows[:, :, first : first + w], start=True, stop=True)
 
         def carry_out(piece, a, b, stepped=True):
+            if piece not in grp:
+                grp[piece] = work.tile([P, piece[3] * PACK], BF16, tag="grpS", bufs=3, align_bytes=64, name="grpS")
             dst = grp[piece][:, a * PACK : b * PACK]
             if stepped:
                 nc.scalar.copy(out=dst, in_=banks[piece][:].rearrange("p j x -> p (j x)"))
@@ -384,7 +386,8 @@ def tile_diffscm_pb_v_kernel(
         x_left = [("x", g, 0, N_TILE) for g in range(GROUPS)]
         x_right = [("x", g, N_TILE, N_TILE) for g in range(GROUPS)]
         begins = {4: d_left[0], 6: x_left[0], 9: d_left[1]}
-        middle = (SCALAR_EARLY + N_TILE) // 2
+        end = N_TILE - 2 * 32
+        middle = (SCALAR_EARLY + end) // 2
         for i in range(2, SLICES):
             if i > 2:
                 first_product(i)
@@ -393,7 +396,7 @@ def tile_diffscm_pb_v_kernel(
             if i in begins:
                 interleave("V", begins[i], SCALAR_EARLY, middle)
             if i - 1 in begins:
-                interleave("V", begins[i - 1], middle, N_TILE)
+                interleave("V", begins[i - 1], middle, end)
             make_dv(i, 0)
             make_dv(i, 1)
             if i > 2:
@@ -407,6 +410,9 @@ def tile_diffscm_pb_v_kernel(
             if i > 2:
                 products0(i - 1, 1)
             products0(i, 0)
+            for step in range(2):
+                if i - step in begins:
+                    carry(begins[i - step], end + step * 32, end + (step + 1) * 32)
             if i == last:
                 interleave("S", x_left[2], 0, N_TILE // 2)
             turn_out(i, 1)
@@ -420,6 +426,9 @@ def tile_diffscm_pb_v_kernel(
                 interleave("S", begins[i - 1], SCALAR_EARLY // 2, SCALAR_EARLY)
             if i < last:
                 results0(i - 1)
+            for step in range(2):
+                if i - step in begins:
+                    carry_out(begins[i - step], end + step * 32, end + (step + 1) * 32)
         quantize(x_left[0])
         quadrant(0, 0, True, False)
         quantize(d_left[1])
@@ -433,7 +442,9 @@ def tile_diffscm_pb_v_kernel(
         interleave("V", d_left[2])
         quantize(x_left[1])
         quadrant(0, 1, False, False)
+        carry(x_right[1], N_TILE - P, N_TILE)
         results0(last)
+        carry_out(x_right[1], N_TILE - P, N_TILE)
         interleave("V", x_right[2], 0, N_TILE // 2)
         quantize(d_left[2])
         quantize(x_left[2])
@@ -441,17 +452,18 @@ def tile_diffscm_pb_v_kernel(
         interleave("V", x_right[2], N_TILE // 2, N_TILE)
         quantize(x_right[0])
         quadrant(1, 0, True, False)
-        interleave("S", x_right[1], 3 * N_TILE // 4, N_TILE)
-        interleave("V", x_right[1], 0, 3 * N_TILE // 4)
+        interleave("S", x_right[1], 320, N_TILE - P)
+        interleave("V", x_right[1], 0, 320)
         quantize(x_right[2])
         quadrant(1, 2, False, False)
         for m in range(ROW_TILES // 2):
             result1("S", m, 0)
             store1(nc.sync, m, 0)
-        interleave_rows("V", 4, 2, 3)
+        interleave_rows("V", 4, 0, 1)
         quantize(x_right[1])
         quadrant(1, 1, False, True)
-        interleave_rows("V", 4, 0, 2)
+        interleave_rows("V", 4, 1, 2)
+        interleave_rows("V", 4, 2, 3)
         interleave_rows("S", 5, 2, 3)
         for m in range(ROW_TILES // 2):
             result1("S", m, 1)

@@ -51,12 +51,15 @@ def tile_diffscm_pb_v_kernel(
         ident = const.tile([P, P], F32, name="ident")
         ident_bf = const.tile([P, P], BF16, name="ident_bf")
 
-        w_codes = keep.tile([P, W_PASSES * D], U32, align_bytes=64, name="w_codes")
-        w_scales = keep.tile([P, W_PASSES * D], U8, align_bytes=64, name="w_scales")
-        x_codes = keep.tile([P, GROUPS * D], U32, align_bytes=64, name="x_codes")
-        x_scales = keep.tile([P, GROUPS * D], U8, align_bytes=64, name="x_scales")
-        d_codes = keep.tile([P, GROUPS * N_TILE], U32, align_bytes=64, name="d_codes")
-        d_scales = keep.tile([P, GROUPS * N_TILE], U8, align_bytes=64, name="d_scales")
+        def mx_operand(pool, width, moving, name, bufs=1):
+            skip_words, skip_bytes = (0, 128) if moving else (16, 192)
+            codes = pool.tile([P, skip_words + width], U32, align_bytes=256, name=name + "_codes", bufs=bufs)
+            scales = pool.tile([P, skip_bytes + width], U8, align_bytes=256, name=name + "_scales", bufs=bufs)
+            return codes[:, skip_words:], scales[:, skip_bytes:]
+
+        w_codes, w_scales = mx_operand(keep, W_PASSES * D, True, name="w")
+        x_codes, x_scales = mx_operand(keep, GROUPS * D, True, name="x")
+        d_codes, d_scales = mx_operand(keep, GROUPS * N_TILE, False, name="d")
         planes = {"w": (w_codes, w_scales, E4M3), "x": (x_codes, x_scales, E4M3), "d": (d_codes, d_scales, E5M2)}
 
         def big_tile(shape, dtype):
@@ -156,8 +159,7 @@ def tile_diffscm_pb_v_kernel(
             copy(engine, dst[:, lo:hi], src[:, lo:hi, first // RUN : (first + P) // RUN])
 
         def quantize_rows(m):
-            codes = work.tile([P, GROUPS * P], U32, tag="rc", bufs=3, align_bytes=64, name="rc")
-            scales = work.tile([P, GROUPS * P], U8, tag="rs", bufs=3, align_bytes=64, name="rs")
+            codes, scales = mx_operand(work, GROUPS * P, False, name="r", bufs=3)
             for lo, hi in ((0, 2 * P), (2 * P, 3 * P)):
                 nc.vector.quantize_mx(
                     out=codes[:, lo:hi].bitcast(E5M2), scales=scales[:, lo:hi], in_=grp[m][:, lo * PACK : hi * PACK]
@@ -217,9 +219,7 @@ def tile_diffscm_pb_v_kernel(
 
         def quantize_dz(i, head):
             if not head:
-                codes = work.tile([P, W_PASSES * P], U32, tag="zc", bufs=4, align_bytes=64, name="zc")
-                scales = work.tile([P, W_PASSES * P], U8, tag="zs", bufs=4, align_bytes=64, name="zs")
-                dz[i] = (codes, scales)
+                dz[i] = mx_operand(work, W_PASSES * P, False, name="z", bufs=3)
             c = slice(head * 2 * P, (head + 1) * 2 * P)
             nc.vector.quantize_mx(
                 out=dz[i][0][:, c].bitcast(E5M2), scales=dz[i][1][:, c], in_=dzt[i][:, head * D : (head + 1) * D]

@@ -9,13 +9,16 @@ PACK = 4
 GROUPS = B // (P * PACK)
 SLICES = GROUPS * PACK
 N_TILE = 512
+HALF = N_TILE // 2
 DMA_ALIGN = 256
 RUN = 8
 W_PASSES = 4
 ROW_TILES = D // P
-CARRIED = [0, 256] + [128] * 5 + [256]
-VECTOR_W = [256, 256] + [208] * 5 + [96]
+CARRIED_W = [0, HALF] + [P] * 5 + [HALF]
+VECTOR_W = [HALF, HALF] + [208] * 5 + [P]
 SCALAR_EARLY = 96
+CARRIED_EARLY = 32
+SCALAR_LAST = 64
 FLOPS = 2 * B * D * D * 3
 BYTES = 2 * (3 * B * D + 2 * D * D + B) + 4 * B * D + 4 * (B * D + D * D)
 
@@ -108,20 +111,22 @@ def tile_diffscm_pb_v_kernel(
             else:
                 nc.scalar.copy(out=out, in_=in_)
 
-        grp, prod, dmu, banks, dzt, dz, acc, acc1, dv_mx, held, res = {}, {}, {}, {}, {}, {}, {}, {}, {}, {}, {}
+        grp, prod, dmu, banks, dzt, dz, acc0, acc1, dv_mx, held, res = {}, {}, {}, {}, {}, {}, {}, {}, {}, {}, {}
+
+        def staging(key, width, engine):
+            if key not in grp:
+                tag = "grp" + engine
+                grp[key] = work.tile([P, width * PACK], BF16, tag=tag, bufs=3, align_bytes=64, name=tag)
+            return grp[key]
 
         def interleave(engine, piece, a=0, b=N_TILE):
-            kind, k, lo, width = piece
-            if piece not in grp:
-                tag = "grp" + engine
-                grp[piece] = work.tile([P, width * PACK], BF16, tag=tag, bufs=3, align_bytes=64, name=tag)
-            tile = grp[piece]
-            dst = tile[:].rearrange("p (c i t) -> p c t i", i=RUN, t=PACK)
+            kind, k, lo = piece
+            dst = staging(piece, N_TILE, engine)[:].rearrange("p (c i t) -> p c t i", i=RUN, t=PACK)
             src = raw[kind, k][:].rearrange("p (t c i) -> p c t i", t=PACK, i=RUN)
             copy(engine, dst[:, a // RUN : b // RUN], src[:, (lo + a) // RUN : (lo + b) // RUN])
 
         def carry(piece, a, b, stepped=True):
-            kind, k, lo, width = piece
+            kind, k, lo = piece
             blocks = -(-(b - a) // P)
             w = (b - a) // blocks
             banks[piece] = take_bank([P, blocks, PACK * w], dtype=BF16)[1]
@@ -132,9 +137,7 @@ def tile_diffscm_pb_v_kernel(
                 nc.tensor.matmul(out, lhsT=ident_bf[:], rhs=rows[:, :, first : first + w], start=True, stop=True)
 
         def carry_out(piece, a, b, stepped=True):
-            if piece not in grp:
-                grp[piece] = work.tile([P, piece[3] * PACK], BF16, tag="grpS", bufs=3, align_bytes=64, name="grpS")
-            dst = grp[piece][:, a * PACK : b * PACK]
+            dst = staging(piece, N_TILE, "S")[:, a * PACK : b * PACK]
             if stepped:
                 nc.scalar.copy(out=dst, in_=banks[piece][:].rearrange("p j x -> p (j x)"))
             else:
@@ -144,18 +147,16 @@ def tile_diffscm_pb_v_kernel(
                 )
 
         def quantize(piece):
-            kind, k, lo, width = piece
+            kind, k, lo = piece
             codes, scales, fmt = planes[kind]
             first = k * (N_TILE if kind == "d" else D) + lo
-            c = slice(first, first + width)
+            c = slice(first, first + N_TILE)
             nc.vector.quantize_mx(out=codes[:, c].bitcast(fmt), scales=scales[:, c], in_=grp[piece][:])
 
         def interleave_rows(engine, m, lo, hi):
-            if m not in grp:
-                grp[m] = work.tile([P, GROUPS * P * PACK], BF16, tag="grpV", bufs=3, align_bytes=64, name="grpV")
             src = e_all[:].rearrange("p (g t c i) -> p g c t i", g=GROUPS, t=PACK, i=RUN)
             first = m * P
-            dst = grp[m][:].rearrange("p (g c i t) -> p g c t i", g=GROUPS, i=RUN, t=PACK)
+            dst = staging(m, GROUPS * P, "V")[:].rearrange("p (g c i t) -> p g c t i", g=GROUPS, i=RUN, t=PACK)
             copy(engine, dst[:, lo:hi], src[:, lo:hi, first // RUN : (first + P) // RUN])
 
         def quantize_rows(m):
@@ -191,7 +192,7 @@ def tile_diffscm_pb_v_kernel(
                 out=sorted_out(dmu[i][:]), in0=sorted_in(part("g", i)), scalar1=t_col[:, i : i + 1], scalar2=None, op0=MULT
             )
 
-        def make_dv(i, half=None):
+        def make_dv(i, half):
             nc.vector.tensor_tensor(
                 out=part("e", i)[:, columns(half)], in0=prod[i][:, columns(half)], in1=part("v", i)[:, columns(half)], op=MULT
             )
@@ -227,20 +228,20 @@ def tile_diffscm_pb_v_kernel(
 
         def product0(i, n, passes):
             if passes[0] == 0:
-                held[i, n], acc[i, n] = take_bank([P, N_TILE], keep_out=True)
+                held[i, n], acc0[i, n] = take_bank([P, N_TILE], keep_out=True)
             codes, scales = dz[i]
             for k in passes:
                 rows = slice(k * P, (k + 1) * P)
                 cols = slice(k * D + n * N_TILE, k * D + (n + 1) * N_TILE)
                 nc.tensor.matmul_mx(
-                    out=acc[i, n][:],
+                    out=acc0[i, n][:],
                     lhsT=codes[:, rows].bitcast(E5M2), lhsT_scale=scales[:, rows],
                     rhs=w_codes[:, cols].bitcast(E4M3), rhs_scale=w_scales[:, cols],
                     start=(k == 0), stop=(k == W_PASSES - 1),
                 )
 
         def result0(i, n):
-            nc.scalar.copy(out=part("v", i)[:, columns(n)], in_=acc[i, n][:])
+            nc.scalar.copy(out=part("v", i)[:, columns(n)], in_=acc0[i, n][:])
             turnover.append(held[i, n])
 
         def store0(i):
@@ -252,13 +253,13 @@ def tile_diffscm_pb_v_kernel(
                 rows = slice(g * N_TILE + m * P, g * N_TILE + (m + 1) * P)
                 dv_mx[g, m] = (d_codes[:, rows], d_scales[:, rows])
 
-        def pass1(m, n, g, first, final, lo=0, hi=N_TILE):
+        def pass1(m, n, g, first, final):
             if first:
-                held["out_1", m, n, lo], acc1[m, n, lo] = take_bank([P, hi - lo], keep_out=True)
+                held["out_1", m, n], acc1[m, n] = take_bank([P, N_TILE], keep_out=True)
             codes, scales = dv_mx[g, m]
-            cols = slice(g * D + n * N_TILE + lo, g * D + n * N_TILE + hi)
+            cols = slice(g * D + n * N_TILE, g * D + (n + 1) * N_TILE)
             nc.tensor.matmul_mx(
-                out=acc1[m, n, lo][:],
+                out=acc1[m, n][:],
                 lhsT=codes.bitcast(E5M2), lhsT_scale=scales,
                 rhs=x_codes[:, cols].bitcast(E4M3), rhs_scale=x_scales[:, cols],
                 start=first, stop=final,
@@ -270,13 +271,13 @@ def tile_diffscm_pb_v_kernel(
                 res[four] = big_tile([P, 4 * N_TILE], F32)
             return res[four][:, place * N_TILE :]
 
-        def result1(engine, m, n, lo=0, hi=N_TILE, bank=0):
-            copy(engine, result_of(m, n)[:, lo:hi], acc1[m, n, bank][:, lo - bank : hi - bank])
-            if lo == bank:
-                turnover.append(held["out_1", m, n, bank])
+        def result1(engine, m, n, lo=0, hi=N_TILE):
+            copy(engine, result_of(m, n)[:, lo:hi], acc1[m, n][:, lo:hi])
+            if lo == 0:
+                turnover.append(held["out_1", m, n])
 
-        def store1(queue, m, n, lo=0, hi=N_TILE):
-            queue.dma_start(out=out1_v[m][:, n * N_TILE + lo : n * N_TILE + hi], in_=result_of(m, n)[:, lo:hi])
+        def store1(m, n, lo=0, hi=N_TILE):
+            nc.sync.dma_start(out=out1_v[m][:, n * N_TILE + lo : n * N_TILE + hi], in_=result_of(m, n)[:, lo:hi])
 
         def products0(i, head):
             for n in range(2):
@@ -334,28 +335,32 @@ def tile_diffscm_pb_v_kernel(
         quantize_dz(0, 1)
         turn_out(1, 0)
 
-        w_pieces = [("w", k, lo, N_TILE) for k in range(W_PASSES) for lo in (0, N_TILE)]
+        w_pieces = [("w", k, lo) for k in range(W_PASSES) for lo in (0, N_TILE)]
+        final = len(w_pieces) - 1
 
         def head_passes(q):
             for i in range(2):
                 product0(i, q % 2, [q // 2])
 
         for q, piece in enumerate(w_pieces):
+            carried, stepped = N_TILE - CARRIED_W[q], q > 1
             if q == 2:
                 quantize_dz(1, 1)
-            if CARRIED[q]:
-                carry(piece, N_TILE - CARRIED[q], N_TILE, q > 1)
+            if CARRIED_W[q]:
+                carry(piece, carried, N_TILE, stepped)
             interleave("V", piece, 0, VECTOR_W[q])
-            if piece == w_pieces[-1]:
+            if q == final:
                 make_dmu(2)
                 turn(2, 0)
-            if VECTOR_W[q] + CARRIED[q] < N_TILE:
-                interleave("S", piece, VECTOR_W[q], N_TILE - CARRIED[q])
+            if VECTOR_W[q] < carried:
+                interleave("S", piece, VECTOR_W[q], carried)
+            if q == final:
+                sigmoid(2, 0)
             if q == 0:
                 turn_out(1, 1)
                 quantize_dz(1, 0)
-            if CARRIED[q]:
-                carry_out(piece, N_TILE - CARRIED[q], N_TILE, q > 1)
+            if CARRIED_W[q]:
+                carry_out(piece, carried, N_TILE, stepped)
             if q > 0:
                 quantize(w_pieces[q - 1])
             if q > 1:
@@ -372,31 +377,30 @@ def tile_diffscm_pb_v_kernel(
         load_x(1)
         load_x(2)
 
-        sigmoid(2)
+        sigmoid(2, 1)
         first_product(2)
         turn_out(2, 0)
-        head_passes(len(w_pieces) - 2)
-        quantize(w_pieces[-1])
-        head_passes(len(w_pieces) - 1)
+        head_passes(final - 1)
+        quantize(w_pieces[final])
+        head_passes(final)
         sigmoid(3)
         results0(0)
 
         last = SLICES - 1
-        d_left = [("d", g, 0, N_TILE) for g in range(GROUPS)]
-        x_left = [("x", g, 0, N_TILE) for g in range(GROUPS)]
-        x_right = [("x", g, N_TILE, N_TILE) for g in range(GROUPS)]
-        begins = {4: d_left[0], 6: x_left[0], 9: d_left[1]}
-        end = N_TILE - 2 * 32
+        d_left = [("d", g, 0) for g in range(GROUPS)]
+        x_left = [("x", g, 0) for g in range(GROUPS)]
+        x_right = [("x", g, N_TILE) for g in range(GROUPS)]
+        begins = {PACK: d_left[0], PACK + 2: x_left[0], 2 * PACK + 1: d_left[1]}
+        end = N_TILE - 2 * CARRIED_EARLY
         middle = (SCALAR_EARLY + end) // 2
         for i in range(2, SLICES):
+            early = [(begins[i - step], step) for step in range(2) if i - step in begins]
             if i > 2:
                 first_product(i)
             if i < last:
                 make_dmu(i + 1)
-            if i in begins:
-                interleave("V", begins[i], SCALAR_EARLY, middle)
-            if i - 1 in begins:
-                interleave("V", begins[i - 1], middle, end)
+            for piece, step in early:
+                interleave("V", piece, *((SCALAR_EARLY, middle), (middle, end))[step])
             make_dv(i, 0)
             make_dv(i, 1)
             if i > 2:
@@ -410,33 +414,29 @@ def tile_diffscm_pb_v_kernel(
             if i > 2:
                 products0(i - 1, 1)
             products0(i, 0)
-            for step in range(2):
-                if i - step in begins:
-                    carry(begins[i - step], end + step * 32, end + (step + 1) * 32)
+            for piece, step in early:
+                carry(piece, end + step * CARRIED_EARLY, end + (step + 1) * CARRIED_EARLY)
             if i == last:
-                interleave("S", x_left[2], 0, N_TILE // 2)
+                interleave("S", x_left[2], 0, HALF)
             turn_out(i, 1)
             if i < last:
                 turn_out(i + 1, 0)
             if i + 2 < SLICES:
                 sigmoid(i + 2)
-            if i in begins:
-                interleave("S", begins[i], 0, SCALAR_EARLY // 2)
-            if i - 1 in begins:
-                interleave("S", begins[i - 1], SCALAR_EARLY // 2, SCALAR_EARLY)
+            for piece, step in early:
+                interleave("S", piece, step * SCALAR_EARLY // 2, (step + 1) * SCALAR_EARLY // 2)
             if i < last:
                 results0(i - 1)
-            for step in range(2):
-                if i - step in begins:
-                    carry_out(begins[i - step], end + step * 32, end + (step + 1) * 32)
+            for piece, step in early:
+                carry_out(piece, end + step * CARRIED_EARLY, end + (step + 1) * CARRIED_EARLY)
+
         quantize(x_left[0])
         quadrant(0, 0, True, False)
         quantize(d_left[1])
-
         interleave("V", x_left[1])
         quantize_dz(last, 1)
         products0(last, 1)
-        interleave("S", x_left[2], N_TILE // 2, N_TILE)
+        interleave("S", x_left[2], HALF, N_TILE)
         results0(last - 1)
         interleave("S", x_right[0])
         interleave("V", d_left[2])
@@ -445,48 +445,46 @@ def tile_diffscm_pb_v_kernel(
         carry(x_right[1], N_TILE - P, N_TILE)
         results0(last)
         carry_out(x_right[1], N_TILE - P, N_TILE)
-        interleave("V", x_right[2], 0, N_TILE // 2)
+        interleave("V", x_right[2], 0, HALF)
         quantize(d_left[2])
         quantize(x_left[2])
         quadrant(0, 2, False, True)
-        interleave("V", x_right[2], N_TILE // 2, N_TILE)
+        interleave("V", x_right[2], HALF, N_TILE)
         quantize(x_right[0])
         quadrant(1, 0, True, False)
-        interleave("S", x_right[1], 320, N_TILE - P)
-        interleave("V", x_right[1], 0, 320)
+        interleave("S", x_right[1], N_TILE - P - SCALAR_LAST, N_TILE - P)
+        interleave("V", x_right[1], 0, N_TILE - P - SCALAR_LAST)
         quantize(x_right[2])
         quadrant(1, 2, False, False)
         for m in range(ROW_TILES // 2):
             result1("S", m, 0)
-            store1(nc.sync, m, 0)
-        interleave_rows("V", 4, 0, 1)
+            store1(m, 0)
+        upper = ROW_TILES // 2
+        interleave_rows("V", upper, 0, 1)
         quantize(x_right[1])
         quadrant(1, 1, False, True)
-        interleave_rows("V", 4, 1, 2)
-        interleave_rows("V", 4, 2, 3)
-        interleave_rows("S", 5, 2, 3)
+        interleave_rows("V", upper, 1, 2)
+        interleave_rows("V", upper, 2, 3)
+        interleave_rows("S", upper + 1, 2, 3)
         for m in range(ROW_TILES // 2):
             result1("S", m, 1)
-            store1(nc.sync, m, 1)
-        for m in range(ROW_TILES // 2, ROW_TILES):
-            if m > 4:
+            store1(m, 1)
+
+        for m in range(upper, ROW_TILES):
+            if m > upper:
                 interleave_rows("V", m, 0, 2)
-            if m > 5:
+            if m > upper + 1:
                 interleave_rows("V", m, 2, 3)
             quantize_rows(m)
             row_tile(m)
-        result1("S", 4, 0)
-        result1("S", 4, 1)
-        store1(nc.sync, 4, 0, 0, D)
-        result1("S", 5, 0)
-        result1("S", 5, 1)
-        store1(nc.sync, 5, 0, 0, D)
-        result1("S", 6, 0)
-        store1(nc.sync, 6, 0)
-        result1("V", 6, 1)
-        store1(nc.sync, 6, 1)
-        result1("S", 7, 0)
-        store1(nc.sync, 7, 0)
-        for lo in (0, N_TILE // 2):
-            result1("V", 7, 1, lo, lo + N_TILE // 2)
-            store1(nc.sync, 7, 1, lo, lo + N_TILE // 2)
+
+        for m in (upper, upper + 1):
+            for n in range(2):
+                result1("S", m, n)
+            store1(m, 0, 0, D)
+        for engine, m, n in (("S", upper + 2, 0), ("V", upper + 2, 1), ("S", upper + 3, 0)):
+            result1(engine, m, n)
+            store1(m, n)
+        for lo in (0, HALF):
+            result1("V", upper + 3, 1, lo, lo + HALF)
+            store1(upper + 3, 1, lo, lo + HALF)

@@ -14,11 +14,14 @@ DMA_ALIGN = 256
 RUN = 8
 W_PASSES = 4
 ROW_TILES = D // P
+POOL_COLUMNS = 384
+STAGING = {"V": 3, "S": 3, "G": 1}
 CARRIED_W = [0, HALF] + [P] * 5 + [HALF]
 VECTOR_W = [HALF, HALF] + [208] * 5 + [P]
-SCALAR_EARLY = 96
+SCALAR_EARLY = 128
 CARRIED_EARLY = 32
 SCALAR_LAST = 64
+
 FLOPS = 2 * B * D * D * 3
 BYTES = 2 * (3 * B * D + 2 * D * D + B) + 4 * B * D + 4 * (B * D + D * D)
 
@@ -29,6 +32,7 @@ U8 = mybir.dt.uint8
 E4M3 = mybir.dt.float8_e4m3fn_x4
 E5M2 = mybir.dt.float8_e5m2_x4
 MULT = mybir.AluOpType.mult
+ADD = mybir.AluOpType.add
 SIGMOID = mybir.ActivationFunctionType.Sigmoid
 
 
@@ -101,6 +105,9 @@ def tile_diffscm_pb_v_kernel(
         def load_w(k):
             nc.sync.dma_start(out=raw["w", k][:], in_=w_hbm[k])
 
+        def rows_of(kind, k, lo, hi):
+            return raw[kind, k][:].rearrange("p (t c) -> p t c", t=PACK)[:, :, lo:hi]
+
         def load_x(g):
             raw["x", g] = big_tile([P, PACK * D], BF16)
             nc.sync.dma_start(out=raw["x", g][:], in_=hbm["x"][g])
@@ -111,33 +118,47 @@ def tile_diffscm_pb_v_kernel(
             else:
                 nc.scalar.copy(out=out, in_=in_)
 
-        grp, prod, dmu, banks, dzt, dz, acc0, acc1, dv_mx, held, res = {}, {}, {}, {}, {}, {}, {}, {}, {}, {}, {}
+        gate, early = {}, {}
+        grp, moved, dmu, banks, dzt, dz, acc0, acc1, dv_mx, held, res = {}, {}, {}, {}, {}, {}, {}, {}, {}, {}, {}
 
-        def staging(key, width, engine):
+        def staging(key, width, tag):
             if key not in grp:
-                tag = "grp" + engine
-                grp[key] = work.tile([P, width * PACK], BF16, tag=tag, bufs=3, align_bytes=64, name=tag)
+                grp[key] = work.tile([P, width * PACK], BF16, tag=tag, bufs=STAGING[tag], align_bytes=64, name=tag)
             return grp[key]
 
-        def interleave(engine, piece, a=0, b=N_TILE):
-            kind, k, lo = piece
-            dst = staging(piece, N_TILE, engine)[:].rearrange("p (c i t) -> p c t i", i=RUN, t=PACK)
-            src = raw[kind, k][:].rearrange("p (t c i) -> p c t i", t=PACK, i=RUN)
-            copy(engine, dst[:, a // RUN : b // RUN], src[:, (lo + a) // RUN : (lo + b) // RUN])
+        def interleave(engine, piece, a=None, b=None, tag=None):
+            kind, k, lo, hi = piece
+            a, b = a or 0, b or hi - lo
+            dst = staging(piece, hi - lo, tag or engine)[:, a * PACK : b * PACK]
+            src = rows_of(kind, k, lo + a, lo + b)
+            if engine == "G":
+                nc.gpsimd.tensor_scalar(
+                    out=dst.rearrange("p (c t) -> p c t", t=PACK), in0=src.rearrange("p t c -> p c t"),
+                    scalar1=1.0, scalar2=0.0, op0=MULT, op1=ADD,
+                )
+            elif kind == "d":
+                rows = rows_of(kind, k, lo, hi).rearrange("p t (u w e) -> p u w t e", u=2, e=2)
+                for u in range(2):
+                    copy(engine, dst.rearrange("p (w u e t) -> p u w t e", u=2, e=2, t=PACK)[:, u], rows[:, u, a // 4 : b // 4])
+            else:
+                copy(
+                    engine,
+                    dst.rearrange("p (c i t) -> p c t i", i=RUN, t=PACK),
+                    src.rearrange("p t (c i) -> p c t i", i=RUN),
+                )
 
         def carry(piece, a, b, stepped=True):
-            kind, k, lo = piece
+            kind, k, lo, hi = piece
             blocks = -(-(b - a) // P)
             w = (b - a) // blocks
             banks[piece] = take_bank([P, blocks, PACK * w], dtype=BF16)[1]
-            rows = raw[kind, k][:].rearrange("p (t c) -> p t c", t=PACK)
             for j in range(blocks):
                 out = banks[piece][:, j].rearrange("p (c t) -> p t c" if stepped else "p (t c) -> p t c", t=PACK)
                 first = lo + a + j * w
-                nc.tensor.matmul(out, lhsT=ident_bf[:], rhs=rows[:, :, first : first + w], start=True, stop=True)
+                nc.tensor.matmul(out, lhsT=ident_bf[:], rhs=rows_of(kind, k, first, first + w), start=True, stop=True)
 
         def carry_out(piece, a, b, stepped=True):
-            dst = staging(piece, N_TILE, "S")[:, a * PACK : b * PACK]
+            dst = staging(piece, piece[3] - piece[2], "S")[:, a * PACK : b * PACK]
             if stepped:
                 nc.scalar.copy(out=dst, in_=banks[piece][:].rearrange("p j x -> p (j x)"))
             else:
@@ -147,17 +168,18 @@ def tile_diffscm_pb_v_kernel(
                 )
 
         def quantize(piece):
-            kind, k, lo = piece
+            kind, k, lo, hi = piece
             codes, scales, fmt = planes[kind]
-            first = k * (N_TILE if kind == "d" else D) + lo
-            c = slice(first, first + N_TILE)
+            first = k * (N_TILE if kind == "d" else D)
+            c = slice(first + lo, first + hi)
             nc.vector.quantize_mx(out=codes[:, c].bitcast(fmt), scales=scales[:, c], in_=grp[piece][:])
 
         def interleave_rows(engine, m, lo, hi):
-            src = e_all[:].rearrange("p (g t c i) -> p g c t i", g=GROUPS, t=PACK, i=RUN)
-            first = m * P
-            dst = staging(m, GROUPS * P, "V")[:].rearrange("p (g c i t) -> p g c t i", g=GROUPS, i=RUN, t=PACK)
-            copy(engine, dst[:, lo:hi], src[:, lo:hi, first // RUN : (first + P) // RUN])
+            src = e_all[:].rearrange("p (g t k u w e) -> p k u g w t e", g=GROUPS, t=PACK, k=2, u=2, e=2)
+            k, first = divmod(m * P, N_TILE)
+            dst = staging(m, GROUPS * P, "V")[:].rearrange("p (g w u e t) -> p u g w t e", g=GROUPS, u=2, e=2, t=PACK)
+            for u in range(2):
+                copy(engine, dst[:, u, lo:hi], src[:, k, u, lo:hi, first // 4 : (first + P) // 4])
 
         def quantize_rows(m):
             codes, scales = mx_operand(work, GROUPS * P, False, name="r", bufs=3)
@@ -171,31 +193,62 @@ def tile_diffscm_pb_v_kernel(
         def columns(half):
             return slice(0, D) if half is None else slice(half * N_TILE, (half + 1) * N_TILE)
 
-        def sigmoid(i, half=None):
-            values = part("v", i)[:, columns(half)]
-            nc.scalar.activation(out=values, in_=values, func=SIGMOID)
-
-        def first_product(i):
-            prod[i] = work.tile([P, D], F32, tag="prod", bufs=2, name="prod")
-            for c in map(columns, (None,) if i < 2 else (0, 1)):
-                nc.vector.scalar_tensor_tensor(
-                    out=prod[i][:, c], in0=part("g", i)[:, c], scalar=t_col[:, i : i + 1], in1=part("e", i)[:, c],
-                    op0=MULT, op1=MULT,
-                )
-
         sorted_in = lambda a: a.rearrange("p (w u e) -> p u w e", u=2, e=2)
         sorted_out = lambda a: a.rearrange("p (u w e) -> p u w e", u=2, e=2)
+
+        def sigmoid(i, half=None):
+            for h in range(2) if half is None else (half,):
+                gate[i, h] = work.tile([P, N_TILE], F32, tag="gate", bufs=4, name="gate")
+                nc.scalar.activation(out=sorted_out(gate[i, h][:]), in_=sorted_in(part("v", i)[:, columns(h)]), func=SIGMOID)
+
+        def move(kind, i):
+            moved[kind, i] = take_bank([P, D], dtype=BF16)[1]
+            for half in range(2):
+                nc.tensor.matmul(
+                    moved[kind, i][:, columns(half)].rearrange("p (u w e) -> p w u e", u=2, e=2),
+                    lhsT=ident_bf[:], rhs=part(kind, i)[:, columns(half)], start=True, stop=True,
+                )
+
+        def source(kind, i, half):
+            if (kind, i) in moved:
+                return sorted_out(moved[kind, i][:, columns(half)])
+            return sorted_in(part(kind, i)[:, columns(half)])
+
+        def first_product(i, half):
+            values = sorted_out(gate[i, half][:])
+            nc.vector.tensor_tensor(out=values, in0=values, in1=source("e", i, half), op=MULT)
 
         def make_dmu(i):
             dmu[i] = work.tile([P, D], BF16, tag="dmu", bufs=2, name="dmu")
             nc.vector.tensor_scalar(
-                out=sorted_out(dmu[i][:]), in0=sorted_in(part("g", i)), scalar1=t_col[:, i : i + 1], scalar2=None, op0=MULT
+                out=dmu[i][:].rearrange("p (u w e) -> p u w e", u=2, e=2), in0=sorted_in(part("g", i)),
+                scalar1=t_col[:, i : i + 1], scalar2=None, op0=MULT,
             )
 
         def make_dv(i, half):
-            nc.vector.tensor_tensor(
-                out=part("e", i)[:, columns(half)], in0=prod[i][:, columns(half)], in1=part("v", i)[:, columns(half)], op=MULT
-            )
+            for u in range(2):
+                nc.vector.scalar_tensor_tensor(
+                    out=sorted_out(part("e", i)[:, columns(half)])[:, u], in0=source("g", i, half)[:, u],
+                    scalar=t_col[:, i : i + 1], in1=sorted_out(gate[i, half][:])[:, u], op0=MULT, op1=MULT,
+                )
+
+        def early_product(i):
+            early[i] = work.tile([P, D], F32, tag="S", bufs=STAGING["S"], align_bytes=64, name="early")
+            for half in range(2):
+                for u in range(2):
+                    nc.vector.scalar_tensor_tensor(
+                        out=sorted_out(early[i][:, columns(half)])[:, u], in0=source("g", i, half)[:, u],
+                        scalar=t_col[:, i : i + 1], in1=source("e", i, half)[:, u], op0=MULT, op1=MULT,
+                    )
+
+        def early_dv(i, half):
+            c = columns(half)
+            nc.vector.tensor_tensor(out=part("e", i)[:, c], in0=early[i][:, c], in1=gate[i, half][:], op=MULT)
+
+        def products(i):
+            for make in (first_product, make_dv):
+                for half in range(2):
+                    make(i, half)
 
         def turn(i, head):
             bank = take_bank([P, 2, 2, P])[1]
@@ -203,7 +256,7 @@ def tile_diffscm_pb_v_kernel(
             for k in range(2):
                 for u in range(2):
                     if head:
-                        block = words[:, 256 * k + u : 256 * (k + 1) : 2]
+                        block = words[:, 256 * k + P * u : 256 * k + P * (u + 1)]
                     else:
                         block = words[:, 256 * u + P * k : 256 * u + P * (k + 1)]
                     nc.tensor.transpose(bank[:, k, u, :], block, ident[:])
@@ -218,15 +271,16 @@ def tile_diffscm_pb_v_kernel(
                 in_=banks[i, head][:].rearrange("p k u c -> p k c u"),
             )
 
-        def quantize_dz(i, head):
-            if not head:
+        def quantize_dz(i, head=None):
+            if i not in dz:
                 dz[i] = mx_operand(work, W_PASSES * P, False, name="z", bufs=3)
-            c = slice(head * 2 * P, (head + 1) * 2 * P)
+            lo, hi = (0, 2) if head is None else (head, head + 1)
+            c = slice(lo * 2 * P, hi * 2 * P)
             nc.vector.quantize_mx(
-                out=dz[i][0][:, c].bitcast(E5M2), scales=dz[i][1][:, c], in_=dzt[i][:, head * D : (head + 1) * D]
+                out=dz[i][0][:, c].bitcast(E5M2), scales=dz[i][1][:, c], in_=dzt[i][:, lo * D : hi * D]
             )
 
-        def product0(i, n, passes):
+        def product0(i, n, passes=range(W_PASSES)):
             if passes[0] == 0:
                 held[i, n], acc0[i, n] = take_bank([P, N_TILE], keep_out=True)
             codes, scales = dz[i]
@@ -315,27 +369,27 @@ def tile_diffscm_pb_v_kernel(
         make_identity(nc, ident_bf[:])
 
         make_dmu(0)
-        first_product(0)
+        early_product(0)
         turn(0, 0)
         for half in range(2):
             sigmoid(0, half)
-            make_dv(0, half)
+            early_dv(0, half)
         turn(0, 1)
         turn_out(0, 0)
         for half in range(2):
             sigmoid(1, half)
         turn_out(0, 1)
-        first_product(1)
+        early_product(1)
         make_dmu(1)
         quantize_dz(0, 0)
         for half in range(2):
-            make_dv(1, half)
+            early_dv(1, half)
         turn(1, 0)
         turn(1, 1)
         quantize_dz(0, 1)
         turn_out(1, 0)
 
-        w_pieces = [("w", k, lo) for k in range(W_PASSES) for lo in (0, N_TILE)]
+        w_pieces = [("w", k, lo, lo + N_TILE) for k in range(W_PASSES) for lo in (0, N_TILE)]
         final = len(w_pieces) - 1
 
         def head_passes(q):
@@ -378,7 +432,7 @@ def tile_diffscm_pb_v_kernel(
         load_x(2)
 
         sigmoid(2, 1)
-        first_product(2)
+        early_product(2)
         turn_out(2, 0)
         head_passes(final - 1)
         quantize(w_pieces[final])
@@ -387,22 +441,24 @@ def tile_diffscm_pb_v_kernel(
         results0(0)
 
         last = SLICES - 1
-        d_left = [("d", g, 0) for g in range(GROUPS)]
-        x_left = [("x", g, 0) for g in range(GROUPS)]
-        x_right = [("x", g, N_TILE) for g in range(GROUPS)]
+        d_left = [("d", g, 0, N_TILE) for g in range(GROUPS)]
+        x_left = [("x", g, 0, N_TILE) for g in range(GROUPS)]
+        x_right = [("x", g, N_TILE, D) for g in range(GROUPS)]
         begins = {PACK: d_left[0], PACK + 2: x_left[0], 2 * PACK + 1: d_left[1]}
-        end = N_TILE - 2 * CARRIED_EARLY
-        middle = (SCALAR_EARLY + end) // 2
+        ends = {"d": N_TILE, "x": N_TILE - 2 * CARRIED_EARLY}
         for i in range(2, SLICES):
-            early = [(begins[i - step], step) for step in range(2) if i - step in begins]
+            early_pieces = [(begins[i - step], step) for step in range(2) if i - step in begins]
             if i > 2:
-                first_product(i)
+                first_product(i, 0)
+                first_product(i, 1)
             if i < last:
                 make_dmu(i + 1)
-            for piece, step in early:
+            for piece, step in early_pieces:
+                end = ends[piece[0]]
+                middle = (SCALAR_EARLY + end) // 2
                 interleave("V", piece, *((SCALAR_EARLY, middle), (middle, end))[step])
-            make_dv(i, 0)
-            make_dv(i, 1)
+            for half in range(2):
+                (make_dv if i > 2 else early_dv)(i, half)
             if i > 2:
                 quantize_dz(i - 1, 1)
             quantize_dz(i, 0)
@@ -414,8 +470,9 @@ def tile_diffscm_pb_v_kernel(
             if i > 2:
                 products0(i - 1, 1)
             products0(i, 0)
-            for piece, step in early:
-                carry(piece, end + step * CARRIED_EARLY, end + (step + 1) * CARRIED_EARLY)
+            carried = [(piece, ends["x"] + step * CARRIED_EARLY) for piece, step in early_pieces if piece[0] == "x"]
+            for piece, first in carried:
+                carry(piece, first, first + CARRIED_EARLY)
             if i == last:
                 interleave("S", x_left[2], 0, HALF)
             turn_out(i, 1)
@@ -423,12 +480,12 @@ def tile_diffscm_pb_v_kernel(
                 turn_out(i + 1, 0)
             if i + 2 < SLICES:
                 sigmoid(i + 2)
-            for piece, step in early:
+            for piece, step in early_pieces:
                 interleave("S", piece, step * SCALAR_EARLY // 2, (step + 1) * SCALAR_EARLY // 2)
             if i < last:
                 results0(i - 1)
-            for piece, step in early:
-                carry_out(piece, end + step * CARRIED_EARLY, end + (step + 1) * CARRIED_EARLY)
+            for piece, first in carried:
+                carry_out(piece, first, first + CARRIED_EARLY)
 
         quantize(x_left[0])
         quadrant(0, 0, True, False)

@@ -14,13 +14,12 @@ DMA_ALIGN = 256
 RUN = 8
 W_PASSES = 4
 ROW_TILES = D // P
-POOL_COLUMNS = 384
-STAGING = {"V": 3, "S": 3, "G": 1}
+POOL_COLUMNS = 368
+STAGING = {"V": 3, "S": 2, "G": 1, "dzt": 3}
 CARRIED_W = [0, HALF] + [P] * 5 + [HALF]
 VECTOR_W = [HALF, HALF] + [208] * 5 + [P]
-SCALAR_EARLY = 128
-CARRIED_EARLY = 32
-SCALAR_LAST = 64
+SCALAR_EARLY = 192
+WINDOWS = [6, 7]
 
 FLOPS = 2 * B * D * D * 3
 BYTES = 2 * (3 * B * D + 2 * D * D + B) + 4 * B * D + 4 * (B * D + D * D)
@@ -82,13 +81,15 @@ def tile_diffscm_pb_v_kernel(
             raw["d", g] = raw["e", g]
             raw["v", g] = inp.tile([P, PACK * D], F32, tag="v", bufs=GROUPS, align_bytes=DMA_ALIGN, name="raw_v")
 
-        turnover = list(range(8))
+        turnover, held, banks = list(range(8)), {}, {}
 
-        def take_bank(shape, keep_out=False, dtype=F32):
-            b = turnover.pop(0)
-            if not keep_out:
-                turnover.append(b)
-            return b, psum.tile(shape, dtype, tag="bank%d" % b, name="bank")
+        def take_bank(key, shape, dtype=F32):
+            held[key] = turnover.pop(0)
+            banks[key] = psum.tile(shape, dtype, tag="bank%d" % held[key], name="bank")
+            return banks[key]
+
+        def give_back(key):
+            turnover.append(held[key])
 
         def part(kind, i, n=1):
             g, j = divmod(i, PACK)
@@ -119,7 +120,7 @@ def tile_diffscm_pb_v_kernel(
                 nc.scalar.copy(out=out, in_=in_)
 
         gate, early = {}, {}
-        grp, moved, dmu, banks, dzt, dz, acc0, acc1, dv_mx, held, res = {}, {}, {}, {}, {}, {}, {}, {}, {}, {}, {}
+        grp, dmu, dzt, dz, dv_mx, res = {}, {}, {}, {}, {}, {}
 
         def staging(key, width, tag):
             if key not in grp:
@@ -151,7 +152,7 @@ def tile_diffscm_pb_v_kernel(
             kind, k, lo, hi = piece
             blocks = -(-(b - a) // P)
             w = (b - a) // blocks
-            banks[piece] = take_bank([P, blocks, PACK * w], dtype=BF16)[1]
+            take_bank(piece, [P, blocks, PACK * w], BF16)
             for j in range(blocks):
                 out = banks[piece][:, j].rearrange("p (c t) -> p t c" if stepped else "p (t c) -> p t c", t=PACK)
                 first = lo + a + j * w
@@ -166,6 +167,7 @@ def tile_diffscm_pb_v_kernel(
                     out=dst.rearrange("p (j c t) -> p j c t", c=P, t=PACK),
                     in_=banks[piece][:].rearrange("p j (t c) -> p j c t", t=PACK),
                 )
+            give_back(piece)
 
         def quantize(piece):
             kind, k, lo, hi = piece
@@ -202,21 +204,23 @@ def tile_diffscm_pb_v_kernel(
                 nc.scalar.activation(out=sorted_out(gate[i, h][:]), in_=sorted_in(part("v", i)[:, columns(h)]), func=SIGMOID)
 
         def move(kind, i):
-            moved[kind, i] = take_bank([P, D], dtype=BF16)[1]
+            bank = take_bank((kind, i), [P, D], BF16)
             for half in range(2):
                 nc.tensor.matmul(
-                    moved[kind, i][:, columns(half)].rearrange("p (u w e) -> p w u e", u=2, e=2),
+                    bank[:, columns(half)].rearrange("p (u w e) -> p w u e", u=2, e=2),
                     lhsT=ident_bf[:], rhs=part(kind, i)[:, columns(half)], start=True, stop=True,
                 )
 
         def source(kind, i, half):
-            if (kind, i) in moved:
-                return sorted_out(moved[kind, i][:, columns(half)])
+            if (kind, i) in banks:
+                return sorted_out(banks[kind, i][:, columns(half)])
             return sorted_in(part(kind, i)[:, columns(half)])
 
         def first_product(i, half):
             values = sorted_out(gate[i, half][:])
             nc.vector.tensor_tensor(out=values, in0=values, in1=source("e", i, half), op=MULT)
+            if half and ("e", i) in banks:
+                give_back(("e", i))
 
         def make_dmu(i):
             dmu[i] = work.tile([P, D], BF16, tag="dmu", bufs=2, name="dmu")
@@ -226,11 +230,14 @@ def tile_diffscm_pb_v_kernel(
             )
 
         def make_dv(i, half):
-            for u in range(2):
+            moved = ("g", i) in banks
+            for u in (slice(None),) if moved else range(2):
                 nc.vector.scalar_tensor_tensor(
                     out=sorted_out(part("e", i)[:, columns(half)])[:, u], in0=source("g", i, half)[:, u],
                     scalar=t_col[:, i : i + 1], in1=sorted_out(gate[i, half][:])[:, u], op0=MULT, op1=MULT,
                 )
+            if half and moved:
+                give_back(("g", i))
 
         def early_product(i):
             early[i] = work.tile([P, D], F32, tag="S", bufs=STAGING["S"], align_bytes=64, name="early")
@@ -251,7 +258,7 @@ def tile_diffscm_pb_v_kernel(
                     make(i, half)
 
         def turn(i, head):
-            bank = take_bank([P, 2, 2, P])[1]
+            bank = take_bank((i, head), [P, 2, 2, P])
             words = (part("e", i) if head else dmu[i][:]).bitcast(F32)
             for k in range(2):
                 for u in range(2):
@@ -260,16 +267,14 @@ def tile_diffscm_pb_v_kernel(
                     else:
                         block = words[:, 256 * u + P * k : 256 * u + P * (k + 1)]
                     nc.tensor.transpose(bank[:, k, u, :], block, ident[:])
-            banks[i, head] = bank
 
-        def turn_out(i, head):
+        def turn_out(i, head, engine="S"):
             if not head:
-                dzt[i] = work.tile([P, 2 * D], BF16, tag="dzt", bufs=3, align_bytes=64, name="dzt")
+                tag = "G" if i + 2 in WINDOWS and i + 1 not in WINDOWS else "dzt"
+                dzt[i] = work.tile([P, 2 * D], BF16, tag=tag, bufs=STAGING[tag], align_bytes=64, name=tag)
             dst = dzt[i][:, head * D : (head + 1) * D].bitcast(F32)
-            nc.scalar.copy(
-                out=dst.rearrange("p (k c u) -> p k c u", k=2, u=2),
-                in_=banks[i, head][:].rearrange("p k u c -> p k c u"),
-            )
+            copy(engine, dst.rearrange("p (k c u) -> p k c u", k=2, u=2), banks[i, head][:].rearrange("p k u c -> p k c u"))
+            give_back((i, head))
 
         def quantize_dz(i, head=None):
             if i not in dz:
@@ -282,21 +287,21 @@ def tile_diffscm_pb_v_kernel(
 
         def product0(i, n, passes=range(W_PASSES)):
             if passes[0] == 0:
-                held[i, n], acc0[i, n] = take_bank([P, N_TILE], keep_out=True)
+                take_bank(("out_0", i, n), [P, N_TILE])
             codes, scales = dz[i]
             for k in passes:
                 rows = slice(k * P, (k + 1) * P)
                 cols = slice(k * D + n * N_TILE, k * D + (n + 1) * N_TILE)
                 nc.tensor.matmul_mx(
-                    out=acc0[i, n][:],
+                    out=banks["out_0", i, n][:],
                     lhsT=codes[:, rows].bitcast(E5M2), lhsT_scale=scales[:, rows],
                     rhs=w_codes[:, cols].bitcast(E4M3), rhs_scale=w_scales[:, cols],
                     start=(k == 0), stop=(k == W_PASSES - 1),
                 )
 
         def result0(i, n):
-            nc.scalar.copy(out=part("v", i)[:, columns(n)], in_=acc0[i, n][:])
-            turnover.append(held[i, n])
+            nc.scalar.copy(out=part("v", i)[:, columns(n)], in_=banks["out_0", i, n][:])
+            give_back(("out_0", i, n))
 
         def store0(i):
             g, j = divmod(i, PACK)
@@ -309,11 +314,11 @@ def tile_diffscm_pb_v_kernel(
 
         def pass1(m, n, g, first, final):
             if first:
-                held["out_1", m, n], acc1[m, n] = take_bank([P, N_TILE], keep_out=True)
+                take_bank(("out_1", m, n), [P, N_TILE])
             codes, scales = dv_mx[g, m]
             cols = slice(g * D + n * N_TILE, g * D + (n + 1) * N_TILE)
             nc.tensor.matmul_mx(
-                out=acc1[m, n][:],
+                out=banks["out_1", m, n][:],
                 lhsT=codes.bitcast(E5M2), lhsT_scale=scales,
                 rhs=x_codes[:, cols].bitcast(E4M3), rhs_scale=x_scales[:, cols],
                 start=first, stop=final,
@@ -326,9 +331,9 @@ def tile_diffscm_pb_v_kernel(
             return res[four][:, place * N_TILE :]
 
         def result1(engine, m, n, lo=0, hi=N_TILE):
-            copy(engine, result_of(m, n)[:, lo:hi], acc1[m, n][:, lo:hi])
+            copy(engine, result_of(m, n)[:, lo:hi], banks["out_1", m, n][:, lo:hi])
             if lo == 0:
-                turnover.append(held["out_1", m, n])
+                give_back(("out_1", m, n))
 
         def store1(m, n, lo=0, hi=N_TILE):
             nc.sync.dma_start(out=out1_v[m][:, n * N_TILE + lo : n * N_TILE + hi], in_=result_of(m, n)[:, lo:hi])
@@ -444,35 +449,42 @@ def tile_diffscm_pb_v_kernel(
         d_left = [("d", g, 0, N_TILE) for g in range(GROUPS)]
         x_left = [("x", g, 0, N_TILE) for g in range(GROUPS)]
         x_right = [("x", g, N_TILE, D) for g in range(GROUPS)]
-        begins = {PACK: d_left[0], PACK + 2: x_left[0], 2 * PACK + 1: d_left[1]}
-        ends = {"d": N_TILE, "x": N_TILE - 2 * CARRIED_EARLY}
+        windows = dict(zip(WINDOWS, (x_left[0], x_right[0], x_left[1], x_right[1])))
+        shares = {5: (d_left[0], 0, 320)}
         for i in range(2, SLICES):
-            early_pieces = [(begins[i - step], step) for step in range(2) if i - step in begins]
-            if i > 2:
-                first_product(i, 0)
-                first_product(i, 1)
-            if i < last:
+            if i in windows:
+                interleave("G", windows[i], 0, POOL_COLUMNS)
+                products(i)
                 make_dmu(i + 1)
-            for piece, step in early_pieces:
-                end = ends[piece[0]]
-                middle = (SCALAR_EARLY + end) // 2
-                interleave("V", piece, *((SCALAR_EARLY, middle), (middle, end))[step])
-            for half in range(2):
-                (make_dv if i > 2 else early_dv)(i, half)
-            if i > 2:
+            else:
+                if i > 2:
+                    first_product(i, 0)
+                    first_product(i, 1)
+                if i < last:
+                    make_dmu(i + 1)
+                for half in range(2):
+                    (make_dv if i > 2 else early_dv)(i, half)
+            if i + 1 in windows and i not in windows:
+                interleave("V", *shares[i])
+                quantize_dz(i, 0)
                 quantize_dz(i - 1, 1)
-            quantize_dz(i, 0)
-            if i == 2 * PACK:
-                quantize(d_left[0])
-            if i < last:
-                turn(i + 1, 0)
-            turn(i, 1)
+            else:
+                if i > 2:
+                    quantize_dz(i - 1, 1)
+                if i in windows:
+                    interleave("V", windows[i], POOL_COLUMNS, N_TILE)
+                quantize_dz(i, 0)
+                if i in windows:
+                    quantize(windows[i])
+            if i + 1 in windows:
+                move("e", i + 1)
+                move("g", i + 1)
+            for s, head in ((i, 1), (i + 1, 0)) if i in windows else ((i + 1, 0), (i, 1)):
+                if s < SLICES:
+                    turn(s, head)
             if i > 2:
                 products0(i - 1, 1)
             products0(i, 0)
-            carried = [(piece, ends["x"] + step * CARRIED_EARLY) for piece, step in early_pieces if piece[0] == "x"]
-            for piece, first in carried:
-                carry(piece, first, first + CARRIED_EARLY)
             if i == last:
                 interleave("S", x_left[2], 0, HALF)
             turn_out(i, 1)
@@ -480,46 +492,40 @@ def tile_diffscm_pb_v_kernel(
                 turn_out(i + 1, 0)
             if i + 2 < SLICES:
                 sigmoid(i + 2)
-            for piece, step in early_pieces:
-                interleave("S", piece, step * SCALAR_EARLY // 2, (step + 1) * SCALAR_EARLY // 2)
             if i < last:
                 results0(i - 1)
-            for piece, first in carried:
-                carry_out(piece, first, first + CARRIED_EARLY)
+            if i in windows and i - 1 in windows:
+                interleave("S", d_left[0], 320, N_TILE)
 
-        quantize(x_left[0])
+        quantize(d_left[0])
         quadrant(0, 0, True, False)
-        quantize(d_left[1])
-        interleave("V", x_left[1])
+        interleave("V", d_left[1])
         quantize_dz(last, 1)
         products0(last, 1)
         interleave("S", x_left[2], HALF, N_TILE)
         results0(last - 1)
-        interleave("S", x_right[0])
-        interleave("V", d_left[2])
+        interleave("V", x_left[1])
+        quantize(d_left[1])
         quantize(x_left[1])
         quadrant(0, 1, False, False)
-        carry(x_right[1], N_TILE - P, N_TILE)
+        interleave("V", d_left[2])
         results0(last)
-        carry_out(x_right[1], N_TILE - P, N_TILE)
-        interleave("V", x_right[2], 0, HALF)
-        quantize(d_left[2])
-        quantize(x_left[2])
-        quadrant(0, 2, False, True)
-        interleave("V", x_right[2], HALF, N_TILE)
-        quantize(x_right[0])
+        interleave("S", x_right[1])
         quadrant(1, 0, True, False)
-        interleave("S", x_right[1], N_TILE - P - SCALAR_LAST, N_TILE - P)
-        interleave("V", x_right[1], 0, N_TILE - P - SCALAR_LAST)
-        quantize(x_right[2])
-        quadrant(1, 2, False, False)
+        quantize(x_left[2])
+        quantize(d_left[2])
+        quadrant(0, 2, False, True)
+        interleave("V", x_right[2], 0, HALF)
+        interleave("V", x_right[2], HALF, N_TILE)
+        quantize(x_right[1])
+        quadrant(1, 1, False, False)
         for m in range(ROW_TILES // 2):
             result1("S", m, 0)
             store1(m, 0)
         upper = ROW_TILES // 2
         interleave_rows("V", upper, 0, 1)
-        quantize(x_right[1])
-        quadrant(1, 1, False, True)
+        quantize(x_right[2])
+        quadrant(1, 2, False, True)
         interleave_rows("V", upper, 1, 2)
         interleave_rows("V", upper, 2, 3)
         interleave_rows("S", upper + 1, 2, 3)

@@ -14,12 +14,13 @@ DMA_ALIGN = 256
 RUN = 8
 W_PASSES = 4
 ROW_TILES = D // P
-POOL_COLUMNS = 368
+POOL_COLUMNS = 320
 STAGING = {"V": 3, "S": 2, "G": 1, "dzt": 3}
 CARRIED_W = [0, HALF] + [P] * 5 + [HALF]
 VECTOR_W = [HALF, HALF] + [208] * 5 + [P]
 SCALAR_EARLY = 192
-WINDOWS = [6, 7]
+WINDOWS = [7, 8, 9]
+SIGMOID_FIRST = 6
 
 FLOPS = 2 * B * D * D * 3
 BYTES = 2 * (3 * B * D + 2 * D * D + B) + 4 * B * D + 4 * (B * D + D * D)
@@ -153,6 +154,14 @@ def tile_diffscm_pb_v_kernel(
             blocks = -(-(b - a) // P)
             w = (b - a) // blocks
             take_bank(piece, [P, blocks, PACK * w], BF16)
+            if kind == "d":
+                rows = rows_of(kind, k, lo, hi).rearrange("p t (u w e) -> p u t w e", u=2, e=2)
+                out = banks[piece][:, 0].rearrange("p (w u e t) -> p u t w e", u=2, e=2, t=PACK)
+                for u in range(2):
+                    nc.tensor.matmul(
+                        out[:, u], lhsT=ident_bf[:], rhs=rows[:, u, :, a // 4 : b // 4], start=True, stop=True
+                    )
+                return
             for j in range(blocks):
                 out = banks[piece][:, j].rearrange("p (c t) -> p t c" if stepped else "p (t c) -> p t c", t=PACK)
                 first = lo + a + j * w
@@ -183,9 +192,10 @@ def tile_diffscm_pb_v_kernel(
             for u in range(2):
                 copy(engine, dst[:, u, lo:hi], src[:, k, u, lo:hi, first // 4 : (first + P) // 4])
 
-        def quantize_rows(m):
+        def quantize_rows(m, third_first=False):
             codes, scales = mx_operand(work, GROUPS * P, False, name="r", bufs=3)
-            for lo, hi in ((0, 2 * P), (2 * P, 3 * P)):
+            parts = ((0, 2 * P), (2 * P, 3 * P))
+            for lo, hi in reversed(parts) if third_first else parts:
                 nc.vector.quantize_mx(
                     out=codes[:, lo:hi].bitcast(E5M2), scales=scales[:, lo:hi], in_=grp[m][:, lo * PACK : hi * PACK]
                 )
@@ -199,9 +209,11 @@ def tile_diffscm_pb_v_kernel(
         sorted_out = lambda a: a.rearrange("p (u w e) -> p u w e", u=2, e=2)
 
         def sigmoid(i, half=None):
+            if not half:
+                gate[i] = work.tile([P, D], F32, tag="gate", bufs=2, name="gate")
             for h in range(2) if half is None else (half,):
-                gate[i, h] = work.tile([P, N_TILE], F32, tag="gate", bufs=4, name="gate")
-                nc.scalar.activation(out=sorted_out(gate[i, h][:]), in_=sorted_in(part("v", i)[:, columns(h)]), func=SIGMOID)
+                c = columns(h)
+                nc.scalar.activation(out=sorted_out(gate[i][:, c]), in_=sorted_in(part("v", i)[:, c]), func=SIGMOID)
 
         def move(kind, i):
             bank = take_bank((kind, i), [P, D], BF16)
@@ -211,46 +223,43 @@ def tile_diffscm_pb_v_kernel(
                     lhsT=ident_bf[:], rhs=part(kind, i)[:, columns(half)], start=True, stop=True,
                 )
 
-        def source(kind, i, half):
-            if (kind, i) in banks:
-                return sorted_out(banks[kind, i][:, columns(half)])
-            return sorted_in(part(kind, i)[:, columns(half)])
+        of_sorted = lambda a, u: a.rearrange("p (k u w e) -> p u k w e", k=2, u=2, e=2)[:, u]
+        of_natural = lambda a, u: a.rearrange("p (k w u e) -> p u k w e", k=2, u=2, e=2)[:, u]
 
         def first_product(i, half):
-            values = sorted_out(gate[i, half][:])
-            nc.vector.tensor_tensor(out=values, in0=values, in1=source("e", i, half), op=MULT)
-            if half and ("e", i) in banks:
+            values, moved = gate[i][:, columns(half)], ("e", i) in banks
+            noise = sorted_out(banks["e", i][:, columns(half)]) if moved else sorted_in(part("e", i)[:, columns(half)])
+            nc.vector.tensor_tensor(out=sorted_out(values), in0=sorted_out(values), in1=noise, op=MULT)
+            if half and moved:
                 give_back(("e", i))
 
         def make_dmu(i):
             dmu[i] = work.tile([P, D], BF16, tag="dmu", bufs=2, name="dmu")
             nc.vector.tensor_scalar(
-                out=dmu[i][:].rearrange("p (u w e) -> p u w e", u=2, e=2), in0=sorted_in(part("g", i)),
-                scalar1=t_col[:, i : i + 1], scalar2=None, op0=MULT,
+                out=sorted_out(dmu[i][:]), in0=sorted_in(part("g", i)), scalar1=t_col[:, i : i + 1], scalar2=None, op0=MULT
             )
 
-        def make_dv(i, half):
+        def make_dv(i, a):
             moved = ("g", i) in banks
-            for u in (slice(None),) if moved else range(2):
-                nc.vector.scalar_tensor_tensor(
-                    out=sorted_out(part("e", i)[:, columns(half)])[:, u], in0=source("g", i, half)[:, u],
-                    scalar=t_col[:, i : i + 1], in1=sorted_out(gate[i, half][:])[:, u], op0=MULT, op1=MULT,
-                )
-            if half and moved:
+            cut = (lambda t, a: t[:, columns(a)]) if moved else of_sorted
+            nc.vector.scalar_tensor_tensor(
+                out=cut(part("e", i), a), in0=cut(banks["g", i], a) if moved else of_natural(part("g", i), a),
+                scalar=t_col[:, i : i + 1], in1=cut(gate[i][:], a), op0=MULT, op1=MULT,
+            )
+            if a and moved:
                 give_back(("g", i))
 
         def early_product(i):
             early[i] = work.tile([P, D], F32, tag="S", bufs=STAGING["S"], align_bytes=64, name="early")
-            for half in range(2):
-                for u in range(2):
-                    nc.vector.scalar_tensor_tensor(
-                        out=sorted_out(early[i][:, columns(half)])[:, u], in0=source("g", i, half)[:, u],
-                        scalar=t_col[:, i : i + 1], in1=source("e", i, half)[:, u], op0=MULT, op1=MULT,
-                    )
+            for u in range(2):
+                nc.vector.scalar_tensor_tensor(
+                    out=of_sorted(early[i][:], u), in0=of_natural(part("g", i), u), scalar=t_col[:, i : i + 1],
+                    in1=of_natural(part("e", i), u), op0=MULT, op1=MULT,
+                )
 
         def early_dv(i, half):
             c = columns(half)
-            nc.vector.tensor_tensor(out=part("e", i)[:, c], in0=early[i][:, c], in1=gate[i, half][:], op=MULT)
+            nc.vector.tensor_tensor(out=part("e", i)[:, c], in0=early[i][:, c], in1=gate[i][:, c], op=MULT)
 
         def products(i):
             for make in (first_product, make_dv):
@@ -260,13 +269,10 @@ def tile_diffscm_pb_v_kernel(
         def turn(i, head):
             bank = take_bank((i, head), [P, 2, 2, P])
             words = (part("e", i) if head else dmu[i][:]).bitcast(F32)
-            for k in range(2):
-                for u in range(2):
-                    if head:
-                        block = words[:, 256 * k + P * u : 256 * k + P * (u + 1)]
-                    else:
-                        block = words[:, 256 * u + P * k : 256 * u + P * (k + 1)]
-                    nc.tensor.transpose(bank[:, k, u, :], block, ident[:])
+            blocks = [(k, u) for k in range(2) for u in range(2)]
+            for k, u in blocks if i in early or i in WINDOWS else sorted(blocks, key=lambda b: b[1]):
+                first = 256 * k + P * u if head else 256 * u + P * k
+                nc.tensor.transpose(bank[:, k, u, :], words[:, first : first + P], ident[:])
 
         def turn_out(i, head, engine="S"):
             if not head:
@@ -425,8 +431,8 @@ def tile_diffscm_pb_v_kernel(
             if q > 1:
                 head_passes(q - 2)
 
-        load("v", 4, 1)
         load("g", 4, 2)
+        load("v", 4, 1)
         load("e", 4, 2)
         load("v", 5, 1)
         load_slices(6, 2)
@@ -449,96 +455,116 @@ def tile_diffscm_pb_v_kernel(
         d_left = [("d", g, 0, N_TILE) for g in range(GROUPS)]
         x_left = [("x", g, 0, N_TILE) for g in range(GROUPS)]
         x_right = [("x", g, N_TILE, D) for g in range(GROUPS)]
-        windows = dict(zip(WINDOWS, (x_left[0], x_right[0], x_left[1], x_right[1])))
-        shares = {5: (d_left[0], 0, 320)}
+        windows = dict(zip(WINDOWS, (("x", 0, 0, 384), ("x", 0, 384, 768), ("x", 0, 768, D))))
+        vector_extra = {5: [(d_left[0], 0, 128)], 6: [(d_left[0], 128, 304)], 10: [(d_left[0], 304, 432), (d_left[1], 0, 64)], 11: [(d_left[1], 64, 256)]}
+        vector_quant = {}
+        scalar_extra = {7: [(d_left[0], 432, 512)], 8: [(d_left[1], 256, 384)], 9: [(d_left[1], 384, 512)], 11: [(x_left[2], 0, HALF)]}
+        carried = {}
         for i in range(2, SLICES):
-            if i in windows:
-                interleave("G", windows[i], 0, POOL_COLUMNS)
-                products(i)
+            window, chained = windows.get(i), i in windows and i + 1 in windows
+            if window:
+                width = window[3] - window[2]
+                interleave("G", window, 0, min(width, POOL_COLUMNS))
+            if i > 2:
+                first_product(i, 0)
+                first_product(i, 1)
+            if chained:
+                move("e", i + 1)
+                products0(i - 1, 0)
+            if i < last and not window:
                 make_dmu(i + 1)
-            else:
-                if i > 2:
-                    first_product(i, 0)
-                    first_product(i, 1)
-                if i < last:
-                    make_dmu(i + 1)
-                for half in range(2):
-                    (make_dv if i > 2 else early_dv)(i, half)
-            if i + 1 in windows and i not in windows:
-                interleave("V", *shares[i])
+            for share in () if window else vector_extra.get(i, ()):
+                interleave("V", *share)
+            for half in range(2):
+                (make_dv if i > 2 else early_dv)(i, half)
+            if window:
+                make_dmu(i + 1)
+            if i + 1 in windows and not window:
                 quantize_dz(i, 0)
                 quantize_dz(i - 1, 1)
+                move("e", i + 1)
             else:
                 if i > 2:
                     quantize_dz(i - 1, 1)
-                if i in windows:
-                    interleave("V", windows[i], POOL_COLUMNS, N_TILE)
+                if window and width > POOL_COLUMNS:
+                    interleave("V", window, POOL_COLUMNS, width)
                 quantize_dz(i, 0)
-                if i in windows:
-                    quantize(windows[i])
+                for piece in vector_quant.get(i, ()):
+                    quantize(piece)
+                if window:
+                    quantize(window)
             if i + 1 in windows:
-                move("e", i + 1)
                 move("g", i + 1)
-            for s, head in ((i, 1), (i + 1, 0)) if i in windows else ((i + 1, 0), (i, 1)):
+            for s, head in ((i, 1), (i + 1, 0)) if window else ((i + 1, 0), (i, 1)):
                 if s < SLICES:
                     turn(s, head)
             if i > 2:
                 products0(i - 1, 1)
-            products0(i, 0)
+            if not (i + 1 in windows and i + 2 in windows):
+                products0(i, 0)
+            if i in carried:
+                carry(*carried[i])
             if i == last:
-                interleave("S", x_left[2], 0, HALF)
+                for share in scalar_extra.get(i, ()):
+                    interleave("S", *share)
+            if i + 2 < SLICES and i >= SIGMOID_FIRST:
+                sigmoid(i + 2)
             turn_out(i, 1)
             if i < last:
                 turn_out(i + 1, 0)
-            if i + 2 < SLICES:
+            if i < SIGMOID_FIRST:
                 sigmoid(i + 2)
             if i < last:
                 results0(i - 1)
-            if i in windows and i - 1 in windows:
-                interleave("S", d_left[0], 320, N_TILE)
+                for share in scalar_extra.get(i, ()):
+                    interleave("S", *share)
+            if i in carried:
+                carry_out(*carried[i])
 
+        upper = ROW_TILES // 2
         quantize(d_left[0])
         quadrant(0, 0, True, False)
-        interleave("V", d_left[1])
+        interleave("V", x_left[1])
+        quantize(d_left[1])
         quantize_dz(last, 1)
         products0(last, 1)
         interleave("S", x_left[2], HALF, N_TILE)
         results0(last - 1)
-        interleave("V", x_left[1])
-        quantize(d_left[1])
         quantize(x_left[1])
         quadrant(0, 1, False, False)
         interleave("V", d_left[2])
         results0(last)
-        interleave("S", x_right[1])
         quadrant(1, 0, True, False)
+        interleave("S", x_right[1], 0, 288)
         quantize(x_left[2])
         quantize(d_left[2])
         quadrant(0, 2, False, True)
+        interleave("V", x_right[1], 288, N_TILE)
         interleave("V", x_right[2], 0, HALF)
-        interleave("V", x_right[2], HALF, N_TILE)
         quantize(x_right[1])
         quadrant(1, 1, False, False)
-        for m in range(ROW_TILES // 2):
+        interleave("S", x_right[2], N_TILE - 96, N_TILE)
+        interleave("V", x_right[2], HALF, N_TILE - 96)
+        for m in range(upper):
             result1("S", m, 0)
             store1(m, 0)
-        upper = ROW_TILES // 2
         interleave_rows("V", upper, 0, 1)
         quantize(x_right[2])
         quadrant(1, 2, False, True)
         interleave_rows("V", upper, 1, 2)
         interleave_rows("V", upper, 2, 3)
         interleave_rows("S", upper + 1, 2, 3)
-        for m in range(ROW_TILES // 2):
+        for m in range(upper):
             result1("S", m, 1)
             store1(m, 1)
+
 
         for m in range(upper, ROW_TILES):
             if m > upper:
                 interleave_rows("V", m, 0, 2)
             if m > upper + 1:
                 interleave_rows("V", m, 2, 3)
-            quantize_rows(m)
+            quantize_rows(m, m == upper + 1)
             row_tile(m)
 
         for m in (upper, upper + 1):

@@ -14,12 +14,12 @@ DMA_ALIGN = 256
 RUN = 8
 W_PASSES = 4
 ROW_TILES = D // P
-POOL_COLUMNS = 320
+POOL_COLUMNS = 304
 STAGING = {"V": 3, "S": 2, "G": 1, "dzt": 3}
 CARRIED_W = [0, HALF] + [P] * 5 + [HALF]
 VECTOR_W = [HALF, HALF] + [208] * 5 + [P]
 SCALAR_EARLY = 192
-WINDOWS = [7, 8, 9]
+WINDOWS = [7, 8]
 SIGMOID_FIRST = 6
 
 FLOPS = 2 * B * D * D * 3
@@ -455,10 +455,10 @@ def tile_diffscm_pb_v_kernel(
         d_left = [("d", g, 0, N_TILE) for g in range(GROUPS)]
         x_left = [("x", g, 0, N_TILE) for g in range(GROUPS)]
         x_right = [("x", g, N_TILE, D) for g in range(GROUPS)]
-        windows = dict(zip(WINDOWS, (("x", 0, 0, 384), ("x", 0, 384, 768), ("x", 0, 768, D))))
-        vector_extra = {5: [(d_left[0], 0, 128)], 6: [(d_left[0], 128, 304)], 10: [(d_left[0], 304, 432), (d_left[1], 0, 64)], 11: [(d_left[1], 64, 256)]}
+        windows = dict(zip(WINDOWS, (("x", 0, 0, 384), ("x", 0, 384, 768))))
+        vector_extra = {5: [(d_left[0], 0, 128)], 6: [(d_left[0], 128, 304)], 9: [(d_left[1], 384, 512)], 10: [(d_left[0], 304, 432), (d_left[1], 0, 64)], 11: [(d_left[1], 64, 256)]}
         vector_quant = {}
-        scalar_extra = {7: [(d_left[0], 432, 512)], 8: [(d_left[1], 256, 384)], 9: [(d_left[1], 384, 512)], 11: [(x_left[2], 0, HALF)]}
+        scalar_extra = {7: [(d_left[0], 432, 512)], 8: [(d_left[1], 256, 384)], 9: [(("x", 0, 768, D), 0, 192, "G")], 11: [(x_left[2], 0, HALF)]}
         carried = {}
         for i in range(2, SLICES):
             window, chained = windows.get(i), i in windows and i + 1 in windows
@@ -488,6 +488,8 @@ def tile_diffscm_pb_v_kernel(
                     quantize_dz(i - 1, 1)
                 if window and width > POOL_COLUMNS:
                     interleave("V", window, POOL_COLUMNS, width)
+                for share in vector_extra.get(i, ()) if window else ():
+                    interleave("V", *share)
                 quantize_dz(i, 0)
                 for piece in vector_quant.get(i, ()):
                     quantize(piece)
@@ -533,18 +535,20 @@ def tile_diffscm_pb_v_kernel(
         quantize(x_left[1])
         quadrant(0, 1, False, False)
         interleave("V", d_left[2])
+        interleave("S", ("x", 0, 768, D), 192, HALF)
         results0(last)
-        quadrant(1, 0, True, False)
-        interleave("S", x_right[1], 0, 288)
+        interleave("S", x_right[1], 0, 256)
         quantize(x_left[2])
         quantize(d_left[2])
         quadrant(0, 2, False, True)
-        interleave("V", x_right[1], 288, N_TILE)
+        quantize(("x", 0, 768, D))
+        quadrant(1, 0, True, False)
+        interleave("V", x_right[1], 256, N_TILE)
         interleave("V", x_right[2], 0, HALF)
         quantize(x_right[1])
         quadrant(1, 1, False, False)
-        interleave("S", x_right[2], N_TILE - 96, N_TILE)
-        interleave("V", x_right[2], HALF, N_TILE - 96)
+        interleave("S", x_right[2], N_TILE - 64, N_TILE)
+        interleave("V", x_right[2], HALF, N_TILE - 64)
         for m in range(upper):
             result1("S", m, 0)
             store1(m, 0)

@@ -139,9 +139,10 @@ def tile_diffscm_pb_v_kernel(
                     scalar1=1.0, scalar2=0.0, op0=MULT, op1=ADD,
                 )
             elif kind == "d":
-                rows = rows_of(kind, k, lo, hi).rearrange("p t (u w e) -> p u w t e", u=2, e=2)
+                rows = rows_of(kind, k, lo, hi).rearrange("p t (u c w e) -> p u c t w e", u=2, w=RUN // 2, e=2)
+                out = dst.rearrange("p (c w u e t) -> p u c t w e", w=RUN // 2, u=2, e=2, t=PACK)
                 for u in range(2):
-                    copy(engine, dst.rearrange("p (w u e t) -> p u w t e", u=2, e=2, t=PACK)[:, u], rows[:, u, a // 4 : b // 4])
+                    copy(engine, out[:, u], rows[:, u, a // (2 * RUN) : b // (2 * RUN)])
             else:
                 copy(
                     engine,
@@ -358,9 +359,21 @@ def tile_diffscm_pb_v_kernel(
                 pass1(m, n, g, first, final)
 
         def row_tile(m):
-            for n in range(2):
+            for n in range(2 if m < ROW_TILES - 1 else 1):
                 for g in range(GROUPS):
                     pass1(m, n, g, g == 0, g == GROUPS - 1)
+
+        def last_half(a):
+            bank = take_bank(("last", a), [P, HALF])
+            for g in range(GROUPS):
+                codes, scales = dv_mx[g, ROW_TILES - 1]
+                cols = slice(g * D + N_TILE + a * HALF, g * D + N_TILE + (a + 1) * HALF)
+                nc.tensor.matmul_mx(
+                    out=bank[:],
+                    lhsT=codes.bitcast(E5M2), lhsT_scale=scales,
+                    rhs=x_codes[:, cols].bitcast(E4M3), rhs_scale=x_scales[:, cols],
+                    start=(g == 0), stop=(g == GROUPS - 1),
+                )
 
         nc.scalar.dma_start(
             out=t_col[:].rearrange("p (g j) -> p g j", j=PACK),
@@ -456,9 +469,9 @@ def tile_diffscm_pb_v_kernel(
         x_left = [("x", g, 0, N_TILE) for g in range(GROUPS)]
         x_right = [("x", g, N_TILE, D) for g in range(GROUPS)]
         windows = dict(zip(WINDOWS, (("x", 0, 0, 384), ("x", 0, 384, 768))))
-        vector_extra = {5: [(d_left[0], 0, 128)], 6: [(d_left[0], 128, 304)], 9: [(d_left[1], 384, 512)], 10: [(d_left[0], 304, 432), (d_left[1], 0, 64)], 11: [(d_left[1], 64, 256)]}
+        vector_extra = {5: [(d_left[0], 0, 128)], 6: [(d_left[0], 128, 288)], 9: [(d_left[1], 384, 512)], 10: [(d_left[0], 288, 416), (d_left[1], 0, 64)], 11: [(d_left[1], 64, 256)]}
         vector_quant = {}
-        scalar_extra = {7: [(d_left[0], 432, 512)], 8: [(d_left[1], 256, 384)], 9: [(("x", 0, 768, D), 0, 192, "G")], 11: [(x_left[2], 0, HALF)]}
+        scalar_extra = {7: [(d_left[0], 416, 512)], 8: [(d_left[1], 256, 384)], 9: [(("x", 0, 768, D), 0, 192, "G")], 11: [(x_left[2], 0, HALF)]}
         carried = {}
         for i in range(2, SLICES):
             window, chained = windows.get(i), i in windows and i + 1 in windows
@@ -575,9 +588,11 @@ def tile_diffscm_pb_v_kernel(
             for n in range(2):
                 result1("S", m, n)
             store1(m, 0, 0, D)
+        for a in range(2):
+            last_half(a)
         for engine, m, n in (("S", upper + 2, 0), ("V", upper + 2, 1), ("S", upper + 3, 0)):
             result1(engine, m, n)
             store1(m, n)
-        for lo in (0, HALF):
-            result1("V", upper + 3, 1, lo, lo + HALF)
-            store1(upper + 3, 1, lo, lo + HALF)
+        for a in range(2):
+            copy("V", result_of(upper + 3, 1)[:, a * HALF : (a + 1) * HALF], banks["last", a][:])
+            store1(upper + 3, 1, a * HALF, (a + 1) * HALF)

@@ -220,18 +220,18 @@ def tile_diffscm_pb_v_kernel(
             bank = take_bank((kind, i), [P, D], BF16)
             for half in range(2):
                 nc.tensor.matmul(
-                    bank[:, columns(half)].rearrange("p (u w e) -> p w u e", u=2, e=2),
-                    lhsT=ident_bf[:], rhs=part(kind, i)[:, columns(half)], start=True, stop=True,
+                    bank[:, columns(half)], lhsT=ident_bf[:], rhs=part(kind, i)[:, columns(half)], start=True, stop=True
                 )
 
         of_sorted = lambda a, u: a.rearrange("p (k u w e) -> p u k w e", k=2, u=2, e=2)[:, u]
         of_natural = lambda a, u: a.rearrange("p (k w u e) -> p u k w e", k=2, u=2, e=2)[:, u]
 
-        def first_product(i, half):
-            values, moved = gate[i][:, columns(half)], ("e", i) in banks
-            noise = sorted_out(banks["e", i][:, columns(half)]) if moved else sorted_in(part("e", i)[:, columns(half)])
-            nc.vector.tensor_tensor(out=sorted_out(values), in0=sorted_out(values), in1=noise, op=MULT)
-            if half and moved:
+        def first_product(i, a):
+            moved = ("e", i) in banks
+            values = of_sorted(gate[i][:], a) if moved else sorted_out(gate[i][:, columns(a)])
+            noise = of_natural(banks["e", i][:], a) if moved else sorted_in(part("e", i)[:, columns(a)])
+            nc.vector.tensor_tensor(out=values, in0=values, in1=noise, op=MULT)
+            if a and moved:
                 give_back(("e", i))
 
         def make_dmu(i):
@@ -240,14 +240,13 @@ def tile_diffscm_pb_v_kernel(
                 out=sorted_out(dmu[i][:]), in0=sorted_in(part("g", i)), scalar1=t_col[:, i : i + 1], scalar2=None, op0=MULT
             )
 
-        def make_dv(i, a):
+        def make_dv(i, u):
             moved = ("g", i) in banks
-            cut = (lambda t, a: t[:, columns(a)]) if moved else of_sorted
             nc.vector.scalar_tensor_tensor(
-                out=cut(part("e", i), a), in0=cut(banks["g", i], a) if moved else of_natural(part("g", i), a),
-                scalar=t_col[:, i : i + 1], in1=cut(gate[i][:], a), op0=MULT, op1=MULT,
+                out=of_sorted(part("e", i), u), in0=of_natural(banks["g", i][:] if moved else part("g", i), u),
+                scalar=t_col[:, i : i + 1], in1=of_sorted(gate[i][:], u), op0=MULT, op1=MULT,
             )
-            if a and moved:
+            if u and moved:
                 give_back(("g", i))
 
         def early_product(i):
@@ -271,7 +270,7 @@ def tile_diffscm_pb_v_kernel(
             bank = take_bank((i, head), [P, 2, 2, P])
             words = (part("e", i) if head else dmu[i][:]).bitcast(F32)
             blocks = [(k, u) for k in range(2) for u in range(2)]
-            for k, u in blocks if i in early or i in WINDOWS else sorted(blocks, key=lambda b: b[1]):
+            for k, u in blocks if i in early else sorted(blocks, key=lambda b: b[1]):
                 first = 256 * k + P * u if head else 256 * u + P * k
                 nc.tensor.transpose(bank[:, k, u, :], words[:, first : first + P], ident[:])
 

@@ -14,14 +14,14 @@ DMA_ALIGN = 256
 RUN = 8
 W_PASSES = 4
 ROW_TILES = D // P
+EARLY = 3
+WINDOW = 7
+WINDOW_PIECE = 384
 POOL_COLUMNS = 304
-STAGING = {"V": 3, "S": 2, "G": 1, "dzt": 3}
+STAGING = {"V": 3, "S": 2, "dzt": 3, "G": 1}
 CARRIED_W = [0, HALF] + [P] * 5 + [HALF]
 VECTOR_W = [HALF, HALF] + [208] * 5 + [P]
-SCALAR_EARLY = 192
-WINDOWS = [7, 8]
-SIGMOID_FIRST = 6
-
+SCALAR_LAST = 64
 FLOPS = 2 * B * D * D * 3
 BYTES = 2 * (3 * B * D + 2 * D * D + B) + 4 * B * D + 4 * (B * D + D * D)
 
@@ -120,17 +120,15 @@ def tile_diffscm_pb_v_kernel(
             else:
                 nc.scalar.copy(out=out, in_=in_)
 
-        gate, early = {}, {}
-        grp, dmu, dzt, dz, dv_mx, res = {}, {}, {}, {}, {}, {}
+        grp, gate, early, dmu, dzt, dz, dv_mx, res = {}, {}, {}, {}, {}, {}, {}, {}
 
         def staging(key, width, tag):
             if key not in grp:
                 grp[key] = work.tile([P, width * PACK], BF16, tag=tag, bufs=STAGING[tag], align_bytes=64, name=tag)
             return grp[key]
 
-        def interleave(engine, piece, a=None, b=None, tag=None):
+        def interleave(engine, piece, a=0, b=N_TILE, tag=None):
             kind, k, lo, hi = piece
-            a, b = a or 0, b or hi - lo
             dst = staging(piece, hi - lo, tag or engine)[:, a * PACK : b * PACK]
             src = rows_of(kind, k, lo + a, lo + b)
             if engine == "G":
@@ -155,14 +153,6 @@ def tile_diffscm_pb_v_kernel(
             blocks = -(-(b - a) // P)
             w = (b - a) // blocks
             take_bank(piece, [P, blocks, PACK * w], BF16)
-            if kind == "d":
-                rows = rows_of(kind, k, lo, hi).rearrange("p t (u w e) -> p u t w e", u=2, e=2)
-                out = banks[piece][:, 0].rearrange("p (w u e t) -> p u t w e", u=2, e=2, t=PACK)
-                for u in range(2):
-                    nc.tensor.matmul(
-                        out[:, u], lhsT=ident_bf[:], rhs=rows[:, u, :, a // 4 : b // 4], start=True, stop=True
-                    )
-                return
             for j in range(blocks):
                 out = banks[piece][:, j].rearrange("p (c t) -> p t c" if stepped else "p (t c) -> p t c", t=PACK)
                 first = lo + a + j * w
@@ -204,7 +194,7 @@ def tile_diffscm_pb_v_kernel(
                 dv_mx[g, m] = (codes[:, g * P : (g + 1) * P], scales[:, g * P : (g + 1) * P])
 
         def columns(half):
-            return slice(0, D) if half is None else slice(half * N_TILE, (half + 1) * N_TILE)
+            return slice(half * N_TILE, (half + 1) * N_TILE)
 
         sorted_in = lambda a: a.rearrange("p (w u e) -> p u w e", u=2, e=2)
         sorted_out = lambda a: a.rearrange("p (u w e) -> p u w e", u=2, e=2)
@@ -237,7 +227,8 @@ def tile_diffscm_pb_v_kernel(
         def make_dmu(i):
             dmu[i] = work.tile([P, D], BF16, tag="dmu", bufs=2, name="dmu")
             nc.vector.tensor_scalar(
-                out=sorted_out(dmu[i][:]), in0=sorted_in(part("g", i)), scalar1=t_col[:, i : i + 1], scalar2=None, op0=MULT
+                out=sorted_out(dmu[i][:]), in0=sorted_in(part("g", i)),
+                scalar1=t_col[:, i : i + 1], scalar2=None, op0=MULT,
             )
 
         def make_dv(i, u):
@@ -261,37 +252,34 @@ def tile_diffscm_pb_v_kernel(
             c = columns(half)
             nc.vector.tensor_tensor(out=part("e", i)[:, c], in0=early[i][:, c], in1=gate[i][:, c], op=MULT)
 
-        def products(i):
-            for make in (first_product, make_dv):
-                for half in range(2):
-                    make(i, half)
-
         def turn(i, head):
             bank = take_bank((i, head), [P, 2, 2, P])
             words = (part("e", i) if head else dmu[i][:]).bitcast(F32)
             blocks = [(k, u) for k in range(2) for u in range(2)]
-            for k, u in blocks if i in early else sorted(blocks, key=lambda b: b[1]):
+            for k, u in blocks if i < EARLY else sorted(blocks, key=lambda b: b[1]):
                 first = 256 * k + P * u if head else 256 * u + P * k
                 nc.tensor.transpose(bank[:, k, u, :], words[:, first : first + P], ident[:])
 
-        def turn_out(i, head, engine="S"):
+        def turn_out(i, head):
             if not head:
-                tag = "G" if i + 2 in WINDOWS and i + 1 not in WINDOWS else "dzt"
+                tag = "G" if i == WINDOW - 2 else "dzt"
                 dzt[i] = work.tile([P, 2 * D], BF16, tag=tag, bufs=STAGING[tag], align_bytes=64, name=tag)
             dst = dzt[i][:, head * D : (head + 1) * D].bitcast(F32)
-            copy(engine, dst.rearrange("p (k c u) -> p k c u", k=2, u=2), banks[i, head][:].rearrange("p k u c -> p k c u"))
+            nc.scalar.copy(
+                out=dst.rearrange("p (k c u) -> p k c u", k=2, u=2),
+                in_=banks[i, head][:].rearrange("p k u c -> p k c u"),
+            )
             give_back((i, head))
 
-        def quantize_dz(i, head=None):
-            if i not in dz:
+        def quantize_dz(i, head):
+            if not head:
                 dz[i] = mx_operand(work, W_PASSES * P, False, name="z", bufs=3)
-            lo, hi = (0, 2) if head is None else (head, head + 1)
-            c = slice(lo * 2 * P, hi * 2 * P)
+            c = slice(head * 2 * P, (head + 1) * 2 * P)
             nc.vector.quantize_mx(
-                out=dz[i][0][:, c].bitcast(E5M2), scales=dz[i][1][:, c], in_=dzt[i][:, lo * D : hi * D]
+                out=dz[i][0][:, c].bitcast(E5M2), scales=dz[i][1][:, c], in_=dzt[i][:, head * D : (head + 1) * D]
             )
 
-        def product0(i, n, passes=range(W_PASSES)):
+        def product0(i, n, passes):
             if passes[0] == 0:
                 take_bank(("out_0", i, n), [P, N_TILE])
             codes, scales = dz[i]
@@ -336,10 +324,9 @@ def tile_diffscm_pb_v_kernel(
                 res[four] = big_tile([P, 4 * N_TILE], F32)
             return res[four][:, place * N_TILE :]
 
-        def result1(engine, m, n, lo=0, hi=N_TILE):
-            copy(engine, result_of(m, n)[:, lo:hi], banks["out_1", m, n][:, lo:hi])
-            if lo == 0:
-                give_back(("out_1", m, n))
+        def result1(engine, m, n):
+            copy(engine, result_of(m, n)[:, :N_TILE], banks["out_1", m, n][:])
+            give_back(("out_1", m, n))
 
         def store1(m, n, lo=0, hi=N_TILE):
             nc.sync.dma_start(out=out1_v[m][:, n * N_TILE + lo : n * N_TILE + hi], in_=result_of(m, n)[:, lo:hi])
@@ -467,44 +454,38 @@ def tile_diffscm_pb_v_kernel(
         d_left = [("d", g, 0, N_TILE) for g in range(GROUPS)]
         x_left = [("x", g, 0, N_TILE) for g in range(GROUPS)]
         x_right = [("x", g, N_TILE, D) for g in range(GROUPS)]
-        windows = dict(zip(WINDOWS, (("x", 0, 0, 384), ("x", 0, 384, 768))))
-        vector_extra = {5: [(d_left[0], 0, 128)], 6: [(d_left[0], 128, 288)], 9: [(d_left[1], 384, 512)], 10: [(d_left[0], 288, 416), (d_left[1], 0, 64)], 11: [(d_left[1], 64, 256)]}
-        vector_quant = {}
-        scalar_extra = {7: [(d_left[0], 416, 512)], 8: [(d_left[1], 256, 384)], 9: [(("x", 0, 768, D), 0, 192, "G")], 11: [(x_left[2], 0, HALF)]}
-        carried = {}
+        windows = {WINDOW + a: ("x", 0, a * WINDOW_PIECE, (a + 1) * WINDOW_PIECE) for a in range(2)}
+        x_rest = ("x", 0, 2 * WINDOW_PIECE, D)
+        begins = (PACK, WINDOW + 2)
         for i in range(2, SLICES):
-            window, chained = windows.get(i), i in windows and i + 1 in windows
+            window = windows.get(i)
             if window:
-                width = window[3] - window[2]
-                interleave("G", window, 0, min(width, POOL_COLUMNS))
-            if i > 2:
+                interleave("G", window, 0, POOL_COLUMNS)
+            if i >= EARLY:
                 first_product(i, 0)
                 first_product(i, 1)
-            if chained:
+            if i == WINDOW:
                 move("e", i + 1)
                 products0(i - 1, 0)
             if i < last and not window:
                 make_dmu(i + 1)
-            for share in () if window else vector_extra.get(i, ()):
-                interleave("V", *share)
-            for half in range(2):
-                (make_dv if i > 2 else early_dv)(i, half)
+            for g, first in enumerate(begins):
+                if 0 <= i - first < 3:
+                    interleave("V", d_left[g], (i - first) * P, (i - first + 1) * P)
+            for a in range(2):
+                (make_dv if i >= EARLY else early_dv)(i, a)
             if window:
                 make_dmu(i + 1)
-            if i + 1 in windows and not window:
+            if i == WINDOW - 1:
                 quantize_dz(i, 0)
                 quantize_dz(i - 1, 1)
                 move("e", i + 1)
             else:
                 if i > 2:
                     quantize_dz(i - 1, 1)
-                if window and width > POOL_COLUMNS:
-                    interleave("V", window, POOL_COLUMNS, width)
-                for share in vector_extra.get(i, ()) if window else ():
-                    interleave("V", *share)
+                if window:
+                    interleave("V", window, POOL_COLUMNS, WINDOW_PIECE)
                 quantize_dz(i, 0)
-                for piece in vector_quant.get(i, ()):
-                    quantize(piece)
                 if window:
                     quantize(window)
             if i + 1 in windows:
@@ -514,26 +495,24 @@ def tile_diffscm_pb_v_kernel(
                     turn(s, head)
             if i > 2:
                 products0(i - 1, 1)
-            if not (i + 1 in windows and i + 2 in windows):
+            if i != WINDOW - 1:
                 products0(i, 0)
-            if i in carried:
-                carry(*carried[i])
             if i == last:
-                for share in scalar_extra.get(i, ()):
-                    interleave("S", *share)
-            if i + 2 < SLICES and i >= SIGMOID_FIRST:
+                interleave("S", x_left[2], 0, HALF)
+            behind = i >= WINDOW - 1
+            if behind and i + 2 < SLICES:
                 sigmoid(i + 2)
             turn_out(i, 1)
             if i < last:
                 turn_out(i + 1, 0)
-            if i < SIGMOID_FIRST:
+            if not behind:
                 sigmoid(i + 2)
             if i < last:
                 results0(i - 1)
-                for share in scalar_extra.get(i, ()):
-                    interleave("S", *share)
-            if i in carried:
-                carry_out(*carried[i])
+            if window:
+                interleave("S", d_left[i - WINDOW], N_TILE - P, N_TILE)
+            if i - 1 in windows and not window:
+                interleave("S", x_rest, 0, P, "G")
 
         upper = ROW_TILES // 2
         quantize(d_left[0])
@@ -547,20 +526,20 @@ def tile_diffscm_pb_v_kernel(
         quantize(x_left[1])
         quadrant(0, 1, False, False)
         interleave("V", d_left[2])
-        interleave("S", ("x", 0, 768, D), 192, HALF)
+        interleave("S", x_rest, P, 2 * P)
         results0(last)
-        interleave("S", x_right[1], 0, 256)
+        interleave("S", x_right[1], 0, HALF)
         quantize(x_left[2])
         quantize(d_left[2])
         quadrant(0, 2, False, True)
-        quantize(("x", 0, 768, D))
+        quantize(x_rest)
         quadrant(1, 0, True, False)
-        interleave("V", x_right[1], 256, N_TILE)
+        interleave("V", x_right[1], HALF, N_TILE)
         interleave("V", x_right[2], 0, HALF)
         quantize(x_right[1])
         quadrant(1, 1, False, False)
-        interleave("S", x_right[2], N_TILE - 64, N_TILE)
-        interleave("V", x_right[2], HALF, N_TILE - 64)
+        interleave("S", x_right[2], N_TILE - SCALAR_LAST, N_TILE)
+        interleave("V", x_right[2], HALF, N_TILE - SCALAR_LAST)
         for m in range(upper):
             result1("S", m, 0)
             store1(m, 0)
@@ -574,13 +553,12 @@ def tile_diffscm_pb_v_kernel(
             result1("S", m, 1)
             store1(m, 1)
 
-
         for m in range(upper, ROW_TILES):
             if m > upper:
                 interleave_rows("V", m, 0, 2)
             if m > upper + 1:
                 interleave_rows("V", m, 2, 3)
-            quantize_rows(m, m == upper + 1)
+            quantize_rows(m, third_first=m == upper + 1)
             row_tile(m)
 
         for m in (upper, upper + 1):

@@ -14,6 +14,7 @@ DMA_ALIGN = 256
 RUN = 8
 W_PASSES = 4
 ROW_TILES = D // P
+SCALAR_LAST = 64
 EARLY = 3
 WINDOW = 7
 WINDOW_PIECE = 384
@@ -21,7 +22,6 @@ POOL_COLUMNS = 304
 STAGING = {"V": 3, "S": 2, "dzt": 3, "G": 1}
 CARRIED_W = [0, HALF] + [P] * 5 + [HALF]
 VECTOR_W = [HALF, HALF] + [208] * 5 + [P]
-SCALAR_LAST = 64
 FLOPS = 2 * B * D * D * 3
 BYTES = 2 * (3 * B * D + 2 * D * D + B) + 4 * B * D + 4 * (B * D + D * D)
 
@@ -493,9 +493,13 @@ def tile_diffscm_pb_v_kernel(
             for s, head in ((i, 1), (i + 1, 0)) if window else ((i + 1, 0), (i, 1)):
                 if s < SLICES:
                     turn(s, head)
+                if i == 3 and not head:
+                    product0(2, 1, (0, 1))
             if i > 2:
                 products0(i - 1, 1)
-            if i != WINDOW - 1:
+            if i == 2:
+                product0(2, 0, (0, 1))
+            elif i != WINDOW - 1:
                 products0(i, 0)
             if i == last:
                 interleave("S", x_left[2], 0, HALF)

@@ -14,7 +14,6 @@ DMA_ALIGN = 256
 RUN = 8
 W_PASSES = 4
 ROW_TILES = D // P
-SCALAR_LAST = 64
 EARLY = 3
 WINDOW = 7
 WINDOW_PIECE = 384
@@ -542,8 +541,8 @@ def tile_diffscm_pb_v_kernel(
         interleave("V", x_right[2], 0, HALF)
         quantize(x_right[1])
         quadrant(1, 1, False, False)
-        interleave("S", x_right[2], N_TILE - SCALAR_LAST, N_TILE)
-        interleave("V", x_right[2], HALF, N_TILE - SCALAR_LAST)
+        interleave("S", x_right[2], N_TILE - P, N_TILE)
+        interleave("V", x_right[2], HALF, N_TILE - P)
         for m in range(upper):
             result1("S", m, 0)
             store1(m, 0)

from contextlib import ExitStack

import concourse.mybir as mybir
from concourse.masks import make_identity

B, D = 1536, 1024
P = 128
PACK = 4
GROUPS = B // (P * PACK)
SLICES = GROUPS * PACK
N_TILE = 512
HALF = N_TILE // 2
DMA_ALIGN = 256
RUN = 8
W_PASSES = 4
ROW_TILES = D // P
EARLY = 3
WINDOW = 7
WINDOW_PIECE = 384
POOL_COLUMNS = 304
STAGING = {"V": 3, "S": 2, "dzt": 3, "G": 1}
CARRIED_W = [0, HALF] + [P] * 5 + [HALF]
VECTOR_W = [HALF, HALF] + [208] * 5 + [P]
FLOPS = 2 * B * D * D * 3
BYTES = 2 * (3 * B * D + 2 * D * D + B) + 4 * B * D + 4 * (B * D + D * D)

F32 = mybir.dt.float32
BF16 = mybir.dt.bfloat16
U32 = mybir.dt.uint32
U8 = mybir.dt.uint8
E4M3 = mybir.dt.float8_e4m3fn_x4
E5M2 = mybir.dt.float8_e5m2_x4
MULT = mybir.AluOpType.mult
ADD = mybir.AluOpType.add
SIGMOID = mybir.ActivationFunctionType.Sigmoid


def tile_diffscm_pb_v_kernel(
    tc, xt, eps, x, t_rand, Wm, bm, Wv, bv, v, grad_out, out_0, out_1
):
    nc = tc.nc
    by_group = lambda a: a.rearrange("(g p j) w -> g p (j w)", p=P, j=PACK)
    hbm = {"x": by_group(xt), "e": by_group(eps), "v": by_group(v), "g": by_group(grad_out)}
    w_hbm = [by_group(w)[k] for w in (Wm, Wv) for k in range(2)]
    out0_v = by_group(out_0)
    out1_v = out_1.rearrange("(m p) w -> m p w", p=P)

    with ExitStack() as ctx:
        const = ctx.enter_context(tc.tile_pool(name="const", bufs=1))
        inp = ctx.enter_context(tc.tile_pool(name="inp", bufs=1))
        keep = ctx.enter_context(tc.tile_pool(name="keep", bufs=1))
        work = ctx.enter_context(tc.tile_pool(name="work", bufs=1))
        psum = ctx.enter_context(tc.psum_pool(name="psum", bufs=1))
        ctx.enter_context(tc.manual_schedule())

        t_col = const.tile([P, SLICES], BF16, name="t_col")
        ident = const.tile([P, P], F32, name="ident")
        ident_bf = const.tile([P, P], BF16, name="ident_bf")

        def mx_operand(pool, width, moving, name, bufs=1):
            skip_words, skip_bytes = (0, 128) if moving else (16, 192)
            codes = pool.tile([P, skip_words + width], U32, align_bytes=256, name=name + "_codes", bufs=bufs)
            scales = pool.tile([P, skip_bytes + width], U8, align_bytes=256, name=name + "_scales", bufs=bufs)
            return codes[:, skip_words:], scales[:, skip_bytes:]

        w_codes, w_scales = mx_operand(keep, W_PASSES * D, True, name="w")
        x_codes, x_scales = mx_operand(keep, GROUPS * D, True, name="x")
        d_codes, d_scales = mx_operand(keep, GROUPS * N_TILE, False, name="d")
        planes = {"w": (w_codes, w_scales, E4M3), "x": (x_codes, x_scales, E4M3), "d": (d_codes, d_scales, E5M2)}

        def big_tile(shape, dtype):
            return inp.tile(shape, dtype, tag="big", bufs=7, align_bytes=DMA_ALIGN, name="big")

        raw = {}
        e_all = inp.tile([P, SLICES * D], BF16, align_bytes=DMA_ALIGN, name="e_all")
        for k in range(W_PASSES):
            raw["w", k] = big_tile([P, PACK * D], BF16)
        for g in range(GROUPS):
            raw["g", g] = big_tile([P, PACK * D], BF16)
            raw["e", g] = e_all[:, g * PACK * D : (g + 1) * PACK * D]
            raw["d", g] = raw["e", g]
            raw["v", g] = inp.tile([P, PACK * D], F32, tag="v", bufs=GROUPS, align_bytes=DMA_ALIGN, name="raw_v")

        turnover, held, banks = list(range(8)), {}, {}

        def take_bank(key, shape, dtype=F32):
            held[key] = turnover.pop(0)
            banks[key] = psum.tile(shape, dtype, tag="bank%d" % held[key], name="bank")
            return banks[key]

        def give_back(key):
            turnover.append(held[key])

        def part(kind, i, n=1):
            g, j = divmod(i, PACK)
            return raw[kind, g][:, j * D : (j + n) * D]

        def load(kind, i, n):
            g, j = divmod(i, PACK)
            nc.sync.dma_start(out=part(kind, i, n), in_=hbm[kind][g][:, j * D : (j + n) * D])

        def load_slices(i, n):
            for kind in "vge":
                load(kind, i, n)

        def load_w(k):
            nc.sync.dma_start(out=raw["w", k][:], in_=w_hbm[k])

        def rows_of(kind, k, lo, hi):
            return raw[kind, k][:].rearrange("p (t c) -> p t c", t=PACK)[:, :, lo:hi]

        def load_x(g):
            raw["x", g] = big_tile([P, PACK * D], BF16)
            nc.sync.dma_start(out=raw["x", g][:], in_=hbm["x"][g])

        def copy(engine, out, in_):
            if engine == "V":
                nc.vector.tensor_copy(out=out, in_=in_)
            else:
                nc.scalar.copy(out=out, in_=in_)

        grp, gate, early, dmu, dzt, dz, dv_mx, res = {}, {}, {}, {}, {}, {}, {}, {}

        def staging(key, width, tag):
            if key not in grp:
                grp[key] = work.tile([P, width * PACK], BF16, tag=tag, bufs=STAGING[tag], align_bytes=64, name=tag)
            return grp[key]

        def interleave(engine, piece, a=0, b=N_TILE, tag=None):
            kind, k, lo, hi = piece
            dst = staging(piece, hi - lo, tag or engine)[:, a * PACK : b * PACK]
            src = rows_of(kind, k, lo + a, lo + b)
            if engine == "G":
                nc.gpsimd.tensor_scalar(
                    out=dst.rearrange("p (c t) -> p c t", t=PACK), in0=src.rearrange("p t c -> p c t"),
                    scalar1=1.0, scalar2=0.0, op0=MULT, op1=ADD,
                )
            elif kind == "d":
                rows = rows_of(kind, k, lo, hi).rearrange("p t (u c w e) -> p u c t w e", u=2, w=RUN // 2, e=2)
                out = dst.rearrange("p (c w u e t) -> p u c t w e", w=RUN // 2, u=2, e=2, t=PACK)
                for u in range(2):
                    copy(engine, out[:, u], rows[:, u, a // (2 * RUN) : b // (2 * RUN)])
            else:
                copy(
                    engine,
                    dst.rearrange("p (c i t) -> p c t i", i=RUN, t=PACK),
                    src.rearrange("p t (c i) -> p c t i", i=RUN),
                )

        def carry(piece, a, b, stepped=True):
            kind, k, lo, hi = piece
            blocks = -(-(b - a) // P)
            w = (b - a) // blocks
            take_bank(piece, [P, blocks, PACK * w], BF16)
            for j in range(blocks):
                out = banks[piece][:, j].rearrange("p (c t) -> p t c" if stepped else "p (t c) -> p t c", t=PACK)
                first = lo + a + j * w
                nc.tensor.matmul(out, lhsT=ident_bf[:], rhs=rows_of(kind, k, first, first + w), start=True, stop=True)

        def carry_out(piece, a, b, stepped=True):
            dst = staging(piece, piece[3] - piece[2], "S")[:, a * PACK : b * PACK]
            if stepped:
                nc.scalar.copy(out=dst, in_=banks[piece][:].rearrange("p j x -> p (j x)"))
            else:
                nc.scalar.copy(
                    out=dst.rearrange("p (j c t) -> p j c t", c=P, t=PACK),
                    in_=banks[piece][:].rearrange("p j (t c) -> p j c t", t=PACK),
                )
            give_back(piece)

        def quantize(piece):
            kind, k, lo, hi = piece
            codes, scales, fmt = planes[kind]
            first = k * (N_TILE if kind == "d" else D)
            c = slice(first + lo, first + hi)
            nc.vector.quantize_mx(out=codes[:, c].bitcast(fmt), scales=scales[:, c], in_=grp[piece][:])

        def interleave_rows(engine, m, lo, hi):
            src = e_all[:].rearrange("p (g t k u w e) -> p k u g w t e", g=GROUPS, t=PACK, k=2, u=2, e=2)
            k, first = divmod(m * P, N_TILE)
            dst = staging(m, GROUPS * P, "V")[:].rearrange("p (g w u e t) -> p u g w t e", g=GROUPS, u=2, e=2, t=PACK)
            for u in range(2):
                copy(engine, dst[:, u, lo:hi], src[:, k, u, lo:hi, first // 4 : (first + P) // 4])

        def quantize_rows(m, third_first=False):
            codes, scales = mx_operand(work, GROUPS * P, False, name="r", bufs=3)
            parts = ((0, 2 * P), (2 * P, 3 * P))
            for lo, hi in reversed(parts) if third_first else parts:
                nc.vector.quantize_mx(
                    out=codes[:, lo:hi].bitcast(E5M2), scales=scales[:, lo:hi], in_=grp[m][:, lo * PACK : hi * PACK]
                )
            for g in range(GROUPS):
                dv_mx[g, m] = (codes[:, g * P : (g + 1) * P], scales[:, g * P : (g + 1) * P])

        def columns(half):
            return slice(half * N_TILE, (half + 1) * N_TILE)

        sorted_in = lambda a: a.rearrange("p (w u e) -> p u w e", u=2, e=2)
        sorted_out = lambda a: a.rearrange("p (u w e) -> p u w e", u=2, e=2)

        def sigmoid(i, half=None):
            if not half:
                gate[i] = work.tile([P, D], F32, tag="gate", bufs=2, name="gate")
            for h in range(2) if half is None else (half,):
                c = columns(h)
                nc.scalar.activation(out=sorted_out(gate[i][:, c]), in_=sorted_in(part("v", i)[:, c]), func=SIGMOID)

        def move(kind, i):
            bank = take_bank((kind, i), [P, D], BF16)
            for half in range(2):
                nc.tensor.matmul(
                    bank[:, columns(half)], lhsT=ident_bf[:], rhs=part(kind, i)[:, columns(half)], start=True, stop=True
                )

        of_sorted = lambda a, u: a.rearrange("p (k u w e) -> p u k w e", k=2, u=2, e=2)[:, u]
        of_natural = lambda a, u: a.rearrange("p (k w u e) -> p u k w e", k=2, u=2, e=2)[:, u]

        def first_product(i, a):
            moved = ("e", i) in banks
            values = of_sorted(gate[i][:], a) if moved else sorted_out(gate[i][:, columns(a)])
            noise = of_natural(banks["e", i][:], a) if moved else sorted_in(part("e", i)[:, columns(a)])
            nc.vector.tensor_tensor(out=values, in0=values, in1=noise, op=MULT)
            if a and moved:
                give_back(("e", i))

        def make_dmu(i):
            dmu[i] = work.tile([P, D], BF16, tag="dmu", bufs=2, name="dmu")
            nc.vector.tensor_scalar(
                out=sorted_out(dmu[i][:]), in0=sorted_in(part("g", i)),
                scalar1=t_col[:, i : i + 1], scalar2=None, op0=MULT,
            )

        def make_dv(i, u):
            moved = ("g", i) in banks
            nc.vector.scalar_tensor_tensor(
                out=of_sorted(part("e", i), u), in0=of_natural(banks["g", i][:] if moved else part("g", i), u),
                scalar=t_col[:, i : i + 1], in1=of_sorted(gate[i][:], u), op0=MULT, op1=MULT,
            )
            if u and moved:
                give_back(("g", i))

        def early_product(i):
            early[i] = work.tile([P, D], F32, tag="S", bufs=STAGING["S"], align_bytes=64, name="early")
            for u in range(2):
                nc.vector.scalar_tensor_tensor(
                    out=of_sorted(early[i][:], u), in0=of_natural(part("g", i), u), scalar=t_col[:, i : i + 1],
                    in1=of_natural(part("e", i), u), op0=MULT, op1=MULT,
                )

        def early_dv(i, half):
            c = columns(half)
            nc.vector.tensor_tensor(out=part("e", i)[:, c], in0=early[i][:, c], in1=gate[i][:, c], op=MULT)

        def turn(i, head):
            bank = take_bank((i, head), [P, 2, 2, P])
            words = (part("e", i) if head else dmu[i][:]).bitcast(F32)
            blocks = [(k, u) for k in range(2) for u in range(2)]
            for k, u in blocks if i < EARLY else sorted(blocks, key=lambda b: b[1]):
                first = 256 * k + P * u if head else 256 * u + P * k
                nc.tensor.transpose(bank[:, k, u, :], words[:, first : first + P], ident[:])

        def turn_out(i, head):
            if not head:
                tag = "G" if i == WINDOW - 2 else "dzt"
                dzt[i] = work.tile([P, 2 * D], BF16, tag=tag, bufs=STAGING[tag], align_bytes=64, name=tag)
            dst = dzt[i][:, head * D : (head + 1) * D].bitcast(F32)
            nc.scalar.copy(
                out=dst.rearrange("p (k c u) -> p k c u", k=2, u=2),
                in_=banks[i, head][:].rearrange("p k u c -> p k c u"),
            )
            give_back((i, head))

        def quantize_dz(i, head):
            if not head:
                dz[i] = mx_operand(work, W_PASSES * P, False, name="z", bufs=3)
            c = slice(head * 2 * P, (head + 1) * 2 * P)
            nc.vector.quantize_mx(
                out=dz[i][0][:, c].bitcast(E5M2), scales=dz[i][1][:, c], in_=dzt[i][:, head * D : (head + 1) * D]
            )

        def product0(i, n, passes):
            if passes[0] == 0:
                take_bank(("out_0", i, n), [P, N_TILE])
            codes, scales = dz[i]
            for k in passes:
                rows = slice(k * P, (k + 1) * P)
                cols = slice(k * D + n * N_TILE, k * D + (n + 1) * N_TILE)
                nc.tensor.matmul_mx(
                    out=banks["out_0", i, n][:],
                    lhsT=codes[:, rows].bitcast(E5M2), lhsT_scale=scales[:, rows],
                    rhs=w_codes[:, cols].bitcast(E4M3), rhs_scale=w_scales[:, cols],
                    start=(k == 0), stop=(k == W_PASSES - 1),
                )

        def result0(i, n):
            nc.scalar.copy(out=part("v", i)[:, columns(n)], in_=banks["out_0", i, n][:])
            give_back(("out_0", i, n))

        def store0(i):
            g, j = divmod(i, PACK)
            nc.sync.dma_start(out=out0_v[g][:, j * D : (j + 1) * D], in_=part("v", i))

        for g in range(GROUPS):
            for m in range(ROW_TILES // 2):
                rows = slice(g * N_TILE + m * P, g * N_TILE + (m + 1) * P)
                dv_mx[g, m] = (d_codes[:, rows], d_scales[:, rows])

        def pass1(m, n, g, first, final):
            if first:
                take_bank(("out_1", m, n), [P, N_TILE])
            codes, scales = dv_mx[g, m]
            cols = slice(g * D + n * N_TILE, g * D + (n + 1) * N_TILE)
            nc.tensor.matmul_mx(
                out=banks["out_1", m, n][:],
                lhsT=codes.bitcast(E5M2), lhsT_scale=scales,
                rhs=x_codes[:, cols].bitcast(E4M3), rhs_scale=x_scales[:, cols],
                start=first, stop=final,
            )

        def result_of(m, n):
            four, place = (n, m) if m < ROW_TILES // 2 else (m // 2, m % 2 * 2 + n)
            if four not in res:
                res[four] = big_tile([P, 4 * N_TILE], F32)
            return res[four][:, place * N_TILE :]

        def result1(engine, m, n):
            copy(engine, result_of(m, n)[:, :N_TILE], banks["out_1", m, n][:])
            give_back(("out_1", m, n))

        def store1(m, n, lo=0, hi=N_TILE):
            nc.sync.dma_start(out=out1_v[m][:, n * N_TILE + lo : n * N_TILE + hi], in_=result_of(m, n)[:, lo:hi])

        def products0(i, head):
            for n in range(2):
                product0(i, n, (2 * head, 2 * head + 1))

        def results0(i):
            for n in range(2):
                result0(i, n)
            store0(i)

        def quadrant(n, g, first, final):
            for m in range(ROW_TILES // 2):
                pass1(m, n, g, first, final)

        def row_tile(m):
            for n in range(2 if m < ROW_TILES - 1 else 1):
                for g in range(GROUPS):
                    pass1(m, n, g, g == 0, g == GROUPS - 1)

        def last_half(a):
            bank = take_bank(("last", a), [P, HALF])
            for g in range(GROUPS):
                codes, scales = dv_mx[g, ROW_TILES - 1]
                cols = slice(g * D + N_TILE + a * HALF, g * D + N_TILE + (a + 1) * HALF)
                nc.tensor.matmul_mx(
                    out=bank[:],
                    lhsT=codes.bitcast(E5M2), lhsT_scale=scales,
                    rhs=x_codes[:, cols].bitcast(E4M3), rhs_scale=x_scales[:, cols],
                    start=(g == 0), stop=(g == GROUPS - 1),
                )

        nc.scalar.dma_start(
            out=t_col[:].rearrange("p (g j) -> p g j", j=PACK),
            in_=t_rand.rearrange("(g p j) o -> p g (j o)", p=P, j=PACK),
        )
        load("g", 0, 1)
        load("e", 0, 1)
        for half in range(2):
            nc.sync.dma_start(out=part("v", 0)[:, columns(half)], in_=hbm["v"][0][:, 0:D][:, columns(half)])
        for kind in "gev":
            load(kind, 1, 1)
        for k in range(W_PASSES):
            load_w(k)
        load_slices(2, 1)
        load_slices(3, 1)
        make_identity(nc, ident[:])
        make_identity(nc, ident_bf[:])

        make_dmu(0)
        early_product(0)
        turn(0, 0)
        for half in range(2):
            sigmoid(0, half)
            early_dv(0, half)
        turn(0, 1)
        turn_out(0, 0)
        for half in range(2):
            sigmoid(1, half)
        turn_out(0, 1)
        early_product(1)
        make_dmu(1)
        quantize_dz(0, 0)
        for half in range(2):
            early_dv(1, half)
        turn(1, 0)
        turn(1, 1)
        quantize_dz(0, 1)
        turn_out(1, 0)

        w_pieces = [("w", k, lo, lo + N_TILE) for k in range(W_PASSES) for lo in (0, N_TILE)]
        final = len(w_pieces) - 1

        def head_passes(q):
            for i in range(2):
                product0(i, q % 2, [q // 2])

        for q, piece in enumerate(w_pieces):
            carried, stepped = N_TILE - CARRIED_W[q], q > 1
            if q == 2:
                quantize_dz(1, 1)
            if CARRIED_W[q]:
                carry(piece, carried, N_TILE, stepped)
            interleave("V", piece, 0, VECTOR_W[q])
            if q == final:
                make_dmu(2)
                turn(2, 0)
            if VECTOR_W[q] < carried:
                interleave("S", piece, VECTOR_W[q], carried)
            if q == final:
                sigmoid(2, 0)
            if q == 0:
                turn_out(1, 1)
                quantize_dz(1, 0)
            if CARRIED_W[q]:
                carry_out(piece, carried, N_TILE, stepped)
            if q > 0:
                quantize(w_pieces[q - 1])
            if q > 1:
                head_passes(q - 2)

        load("g", 4, 2)
        load("v", 4, 1)
        load("e", 4, 2)
        load("v", 5, 1)
        load_slices(6, 2)
        load_x(0)
        load_slices(8, 2)
        load_slices(10, 2)
        load_x(1)
        load_x(2)

        sigmoid(2, 1)
        early_product(2)
        turn_out(2, 0)
        head_passes(final - 1)
        quantize(w_pieces[final])
        head_passes(final)
        sigmoid(3)
        results0(0)

        last = SLICES - 1
        d_left = [("d", g, 0, N_TILE) for g in range(GROUPS)]
        x_left = [("x", g, 0, N_TILE) for g in range(GROUPS)]
        x_right = [("x", g, N_TILE, D) for g in range(GROUPS)]
        windows = {WINDOW + a: ("x", 0, a * WINDOW_PIECE, (a + 1) * WINDOW_PIECE) for a in range(2)}
        x_rest = ("x", 0, 2 * WINDOW_PIECE, D)
        begins = (PACK, WINDOW + 2)
        for i in range(2, SLICES):
            window = windows.get(i)
            if window:
                interleave("G", window, 0, POOL_COLUMNS)
            if i >= EARLY:
                first_product(i, 0)
                first_product(i, 1)
            if i == WINDOW:
                move("e", i + 1)
                products0(i - 1, 0)
            if i < last and not window:
                make_dmu(i + 1)
            for g, first in enumerate(begins):
                if 0 <= i - first < 3:
                    interleave("V", d_left[g], (i - first) * P, (i - first + 1) * P)
            for a in range(2):
                (make_dv if i >= EARLY else early_dv)(i, a)
            if window:
                make_dmu(i + 1)
            if i == WINDOW - 1:
                quantize_dz(i, 0)
                quantize_dz(i - 1, 1)
                move("e", i + 1)
            else:
                if i > 2:
                    quantize_dz(i - 1, 1)
                if window:
                    interleave("V", window, POOL_COLUMNS, WINDOW_PIECE)
                quantize_dz(i, 0)
                if window:
                    quantize(window)
            if i + 1 in windows:
                move("g", i + 1)
            for s, head in ((i, 1), (i + 1, 0)) if window else ((i + 1, 0), (i, 1)):
                if s < SLICES:
                    turn(s, head)
                if i == 3 and not head:
                    product0(2, 1, (0, 1))
            if i > 2:
                products0(i - 1, 1)
            if i == 2:
                product0(2, 0, (0, 1))
            elif i != WINDOW - 1:
                products0(i, 0)
            if i == last:
                interleave("S", x_left[2], 0, HALF)
            behind = i >= WINDOW - 1
            if behind and i + 2 < SLICES:
                sigmoid(i + 2)
            turn_out(i, 1)
            if i < last:
                turn_out(i + 1, 0)
            if not behind:
                sigmoid(i + 2)
            if i < last:
                results0(i - 1)
            if window:
                interleave("S", d_left[i - WINDOW], N_TILE - P, N_TILE)
            if i - 1 in windows and not window:
                interleave("S", x_rest, 0, P, "G")

        upper = ROW_TILES // 2
        quantize(d_left[0])
        quadrant(0, 0, True, False)
        interleave("V", x_left[1])
        quantize(d_left[1])
        quantize_dz(last, 1)
        products0(last, 1)
        interleave("S", x_left[2], HALF, N_TILE)
        results0(last - 1)
        quantize(x_left[1])
        quadrant(0, 1, False, False)
        interleave("V", d_left[2])
        interleave("S", x_rest, P, 2 * P)
        results0(last)
        interleave("S", x_right[1], 0, HALF)
        quantize(x_left[2])
        quantize(d_left[2])
        quadrant(0, 2, False, True)
        quantize(x_rest)
        quadrant(1, 0, True, False)
        interleave("V", x_right[1], HALF, N_TILE)
        interleave("V", x_right[2], 0, HALF)
        quantize(x_right[1])
        quadrant(1, 1, False, False)
        interleave("S", x_right[2], N_TILE - P, N_TILE)
        interleave("V", x_right[2], HALF, N_TILE - P)
        for m in range(upper):
            result1("S", m, 0)
            store1(m, 0)
        interleave_rows("V", upper, 0, 1)
        quantize(x_right[2])
        quadrant(1, 2, False, True)
        interleave_rows("V", upper, 1, 2)
        interleave_rows("V", upper, 2, 3)
        interleave_rows("S", upper + 1, 2, 3)
        for m in range(upper):
            result1("S", m, 1)
            store1(m, 1)

        for m in range(upper, ROW_TILES):
            if m > upper:
                interleave_rows("V", m, 0, 2)
            if m > upper + 1:
                interleave_rows("V", m, 2, 3)
            quantize_rows(m, third_first=m == upper + 1)
            row_tile(m)

        for m in (upper, upper + 1):
            for n in range(2):
                result1("S", m, n)
            store1(m, 0, 0, D)
        for a in range(2):
            last_half(a)
        for engine, m, n in (("S", upper + 2, 0), ("V", upper + 2, 1), ("S", upper + 3, 0)):
            result1(engine, m, n)
            store1(m, n)
        for a in range(2):
            copy("V", result_of(upper + 3, 1)[:, a * HALF : (a + 1) * HALF], banks["last", a][:])
            store1(upper + 3, 1, a * HALF, (a + 1) * HALF)
